import numpy as np
import ml_dtypes


def mxq(x, axis, fmt="e4m3"):
    dtype, down = {"e4m3": (ml_dtypes.float8_e4m3fn, 7), "e5m2": (ml_dtypes.float8_e5m2, 14)}[fmt]
    v = np.moveaxis(np.asarray(x, np.float32).astype(ml_dtypes.bfloat16).astype(np.float64), axis, -1)
    blocks = v.reshape(v.shape[:-1] + (-1, 32))
    amax = np.abs(blocks).max(-1, keepdims=True)
    byte = np.maximum(np.where(amax > 0, np.frexp(amax)[1] - 1 + 127, 0) - down, 1)
    scale = np.exp2(byte - 127.0)
    codes = (blocks / scale).astype(np.float32).astype(dtype).astype(np.float64)
    return np.moveaxis((codes * scale).reshape(v.shape), -1, axis)


WIDE = False


def mx_kscale(k):
    if not WIDE:
        return np.ones(k)
    levels = np.array([10, -10, 5, -5, 0])
    a = np.random.permutation(np.resize(levels, k // 512 * 4)).reshape(k // 512, 4)
    idx = np.arange(k)
    return np.exp2(a[idx // 512, idx % 128 // 32])


BF16 = ml_dtypes.bfloat16


def bf(x):
    return np.asarray(x, np.float32).astype(BF16)


def f64(x):
    return np.asarray(x).astype(np.float64)


E2M1 = np.array([0.0, 0.5, 1.0, 1.5, 2.0, 3.0, 4.0, 6.0, -0.0, -0.5, -1.0, -1.5, -2.0, -3.0, -4.0, -6.0])


def pack_weight(w, fmt):
    k, n = w.shape
    w = f64(bf(w)).reshape(k // 32, 32, n)
    amax = np.abs(w).max(1)
    if fmt == "e4m3":
        byte = np.frexp(amax)[1] - 1 + 127 - 7
    else:
        mant, ex = np.frexp(amax / 6.0)
        byte = np.where(mant > 0.5, ex, ex - 1) + 127
    byte = np.clip(np.where(amax > 0, byte, 1), 1, 254)
    scaled = (w * np.exp2(127.0 - byte)[:, None, :]).reshape(k, n).astype(np.float32)
    by_word = np.ascontiguousarray(scaled.reshape(k // 512, 128, 4, n).transpose(0, 1, 3, 2))
    if fmt == "e4m3":
        words = by_word.astype(ml_dtypes.float8_e4m3fn).view(np.uint8)
    else:
        c = by_word.astype(ml_dtypes.float4_e2m1fn).view(np.uint8) & 0xF
        words = c[..., 0::2] | (c[..., 1::2] << 4)
    return np.ascontiguousarray(words), np.ascontiguousarray(byte.astype(np.uint8).reshape(k // 512, 16, n))


def unpack_weight(words, scales, fmt):
    g, p, n, _ = words.shape
    if fmt == "e4m3":
        vals = np.ascontiguousarray(words).view(ml_dtypes.float8_e4m3fn).astype(np.float64)
    else:
        nib = np.empty((g, p, n, 4), np.uint8)
        nib[..., 0::2] = words & 0xF
        nib[..., 1::2] = words >> 4
        vals = E2M1[nib]
    vals = vals * np.repeat(np.exp2(scales.astype(np.float64) - 127.0), 8, axis=1)[..., None]
    return vals.transpose(0, 1, 3, 2).reshape(g * 512, n)


B, H, W, WS, C, NH, DH, F, PT = 2, 56, 56, 14, 512, 4, 64, 2048, 16
E = NH * DH
N = WS * WS
GH, GW = H // WS, W // WS
BW = B * GH * GW
HALF = DH // 2
EPS = 1e-6
THETA = 10000.0
FMT = "e4m3"


def layer_norm(v, w, b):
    mu = v.mean(-1, keepdims=True)
    var = ((v - mu) ** 2).mean(-1, keepdims=True)
    return (v - mu) / np.sqrt(var + EPS) * w + b


def rotate_half(u):
    ur = u.reshape(u.shape[:-1] + (-1, 2))
    return np.stack((-ur[..., 1], ur[..., 0]), -1).reshape(u.shape)


def rope_tables():
    freqs = 1.0 / THETA ** (np.arange(0, HALF, 2) / HALF)
    ang = np.repeat((np.arange(WS) / WS * PT)[:, None] * freqs[None, :], 2, axis=-1)
    f = np.concatenate([np.broadcast_to(ang[:, None, :], (WS, WS, HALF)),
                        np.broadcast_to(ang[None, :, :], (WS, WS, HALF))], -1).reshape(N, DH)
    return np.cos(f), np.sin(f)


def setup_inputs():
    s = mx_kscale(C)
    r = np.random.standard_normal
    x = bf(1.5 * r((B, H, W, C)) + 0.5 * r((B, H, W, 1)))
    ln1_w = bf((1.0 + 0.1 * r(C)) * s)
    ln1_b = bf(0.2 * r(C) * s)
    q_w_words, q_w_scales = pack_weight(r((C, E)) / np.sqrt(C) / s[:, None], FMT)
    q_b = bf(0.3 * r(E))
    k_w_words, k_w_scales = pack_weight(r((C, E)) / np.sqrt(C) / s[:, None], FMT)
    v_w_words, v_w_scales = pack_weight(r((C, E)) / np.sqrt(C) / s[:, None], FMT)
    v_b = bf(0.3 * r(E))
    return {"x": x,
            "ln1_w": ln1_w, "ln1_b": ln1_b,
            "q_w_words": q_w_words, "q_w_scales": q_w_scales, "q_b": q_b,
            "k_w_words": k_w_words, "k_w_scales": k_w_scales,
            "v_w_words": v_w_words, "v_w_scales": v_w_scales, "v_b": v_b}


def reference(x, ln1_w, ln1_b, q_w_words, q_w_scales, q_b, k_w_words, k_w_scales, v_w_words, v_w_scales, v_b):
    h = layer_norm(f64(x), f64(ln1_w), f64(ln1_b))
    t = h.reshape(B, GH, WS, GW, WS, C).transpose(0, 1, 3, 2, 4, 5).reshape(BW, N, C)
    tq = mxq(t, 2, "e4m3")
    q = (tq @ unpack_weight(q_w_words, q_w_scales, FMT)) + f64(q_b)
    k = tq @ unpack_weight(k_w_words, k_w_scales, FMT)
    v = (tq @ unpack_weight(v_w_words, v_w_scales, FMT)) + f64(v_b)
    q = q.reshape(BW, N, NH, DH).transpose(0, 2, 1, 3)
    k = k.reshape(BW, N, NH, DH).transpose(0, 2, 1, 3)
    v = v.reshape(BW, N, NH, DH).transpose(0, 2, 1, 3)
    cos, sin = rope_tables()
    q = q * cos + rotate_half(q) * sin
    k = k * cos + rotate_half(k) * sin
    return q, k, v

@@ -1,0 +1,401 @@
+import math
+from contextlib import ExitStack
+
+import concourse.mybir as mybir
+from concourse.masks import make_identity
+
+F32 = mybir.dt.float32
+BF16 = mybir.dt.bfloat16
+I32 = mybir.dt.int32
+U32 = mybir.dt.uint32
+U8 = mybir.dt.uint8
+FP8X4 = mybir.dt.float8_e4m3fn_x4
+ALU = mybir.AluOpType
+ACT = mybir.ActivationFunctionType
+
+P = 128
+C = 512
+PACK = 4
+E = 256
+HEADS = 4
+DH = 64
+HALF = 32
+FREQS = 16
+UNIT = 7
+BANK_TILES = 4
+EPS = 1e-6
+THETA = 10000.0
+STEP = 16.0 / 14.0
+
+FLOPS = 2 * 2 * 56 * 56 * C * 3 * E
+
+
+def tile_block_pa_t_kernel(
+    tc, x, ln1_w, ln1_b, q_w_words, q_w_scales, q_b, k_w_words, k_w_scales,
+    v_w_words, v_w_scales, v_b, out_0, out_1, out_2,
+):
+    nc = tc.nc
+    groups = [
+        (s, first, min(BANK_TILES, UNIT - first))
+        for s in range(UNIT) for first in range(0, UNIT, BANK_TILES)
+    ]
+    tiles = [(g, slot) for g, (s, first, count) in enumerate(groups) for slot in range(count)]
+
+    with ExitStack() as ctx:
+        consts = ctx.enter_context(tc.tile_pool(name="consts", bufs=1))
+        setup = ctx.enter_context(tc.tile_pool(name="setup", bufs=1))
+        x_pool = ctx.enter_context(tc.tile_pool(name="x", bufs=1))
+        small = ctx.enter_context(tc.tile_pool(name="small", bufs=4))
+        xhat_pool = ctx.enter_context(tc.tile_pool(name="xhat", bufs=2 * BANK_TILES))
+        quant = ctx.enter_context(tc.tile_pool(name="quant", bufs=2))
+        rope = ctx.enter_context(tc.tile_pool(name="rope", bufs=3))
+        stage_pool = ctx.enter_context(tc.tile_pool(name="stage", bufs=2))
+        psum_t = ctx.enter_context(tc.psum_pool(name="psum_t", bufs=1))
+        psum_qk = ctx.enter_context(tc.psum_pool(name="psum_qk", bufs=2))
+        psum_v = ctx.enter_context(tc.psum_pool(name="psum_v", bufs=2))
+        ctx.enter_context(tc.manual_schedule())
+
+        x_rounds = x.rearrange(
+            "b (i r s) (u c) k -> s (b i r) u (c k)", i=4, r=2, s=UNIT, u=8, c=UNIT
+        )
+        x_sb = [x_pool.tile([P, UNIT, C], BF16, name="x%d" % s) for s in range(UNIT)]
+
+        def load_group(g):
+            s, first, count = groups[g]
+            nc.sync.dma_start(
+                out=x_sb[s][:, first : first + count, :].rearrange("p c k -> p (c k)"),
+                in_=x_rounds[s, :, :, first * C : (first + count) * C],
+            )
+
+        load_group(0)
+
+        gain_bf = setup.tile([P, PACK], BF16)
+        shift_bf = setup.tile([P, PACK], BF16)
+        nc.sync.dma_start(out=gain_bf[:], in_=ln1_w.rearrange("(p t) -> p t", t=PACK))
+        nc.sync.dma_start(out=shift_bf[:], in_=ln1_b.rearrange("(p t) -> p t", t=PACK))
+        load_group(1)
+
+        w_words = consts.tile([P, 3 * E * PACK], U8, align_bytes=64)
+        w_scales = consts.tile([P, 3 * E], U8, align_bytes=64)
+        nc.vector.memset(w_scales[:].bitcast(I32), 0)
+        q_bias_bf = setup.tile([P, E], BF16)
+        v_bias_bf = setup.tile([P, E], BF16)
+        nc.sync.dma_start(out=q_bias_bf[:], in_=q_b.partition_broadcast(P))
+        for n, (words, scales) in enumerate(
+            ((q_w_words, q_w_scales), (k_w_words, k_w_scales), (v_w_words, v_w_scales))
+        ):
+            nc.sync.dma_start(
+                out=w_words[:, n * E * PACK : (n + 1) * E * PACK].bitcast(I32),
+                in_=words[0].rearrange("p n t -> p (n t)").bitcast(I32),
+            )
+            for quadrant in range(4):
+                nc.sync.dma_start(
+                    out=w_scales[32 * quadrant : 32 * quadrant + 4, n * E : (n + 1) * E].bitcast(I32),
+                    in_=scales[0, 4 * quadrant : 4 * quadrant + 4, :].bitcast(I32),
+                )
+        nc.sync.dma_start(out=v_bias_bf[:], in_=v_b.partition_broadcast(P))
+        for g in range(2, len(groups)):
+            load_group(g)
+
+        ident = setup.tile([P, P], F32)
+        make_identity(nc, ident[:])
+        order = consts.tile([P, P], F32)
+        nc.vector.tensor_copy(
+            out=order[:].rearrange("p (a j r h) -> p a j r h", a=8, j=4, r=2, h=2),
+            in_=ident[:].rearrange("p (a r j h) -> p a j r h", a=8, r=2, j=4, h=2),
+        )
+
+        part = setup.tile([P, 1], I32)
+        nc.gpsimd.iota(part[:], pattern=[[0, 1]], base=0, channel_multiplier=1)
+        count_i = setup.tile([P, 2, UNIT], I32)
+        nc.gpsimd.iota(count_i[:], pattern=[[0, 2], [1, UNIT]], base=0, channel_multiplier=0)
+        one = setup.tile([P, 1], F32)
+        nc.vector.memset(one[:], 1.0)
+        warm = setup.tile([P, 2], F32)
+        nc.scalar.activation(out=warm[:, 0:1], in_=one[:], func=ACT.Sin)
+        bits_i = setup.tile([P, 2], I32)
+        nc.vector.tensor_scalar(
+            out=bits_i[:, 0:1], in0=part[:], scalar1=1, scalar2=1,
+            op0=ALU.logical_shift_right, op1=ALU.bitwise_and,
+        )
+        nc.vector.tensor_single_scalar(out=bits_i[:, 1:2], in_=part[:], scalar=1, op=ALU.bitwise_and)
+        bits = setup.tile([P, 2], F32)
+        nc.vector.tensor_copy(out=bits[:], in_=bits_i[:])
+        count_f = setup.tile([P, 2, UNIT], F32)
+        nc.vector.tensor_copy(out=count_f[:], in_=count_i[:])
+        place = setup.tile([P, 2, UNIT], F32)
+        nc.vector.scalar_tensor_tensor(
+            out=place[:], in0=bits[:].unsqueeze(2).to_broadcast([P, 2, UNIT]), scalar=float(UNIT),
+            in1=count_f[:], op0=ALU.mult, op1=ALU.add,
+        )
+        freq = setup.tile([P, FREQS], F32)
+        nc.vector.tensor_scalar_mul(out=freq[:, 0:1], in0=one[:], scalar1=STEP)
+        for width in (1, 2, 4, 8):
+            nc.vector.tensor_scalar_mul(
+                out=freq[:, width : 2 * width], in0=freq[:, 0:width],
+                scalar1=THETA ** (-width / FREQS),
+            )
+        rows = 2 * UNIT
+        phase = setup.tile([P, 2, rows, FREQS], F32)
+        nc.vector.tensor_tensor(
+            out=phase[:, 1],
+            in0=place[:].rearrange("p g i -> p (g i)").unsqueeze(2).to_broadcast([P, rows, FREQS]),
+            in1=freq[:].unsqueeze(1).to_broadcast([P, rows, FREQS]),
+            op=ALU.mult,
+        )
+        nc.vector.tensor_scalar_add(out=phase[:, 0], in0=phase[:, 1], scalar1=math.pi / 2)
+        turns = setup.tile([P, 2, rows, FREQS], F32)
+        nc.vector.tensor_single_scalar(out=turns[:], in_=phase[:], scalar=math.pi, op=ALU.is_ge)
+        for odd in (3, 5):
+            nc.vector.scalar_tensor_tensor(
+                out=turns[:].rearrange("p a b c -> p (a b c)"),
+                in0=phase[:].rearrange("p a b c -> p (a b c)"), scalar=odd * math.pi,
+                in1=turns[:].rearrange("p a b c -> p (a b c)"), op0=ALU.is_ge, op1=ALU.add,
+            )
+        wrapped = setup.tile([P, 2, rows, FREQS], F32)
+        nc.vector.scalar_tensor_tensor(
+            out=wrapped[:].rearrange("p a b c -> p (a b c)"),
+            in0=turns[:].rearrange("p a b c -> p (a b c)"), scalar=-2.0 * math.pi,
+            in1=phase[:].rearrange("p a b c -> p (a b c)"), op0=ALU.mult, op1=ALU.add,
+        )
+        cos_sin = setup.tile([P, 2, rows, FREQS], F32)
+        nc.scalar.activation(out=cos_sin[:], in_=wrapped[:], func=ACT.Sin)
+        nc.scalar.activation(out=warm[:, 1:2], in_=one[:], func=ACT.Abs_reciprocal_sqrt)
+        sign = setup.tile([P, 2], F32)
+        nc.vector.memset(sign[:, 0:1], -1.0)
+        nc.vector.memset(sign[:, 1:2], 1.0)
+
+        stats, mean_var, rstd, minus_mean_rstd = {}, {}, {}, {}
+        xhat, banks, grouped, codes, code_scales = {}, {}, {}, {}, {}
+        qk, v, stage = {}, {}, {}
+
+        def stats_of_tile(g, slot):
+            s, first, count = groups[g]
+            if slot == 0:
+                stats[g] = small.tile([P, BANK_TILES, 6], F32, name="stats")
+                mean_var[g] = small.tile([P, BANK_TILES, 2], F32, name="mean_var")
+            nc.vector.bn_stats(out=stats[g][:, slot, :], in_=x_sb[s][:, first + slot, :])
+            nc.vector.bn_aggr(out=mean_var[g][:, slot, :], in_=stats[g][:, slot, :])
+
+        def finish_stats(g):
+            count = groups[g][2]
+            mean = mean_var[g][:, 0:count, 0]
+            var = mean_var[g][:, 0:count, 1]
+            guess = small.tile([P, BANK_TILES], F32, name="guess")
+            nc.scalar.activation(out=guess[:, 0:count], in_=var, func=ACT.Abs_reciprocal_sqrt, bias=EPS)
+            newton = small.tile([P, 3, BANK_TILES], F32, name="newton")
+            nc.vector.scalar_tensor_tensor(
+                out=newton[:, 0, 0:count], in0=var, scalar=EPS, in1=guess[:, 0:count],
+                op0=ALU.add, op1=ALU.mult,
+            )
+            nc.vector.tensor_tensor(
+                out=newton[:, 1, 0:count], in0=newton[:, 0, 0:count], in1=guess[:, 0:count], op=ALU.mult
+            )
+            nc.vector.tensor_scalar(
+                out=newton[:, 2, 0:count], in0=newton[:, 1, 0:count], scalar1=-0.5, scalar2=1.5,
+                op0=ALU.mult, op1=ALU.add,
+            )
+            rstd[g] = small.tile([P, BANK_TILES], F32, name="rstd")
+            nc.vector.tensor_tensor(
+                out=rstd[g][:, 0:count], in0=guess[:, 0:count], in1=newton[:, 2, 0:count], op=ALU.mult
+            )
+            minus_mean_rstd[g] = small.tile([P, BANK_TILES], F32, name="minus_mean_rstd")
+            nc.vector.scalar_tensor_tensor(
+                out=minus_mean_rstd[g][:, 0:count], in0=mean, scalar=-1.0, in1=rstd[g][:, 0:count],
+                op0=ALU.mult, op1=ALU.mult,
+            )
+
+        def normalise(g):
+            s, first, count = groups[g]
+            xhat[g] = []
+            for slot in range(count):
+                normal = xhat_pool.tile([P, PACK, P], F32, name="xhat")
+                nc.scalar.activation(
+                    out=normal[:], in_=x_sb[s][:, first + slot, :].rearrange("p (q t) -> p t q", t=PACK),
+                    func=ACT.Identity, scale=rstd[g][:, slot : slot + 1],
+                    bias=minus_mean_rstd[g][:, slot : slot + 1],
+                )
+                xhat[g].append(normal)
+
+        def transpose(g):
+            banks[g] = [psum_t.tile([P, BANK_TILES * P], F32, name="bank%d" % t) for t in range(PACK)]
+            for slot, normal in enumerate(xhat[g]):
+                for t in range(PACK):
+                    nc.tensor.transpose(banks[g][t][:, slot * P : (slot + 1) * P], normal[:, t, :], order[:])
+
+        def affine(g):
+            cols = groups[g][2] * P
+            planes = quant.tile([P, PACK, BANK_TILES * P], BF16, name="planes")
+            for t in range(PACK):
+                nc.scalar.activation(
+                    out=planes[:, t, 0:cols], in_=banks[g][t][:, 0:cols], func=ACT.Identity,
+                    scale=gain[:, t : t + 1], bias=shift[:, t : t + 1],
+                )
+            grouped[g] = quant.tile([P, BANK_TILES * P, PACK], BF16, name="grouped", align_bytes=64)
+            nc.scalar.copy(
+                out=grouped[g][:, 0:cols, :], in_=planes[:, :, 0:cols].rearrange("p t j -> p j t")
+            )
+
+        def quantise(g):
+            codes[g] = quant.tile([P, BANK_TILES * P], U32, name="codes", align_bytes=64)
+            code_scales[g] = quant.tile([P, BANK_TILES * P], U8, name="code_scales", align_bytes=64)
+            for slot in range(groups[g][2]):
+                tokens = slice(slot * P, (slot + 1) * P)
+                nc.vector.quantize_mx(
+                    out=codes[g][:, tokens].bitcast(FP8X4), scales=code_scales[g][:, tokens],
+                    in_=grouped[g][:, tokens, :].rearrange("p j t -> p (j t)"),
+                )
+
+        def project(j):
+            g, slot = tiles[j]
+            tokens = slice(slot * P, (slot + 1) * P)
+            qk[j] = psum_qk.tile([P, 2 * E], F32, name="qk")
+            nc.tensor.matmul_mx(
+                out=qk[j][:], lhsT=codes[g][:, tokens].bitcast(FP8X4), lhsT_scale=code_scales[g][:, tokens],
+                rhs=w_words[:, 0 : 2 * E * PACK].bitcast(FP8X4), rhs_scale=w_scales[:, 0 : 2 * E],
+                start=True, stop=True,
+            )
+            v[j] = psum_v.tile([P, E], F32, name="v")
+            nc.tensor.matmul_mx(
+                out=v[j][:], lhsT=codes[g][:, tokens].bitcast(FP8X4), lhsT_scale=code_scales[g][:, tokens],
+                rhs=w_words[:, 2 * E * PACK : 3 * E * PACK].bitcast(FP8X4),
+                rhs_scale=w_scales[:, 2 * E : 3 * E], start=True, stop=True,
+            )
+
+        def rotate(j):
+            g, slot = tiles[j]
+            s, first, count = groups[g]
+            c = first + slot
+            if c == 0:
+                stage[s] = stage_pool.tile([P, 3 * HEADS, UNIT, DH], F32, name="stage")
+            halves = slice(s, UNIT + c + 1, UNIT + c - s)
+            shape = [P, 2 * HEADS, 2, FREQS, 2]
+            by_cos = rope.tile([P, 2 * E], F32, name="by_cos")
+            by_sin = rope.tile([P, 2 * E], F32, name="by_sin")
+            nc.vector.tensor_tensor(
+                out=by_cos[:].rearrange("p (a g m e) -> p a g m e", g=2, m=FREQS, e=2),
+                in0=qk[j][:].rearrange("p (a g m e) -> p a g m e", g=2, m=FREQS, e=2),
+                in1=cos_tab[:, halves].unsqueeze(1).to_broadcast(shape),
+                op=ALU.mult,
+            )
+            nc.vector.tensor_tensor(
+                out=by_sin[:].rearrange("p (a g m e) -> p a g m e", g=2, m=FREQS, e=2),
+                in0=qk[j][:].rearrange("p (a g m e) -> p a g m e", g=2, m=FREQS, e=2)[:, :, :, :, ::-1],
+                in1=sin_tab[:, halves].unsqueeze(1).to_broadcast(shape),
+                op=ALU.mult,
+            )
+            nc.gpsimd.tensor_tensor(
+                out=stage[s][:, 0 : 2 * HEADS, c, :],
+                in0=by_cos[:].rearrange("p (a d) -> p a d", d=DH),
+                in1=by_sin[:].rearrange("p (a d) -> p a d", d=DH),
+                op=ALU.add,
+            )
+            nc.gpsimd.tensor_tensor(
+                out=stage[s][:, 0:HEADS, c, :].rearrange("p h (g d) -> p h g d", g=2),
+                in0=stage[s][:, 0:HEADS, c, :].rearrange("p h (g d) -> p h g d", g=2),
+                in1=bias_tab[:, halves].rearrange("p g h d -> p h g d"),
+                op=ALU.add,
+            )
+            nc.vector.tensor_tensor(
+                out=stage[s][:, 2 * HEADS : 3 * HEADS, c, :],
+                in0=v[j][:].rearrange("p (h d) -> p h d", d=DH),
+                in1=v_bias[:].rearrange("p (h d) -> p h d", d=DH),
+                op=ALU.add,
+            )
+
+        out_views = [
+            o.rearrange("w h (r s f c) d -> s h w r f (c d)", r=2, s=UNIT, f=2, c=UNIT)
+            for o in (out_0, out_1, out_2)
+        ]
+
+        def store(s):
+            for a in range(3 * HEADS):
+                for f in range(2):
+                    nc.sync.dma_start(
+                        out=out_views[a // HEADS][s, a % HEADS, :, :, f, :],
+                        in_=stage[s][f:P:2, a].rearrange("p c d -> p (c d)"),
+                    )
+
+        def prepare(g):
+            if g + 1 < len(groups):
+                transpose(g + 1)
+            if g + 2 < len(groups):
+                finish_stats(g + 2)
+            quantise(g)
+            if g + 2 < len(groups):
+                normalise(g + 2)
+            if g + 1 < len(groups):
+                affine(g + 1)
+
+        ahead = 4
+        for g in range(2):
+            for slot in range(groups[g][2]):
+                stats_of_tile(g, slot)
+            finish_stats(g)
+            normalise(g)
+        gain = consts.tile([P, PACK], F32)
+        shift = consts.tile([P, PACK], F32)
+        nc.vector.tensor_copy(out=gain[:], in_=gain_bf[:])
+        nc.vector.tensor_copy(out=shift[:], in_=shift_bf[:])
+        transpose(0)
+        affine(0)
+
+        cos_tab = consts.tile([P, rows, FREQS, 2], F32)
+        sin_tab = consts.tile([P, rows, FREQS, 2], F32)
+        pairs = rows * FREQS
+        nc.vector.tensor_copy(
+            out=cos_tab[:].rearrange("p i m e -> p (i m) e"),
+            in_=cos_sin[:, 0].rearrange("p i m -> p (i m)").unsqueeze(2).to_broadcast([P, pairs, 2]),
+        )
+        nc.vector.tensor_tensor(
+            out=sin_tab[:].rearrange("p i m e -> p (i m) e"),
+            in0=cos_sin[:, 1].rearrange("p i m -> p (i m)").unsqueeze(2).to_broadcast([P, pairs, 2]),
+            in1=sign[:].unsqueeze(1).to_broadcast([P, pairs, 2]),
+            op=ALU.mult,
+        )
+        q_bias = setup.tile([P, E], F32)
+        q_bias_swapped = setup.tile([P, E], F32)
+        v_bias = consts.tile([P, E], F32)
+        nc.vector.tensor_copy(out=q_bias[:], in_=q_bias_bf[:])
+        nc.vector.tensor_copy(
+            out=q_bias_swapped[:].rearrange("p (m e) -> p m e", e=2),
+            in_=q_bias_bf[:].rearrange("p (m e) -> p m e", e=2)[:, :, ::-1],
+        )
+        nc.vector.tensor_copy(out=v_bias[:], in_=v_bias_bf[:])
+        bias_tab = consts.tile([P, rows, HEADS, HALF], F32)
+        bias_cos = setup.tile([P, rows, HEADS, HALF], F32)
+        bias_sin = setup.tile([P, rows, HEADS, HALF], F32)
+        for half in range(2):
+            half_rows = slice(half * UNIT, (half + 1) * UNIT)
+            shape = [P, UNIT, HEADS, HALF]
+            for product, bias, table in (
+                (bias_cos, q_bias, cos_tab), (bias_sin, q_bias_swapped, sin_tab)
+            ):
+                nc.gpsimd.tensor_tensor(
+                    out=product[:, half_rows],
+                    in0=bias[:].rearrange("p (h g d) -> p g h d", h=HEADS, g=2)[:, half]
+                    .unsqueeze(1).to_broadcast(shape),
+                    in1=table[:, half_rows].rearrange("p i m e -> p i (m e)")
+                    .unsqueeze(2).to_broadcast(shape),
+                    op=ALU.mult,
+                )
+        nc.gpsimd.tensor_tensor(out=bias_tab[:], in0=bias_cos[:], in1=bias_sin[:], op=ALU.add)
+
+        for g in range(2, ahead):
+            for slot in range(groups[g][2]):
+                stats_of_tile(g, slot)
+        prepare(0)
+        project(0)
+        project(1)
+
+        for j, (g, slot) in enumerate(tiles):
+            rotate(j)
+            if j + 2 < len(tiles):
+                if tiles[j + 2][1] == 0:
+                    prepare(tiles[j + 2][0])
+                project(j + 2)
+            if g + ahead < len(groups):
+                stats_of_tile(g + ahead, slot)
+            s, first, count = groups[g]
+            if first + slot == UNIT - 1:
+                store(s)

@@ -22,6 +22,7 @@ DH = 64
 HALF = 32
 FREQS = 16
 UNIT = 7
+TILES = UNIT * UNIT
 BANK_TILES = 4
 EPS = 1e-6
 THETA = 10000.0
@@ -35,20 +36,20 @@ def tile_block_pa_t_kernel(
     v_w_words, v_w_scales, v_b, out_0, out_1, out_2,
 ):
     nc = tc.nc
-    groups = [
+    pieces = [
         (s, first, min(BANK_TILES, UNIT - first))
         for s in range(UNIT) for first in range(0, UNIT, BANK_TILES)
     ]
-    tiles = [(g, slot) for g, (s, first, count) in enumerate(groups) for slot in range(count)]
+    groups = [list(range(first, min(first + BANK_TILES, TILES))) for first in range(0, TILES, BANK_TILES)]
 
     with ExitStack() as ctx:
         consts = ctx.enter_context(tc.tile_pool(name="consts", bufs=1))
         setup = ctx.enter_context(tc.tile_pool(name="setup", bufs=1))
         x_pool = ctx.enter_context(tc.tile_pool(name="x", bufs=1))
         small = ctx.enter_context(tc.tile_pool(name="small", bufs=4))
-        xhat_pool = ctx.enter_context(tc.tile_pool(name="xhat", bufs=2 * BANK_TILES))
-        quant = ctx.enter_context(tc.tile_pool(name="quant", bufs=2))
-        rope = ctx.enter_context(tc.tile_pool(name="rope", bufs=3))
+        xhat_pool = ctx.enter_context(tc.tile_pool(name="xhat", bufs=3 * BANK_TILES))
+        quant = ctx.enter_context(tc.tile_pool(name="quant", bufs=3))
+        rope = ctx.enter_context(tc.tile_pool(name="rope", bufs=4))
         stage_pool = ctx.enter_context(tc.tile_pool(name="stage", bufs=2))
         psum_t = ctx.enter_context(tc.psum_pool(name="psum_t", bufs=1))
         psum_qk = ctx.enter_context(tc.psum_pool(name="psum_qk", bufs=2))
@@ -61,7 +62,7 @@ def tile_block_pa_t_kernel(
         x_sb = [x_pool.tile([P, UNIT, C], BF16, name="x%d" % s) for s in range(UNIT)]
 
         def load_group(g):
-            s, first, count = groups[g]
+            s, first, count = pieces[g]
             nc.sync.dma_start(
                 out=x_sb[s][:, first : first + count, :].rearrange("p c k -> p (c k)"),
                 in_=x_rounds[s, :, :, first * C : (first + count) * C],
@@ -94,7 +95,7 @@ def tile_block_pa_t_kernel(
                     in_=scales[0, 4 * quadrant : 4 * quadrant + 4, :].bitcast(I32),
                 )
         nc.sync.dma_start(out=v_bias_bf[:], in_=v_b.partition_broadcast(P))
-        for g in range(2, len(groups)):
+        for g in range(2, len(pieces)):
             load_group(g)
 
         ident = setup.tile([P, P], F32)
@@ -165,89 +166,104 @@ def tile_block_pa_t_kernel(
         nc.vector.memset(sign[:, 0:1], -1.0)
         nc.vector.memset(sign[:, 1:2], 1.0)
 
-        stats, mean_var, rstd, minus_mean_rstd = {}, {}, {}, {}
-        xhat, banks, grouped, codes, code_scales = {}, {}, {}, {}, {}
-        qk, v, stage = {}, {}, {}
+        stats, mean_var, guess, rstd, minus_mean_rstd = {}, {}, {}, {}, {}
+        xhat, banks, planes, grouped, codes, code_scales = {}, {}, {}, {}, {}, {}
+        qk, v_pair, stage = {}, {}, {}
 
-        def stats_of_tile(g, slot):
-            s, first, count = groups[g]
+        def stats_of_tile(j):
+            s, c = divmod(j, UNIT)
+            g, slot = divmod(j, BANK_TILES)
             if slot == 0:
                 stats[g] = small.tile([P, BANK_TILES, 6], F32, name="stats")
                 mean_var[g] = small.tile([P, BANK_TILES, 2], F32, name="mean_var")
-            nc.vector.bn_stats(out=stats[g][:, slot, :], in_=x_sb[s][:, first + slot, :])
+            nc.vector.bn_stats(out=stats[g][:, slot, :], in_=x_sb[s][:, c, :])
             nc.vector.bn_aggr(out=mean_var[g][:, slot, :], in_=stats[g][:, slot, :])
 
-        def finish_stats(g):
-            count = groups[g][2]
+        def first_guess(g):
+            count = len(groups[g])
+            guess[g] = small.tile([P, BANK_TILES], F32, name="guess")
+            nc.scalar.activation(
+                out=guess[g][:, 0:count], in_=mean_var[g][:, 0:count, 1],
+                func=ACT.Abs_reciprocal_sqrt, bias=EPS,
+            )
+
+        def newton(g):
+            count = len(groups[g])
             mean = mean_var[g][:, 0:count, 0]
             var = mean_var[g][:, 0:count, 1]
-            guess = small.tile([P, BANK_TILES], F32, name="guess")
-            nc.scalar.activation(out=guess[:, 0:count], in_=var, func=ACT.Abs_reciprocal_sqrt, bias=EPS)
-            newton = small.tile([P, 3, BANK_TILES], F32, name="newton")
-            nc.vector.scalar_tensor_tensor(
-                out=newton[:, 0, 0:count], in0=var, scalar=EPS, in1=guess[:, 0:count],
-                op0=ALU.add, op1=ALU.mult,
+            y = guess[g][:, 0:count]
+            half = small.tile([P, BANK_TILES], F32, name="half")
+            square = small.tile([P, BANK_TILES], F32, name="square")
+            product = small.tile([P, BANK_TILES], F32, name="product")
+            factor = small.tile([P, BANK_TILES], F32, name="factor")
+            mean_rstd = small.tile([P, BANK_TILES], F32, name="mean_rstd")
+            rstd[g] = small.tile([P, BANK_TILES], F32, name="rstd")
+            minus_mean_rstd[g] = small.tile([P, BANK_TILES], F32, name="minus_mean_rstd")
+            nc.gpsimd.tensor_scalar(
+                out=half[:, 0:count], in0=var, scalar1=-0.5, scalar2=-0.5 * EPS, op0=ALU.mult, op1=ALU.add
             )
-            nc.vector.tensor_tensor(
-                out=newton[:, 1, 0:count], in0=newton[:, 0, 0:count], in1=guess[:, 0:count], op=ALU.mult
+            nc.gpsimd.tensor_tensor(out=square[:, 0:count], in0=y, in1=y, op=ALU.mult)
+            nc.gpsimd.tensor_tensor(
+                out=product[:, 0:count], in0=half[:, 0:count], in1=square[:, 0:count], op=ALU.mult
             )
-            nc.vector.tensor_scalar(
-                out=newton[:, 2, 0:count], in0=newton[:, 1, 0:count], scalar1=-0.5, scalar2=1.5,
+            nc.gpsimd.tensor_scalar(
+                out=factor[:, 0:count], in0=product[:, 0:count], scalar1=1.0, scalar2=1.5,
                 op0=ALU.mult, op1=ALU.add,
             )
-            rstd[g] = small.tile([P, BANK_TILES], F32, name="rstd")
-            nc.vector.tensor_tensor(
-                out=rstd[g][:, 0:count], in0=guess[:, 0:count], in1=newton[:, 2, 0:count], op=ALU.mult
+            nc.gpsimd.tensor_tensor(out=rstd[g][:, 0:count], in0=y, in1=factor[:, 0:count], op=ALU.mult)
+            nc.gpsimd.tensor_tensor(
+                out=mean_rstd[:, 0:count], in0=mean, in1=rstd[g][:, 0:count], op=ALU.mult
             )
-            minus_mean_rstd[g] = small.tile([P, BANK_TILES], F32, name="minus_mean_rstd")
-            nc.vector.scalar_tensor_tensor(
-                out=minus_mean_rstd[g][:, 0:count], in0=mean, scalar=-1.0, in1=rstd[g][:, 0:count],
-                op0=ALU.mult, op1=ALU.mult,
+            nc.gpsimd.tensor_scalar(
+                out=minus_mean_rstd[g][:, 0:count], in0=mean_rstd[:, 0:count], scalar1=-1.0, scalar2=0.0,
+                op0=ALU.mult, op1=ALU.add,
             )
 
-        def normalise(g):
-            s, first, count = groups[g]
-            xhat[g] = []
-            for slot in range(count):
-                normal = xhat_pool.tile([P, PACK, P], F32, name="xhat")
-                nc.scalar.activation(
-                    out=normal[:], in_=x_sb[s][:, first + slot, :].rearrange("p (q t) -> p t q", t=PACK),
-                    func=ACT.Identity, scale=rstd[g][:, slot : slot + 1],
-                    bias=minus_mean_rstd[g][:, slot : slot + 1],
-                )
-                xhat[g].append(normal)
+        def normalise(j):
+            s, c = divmod(j, UNIT)
+            g, slot = divmod(j, BANK_TILES)
+            xhat[j] = xhat_pool.tile([P, PACK, P], F32, name="xhat")
+            nc.scalar.activation(
+                out=xhat[j][:], in_=x_sb[s][:, c, :].rearrange("p (q t) -> p t q", t=PACK),
+                func=ACT.Identity, scale=rstd[g][:, slot : slot + 1],
+                bias=minus_mean_rstd[g][:, slot : slot + 1],
+            )
 
-        def transpose(g):
-            banks[g] = [psum_t.tile([P, BANK_TILES * P], F32, name="bank%d" % t) for t in range(PACK)]
-            for slot, normal in enumerate(xhat[g]):
-                for t in range(PACK):
-                    nc.tensor.transpose(banks[g][t][:, slot * P : (slot + 1) * P], normal[:, t, :], order[:])
+        def transpose(g, t):
+            banks[g, t] = psum_t.tile([P, BANK_TILES * P], F32, name="bank%d" % t)
+            for slot, j in enumerate(groups[g]):
+                nc.tensor.transpose(banks[g, t][:, slot * P : (slot + 1) * P], xhat[j][:, t, :], order[:])
 
-        def affine(g):
-            cols = groups[g][2] * P
-            planes = quant.tile([P, PACK, BANK_TILES * P], BF16, name="planes")
-            for t in range(PACK):
-                nc.scalar.activation(
-                    out=planes[:, t, 0:cols], in_=banks[g][t][:, 0:cols], func=ACT.Identity,
-                    scale=gain[:, t : t + 1], bias=shift[:, t : t + 1],
-                )
-            grouped[g] = quant.tile([P, BANK_TILES * P, PACK], BF16, name="grouped", align_bytes=64)
+        def affine(g, t):
+            cols = len(groups[g]) * P
+            if t == 0:
+                planes[g] = quant.tile([P, PACK, BANK_TILES * P], BF16, name="planes")
+            nc.scalar.activation(
+                out=planes[g][:, t, 0:cols], in_=banks[g, t][:, 0:cols], func=ACT.Identity,
+                scale=gain[:, t : t + 1], bias=shift[:, t : t + 1],
+            )
+
+        def interleave(j):
+            g, slot = divmod(j, BANK_TILES)
+            if slot == 0:
+                grouped[g] = quant.tile([P, BANK_TILES * P, PACK], BF16, name="grouped", align_bytes=64)
+            tokens = slice(slot * P, (slot + 1) * P)
             nc.scalar.copy(
-                out=grouped[g][:, 0:cols, :], in_=planes[:, :, 0:cols].rearrange("p t j -> p j t")
+                out=grouped[g][:, tokens, :], in_=planes[g][:, :, tokens].rearrange("p t j -> p j t")
             )
 
         def quantise(g):
+            cols = len(groups[g]) * P
             codes[g] = quant.tile([P, BANK_TILES * P], U32, name="codes", align_bytes=64)
             code_scales[g] = quant.tile([P, BANK_TILES * P], U8, name="code_scales", align_bytes=64)
-            for slot in range(groups[g][2]):
-                tokens = slice(slot * P, (slot + 1) * P)
-                nc.vector.quantize_mx(
-                    out=codes[g][:, tokens].bitcast(FP8X4), scales=code_scales[g][:, tokens],
-                    in_=grouped[g][:, tokens, :].rearrange("p j t -> p (j t)"),
-                )
+            nc.vector.quantize_mx(
+                out=codes[g][:, 0:cols].bitcast(FP8X4), scales=code_scales[g][:, 0:cols],
+                in_=grouped[g][:, 0:cols, :].rearrange("p j t -> p (j t)"),
+            )
 
         def project(j):
-            g, slot = tiles[j]
+            s, c = divmod(j, UNIT)
+            g, slot = divmod(j, BANK_TILES)
             tokens = slice(slot * P, (slot + 1) * P)
             qk[j] = psum_qk.tile([P, 2 * E], F32, name="qk")
             nc.tensor.matmul_mx(
@@ -255,51 +271,58 @@ def tile_block_pa_t_kernel(
                 rhs=w_words[:, 0 : 2 * E * PACK].bitcast(FP8X4), rhs_scale=w_scales[:, 0 : 2 * E],
                 start=True, stop=True,
             )
-            v[j] = psum_v.tile([P, E], F32, name="v")
+            if c % 2 == 0:
+                v_pair[s, c // 2] = psum_v.tile([P, 2, E], F32, name="v")
             nc.tensor.matmul_mx(
-                out=v[j][:], lhsT=codes[g][:, tokens].bitcast(FP8X4), lhsT_scale=code_scales[g][:, tokens],
+                out=v_pair[s, c // 2][:, c % 2, :],
+                lhsT=codes[g][:, tokens].bitcast(FP8X4), lhsT_scale=code_scales[g][:, tokens],
                 rhs=w_words[:, 2 * E * PACK : 3 * E * PACK].bitcast(FP8X4),
                 rhs_scale=w_scales[:, 2 * E : 3 * E], start=True, stop=True,
             )
 
         def rotate(j):
-            g, slot = tiles[j]
-            s, first, count = groups[g]
-            c = first + slot
+            s, c = divmod(j, UNIT)
             if c == 0:
                 stage[s] = stage_pool.tile([P, 3 * HEADS, UNIT, DH], F32, name="stage")
             halves = slice(s, UNIT + c + 1, UNIT + c - s)
             shape = [P, 2 * HEADS, 2, FREQS, 2]
-            by_cos = rope.tile([P, 2 * E], F32, name="by_cos")
-            by_sin = rope.tile([P, 2 * E], F32, name="by_sin")
+            cos_part = rope.tile([P, 2 * E], F32, name="by_cos")
+            sin_part = rope.tile([P, 2 * E], F32, name="by_sin")
             nc.vector.tensor_tensor(
-                out=by_cos[:].rearrange("p (a g m e) -> p a g m e", g=2, m=FREQS, e=2),
+                out=cos_part[:].rearrange("p (a g m e) -> p a g m e", g=2, m=FREQS, e=2),
                 in0=qk[j][:].rearrange("p (a g m e) -> p a g m e", g=2, m=FREQS, e=2),
                 in1=cos_tab[:, halves].unsqueeze(1).to_broadcast(shape),
                 op=ALU.mult,
             )
+            nc.gpsimd.tensor_tensor(
+                out=cos_part[:, 0:E].rearrange("p (h g d) -> p h g d", h=HEADS, g=2),
+                in0=cos_part[:, 0:E].rearrange("p (h g d) -> p h g d", h=HEADS, g=2),
+                in1=bias_tab[:, halves].rearrange("p g h d -> p h g d"),
+                op=ALU.add,
+            )
             nc.vector.tensor_tensor(
-                out=by_sin[:].rearrange("p (a g m e) -> p a g m e", g=2, m=FREQS, e=2),
+                out=sin_part[:].rearrange("p (a g m e) -> p a g m e", g=2, m=FREQS, e=2),
                 in0=qk[j][:].rearrange("p (a g m e) -> p a g m e", g=2, m=FREQS, e=2)[:, :, :, :, ::-1],
                 in1=sin_tab[:, halves].unsqueeze(1).to_broadcast(shape),
                 op=ALU.mult,
             )
             nc.gpsimd.tensor_tensor(
                 out=stage[s][:, 0 : 2 * HEADS, c, :],
-                in0=by_cos[:].rearrange("p (a d) -> p a d", d=DH),
-                in1=by_sin[:].rearrange("p (a d) -> p a d", d=DH),
+                in0=cos_part[:].rearrange("p (a d) -> p a d", d=DH),
+                in1=sin_part[:].rearrange("p (a d) -> p a d", d=DH),
                 op=ALU.add,
             )
-            nc.gpsimd.tensor_tensor(
-                out=stage[s][:, 0:HEADS, c, :].rearrange("p h (g d) -> p h g d", g=2),
-                in0=stage[s][:, 0:HEADS, c, :].rearrange("p h (g d) -> p h g d", g=2),
-                in1=bias_tab[:, halves].rearrange("p g h d -> p h g d"),
-                op=ALU.add,
-            )
+
+        def bias_v(j):
+            s, c = divmod(j, UNIT)
+            if c % 2 == 0 and c != UNIT - 1:
+                return
+            count = c % 2 + 1
+            first = c + 1 - count
             nc.vector.tensor_tensor(
-                out=stage[s][:, 2 * HEADS : 3 * HEADS, c, :],
-                in0=v[j][:].rearrange("p (h d) -> p h d", d=DH),
-                in1=v_bias[:].rearrange("p (h d) -> p h d", d=DH),
+                out=stage[s][:, 2 * HEADS : 3 * HEADS, first : first + count, :].rearrange("p h c d -> p c h d"),
+                in0=v_pair[s, c // 2][:, 0:count, :].rearrange("p c (h d) -> p c h d", d=DH),
+                in1=v_bias[:].rearrange("p (h d) -> p h d", d=DH).unsqueeze(1).to_broadcast([P, count, HEADS, DH]),
                 op=ALU.add,
             )
 
@@ -316,86 +339,99 @@ def tile_block_pa_t_kernel(
                         in_=stage[s][f:P:2, a].rearrange("p c d -> p (c d)"),
                     )
 
-        def prepare(g):
-            if g + 1 < len(groups):
-                transpose(g + 1)
-            if g + 2 < len(groups):
-                finish_stats(g + 2)
-            quantise(g)
-            if g + 2 < len(groups):
-                normalise(g + 2)
-            if g + 1 < len(groups):
-                affine(g + 1)
-
-        ahead = 4
-        for g in range(2):
-            for slot in range(groups[g][2]):
-                stats_of_tile(g, slot)
-            finish_stats(g)
-            normalise(g)
         gain = consts.tile([P, PACK], F32)
         shift = consts.tile([P, PACK], F32)
         nc.vector.tensor_copy(out=gain[:], in_=gain_bf[:])
         nc.vector.tensor_copy(out=shift[:], in_=shift_bf[:])
-        transpose(0)
-        affine(0)
-
         cos_tab = consts.tile([P, rows, FREQS, 2], F32)
         sin_tab = consts.tile([P, rows, FREQS, 2], F32)
-        pairs = rows * FREQS
-        nc.vector.tensor_copy(
-            out=cos_tab[:].rearrange("p i m e -> p (i m) e"),
-            in_=cos_sin[:, 0].rearrange("p i m -> p (i m)").unsqueeze(2).to_broadcast([P, pairs, 2]),
-        )
-        nc.vector.tensor_tensor(
-            out=sin_tab[:].rearrange("p i m e -> p (i m) e"),
-            in0=cos_sin[:, 1].rearrange("p i m -> p (i m)").unsqueeze(2).to_broadcast([P, pairs, 2]),
-            in1=sign[:].unsqueeze(1).to_broadcast([P, pairs, 2]),
-            op=ALU.mult,
-        )
         q_bias = setup.tile([P, E], F32)
         q_bias_swapped = setup.tile([P, E], F32)
         v_bias = consts.tile([P, E], F32)
-        nc.vector.tensor_copy(out=q_bias[:], in_=q_bias_bf[:])
-        nc.vector.tensor_copy(
-            out=q_bias_swapped[:].rearrange("p (m e) -> p m e", e=2),
-            in_=q_bias_bf[:].rearrange("p (m e) -> p m e", e=2)[:, :, ::-1],
-        )
-        nc.vector.tensor_copy(out=v_bias[:], in_=v_bias_bf[:])
         bias_tab = consts.tile([P, rows, HEADS, HALF], F32)
         bias_cos = setup.tile([P, rows, HEADS, HALF], F32)
         bias_sin = setup.tile([P, rows, HEADS, HALF], F32)
-        for half in range(2):
+
+        def vector_tables():
+            pairs = rows * FREQS
+            nc.vector.tensor_copy(
+                out=cos_tab[:].rearrange("p i m e -> p (i m) e"),
+                in_=cos_sin[:, 0].rearrange("p i m -> p (i m)").unsqueeze(2).to_broadcast([P, pairs, 2]),
+            )
+            nc.vector.tensor_tensor(
+                out=sin_tab[:].rearrange("p i m e -> p (i m) e"),
+                in0=cos_sin[:, 1].rearrange("p i m -> p (i m)").unsqueeze(2).to_broadcast([P, pairs, 2]),
+                in1=sign[:].unsqueeze(1).to_broadcast([P, pairs, 2]),
+                op=ALU.mult,
+            )
+            nc.vector.tensor_copy(out=q_bias[:], in_=q_bias_bf[:])
+            nc.vector.tensor_copy(
+                out=q_bias_swapped[:].rearrange("p (m e) -> p m e", e=2),
+                in_=q_bias_bf[:].rearrange("p (m e) -> p m e", e=2)[:, :, ::-1],
+            )
+            nc.vector.tensor_copy(out=v_bias[:], in_=v_bias_bf[:])
+
+        def bias_product(half, product, bias, table):
             half_rows = slice(half * UNIT, (half + 1) * UNIT)
             shape = [P, UNIT, HEADS, HALF]
-            for product, bias, table in (
-                (bias_cos, q_bias, cos_tab), (bias_sin, q_bias_swapped, sin_tab)
-            ):
-                nc.gpsimd.tensor_tensor(
-                    out=product[:, half_rows],
-                    in0=bias[:].rearrange("p (h g d) -> p g h d", h=HEADS, g=2)[:, half]
-                    .unsqueeze(1).to_broadcast(shape),
-                    in1=table[:, half_rows].rearrange("p i m e -> p i (m e)")
-                    .unsqueeze(2).to_broadcast(shape),
-                    op=ALU.mult,
-                )
-        nc.gpsimd.tensor_tensor(out=bias_tab[:], in0=bias_cos[:], in1=bias_sin[:], op=ALU.add)
+            nc.gpsimd.tensor_tensor(
+                out=product[:, half_rows],
+                in0=bias[:].rearrange("p (h g d) -> p g h d", h=HEADS, g=2)[:, half]
+                .unsqueeze(1).to_broadcast(shape),
+                in1=table[:, half_rows].rearrange("p i m e -> p i (m e)")
+                .unsqueeze(2).to_broadcast(shape),
+                op=ALU.mult,
+            )
 
-        for g in range(2, ahead):
-            for slot in range(groups[g][2]):
-                stats_of_tile(g, slot)
-        prepare(0)
-        project(0)
-        project(1)
+        def bias_sum(half):
+            half_rows = slice(half * UNIT, (half + 1) * UNIT)
+            nc.gpsimd.tensor_tensor(
+                out=bias_tab[:, half_rows], in0=bias_cos[:, half_rows], in1=bias_sin[:, half_rows], op=ALU.add
+            )
 
-        for j, (g, slot) in enumerate(tiles):
-            rotate(j)
-            if j + 2 < len(tiles):
-                if tiles[j + 2][1] == 0:
-                    prepare(tiles[j + 2][0])
-                project(j + 2)
-            if g + ahead < len(groups):
-                stats_of_tile(g + ahead, slot)
-            s, first, count = groups[g]
-            if first + slot == UNIT - 1:
-                store(s)
+        gpsimd_tables = {
+            -18: lambda: bias_product(0, bias_cos, q_bias, cos_tab),
+            -17: lambda: bias_product(0, bias_sin, q_bias_swapped, sin_tab),
+            -14: lambda: bias_product(1, bias_cos, q_bias, cos_tab),
+            -13: lambda: bias_product(1, bias_sin, q_bias_swapped, sin_tab),
+            -10: lambda: bias_sum(0),
+            -9: lambda: bias_sum(1),
+        }
+
+        STATS, GUESS, NEWTON, NORMALISE, TRANSPOSE, AFFINE, INTERLEAVE, QUANTISE, PROJECT = (
+            28, 20, 19, 17, 13, 12, 8, 3, 2
+        )
+        for step in range(-STATS, TILES):
+            g, slot = divmod(step + QUANTISE, BANK_TILES)
+            if slot == 0 and 0 <= g < len(groups):
+                quantise(g)
+            g, t = divmod(step + TRANSPOSE, BANK_TILES)
+            if 0 <= g < len(groups):
+                transpose(g, t)
+            if step >= 0:
+                rotate(step)
+            if 0 <= step + PROJECT < TILES:
+                project(step + PROJECT)
+            if step >= 0:
+                bias_v(step)
+            if step + STATS < TILES:
+                stats_of_tile(step + STATS)
+            if step == 8 - STATS:
+                vector_tables()
+            g, slot = divmod(step + GUESS, BANK_TILES)
+            if slot == 0 and 0 <= g < len(groups):
+                first_guess(g)
+            g, t = divmod(step + AFFINE, BANK_TILES)
+            if 0 <= g < len(groups):
+                affine(g, t)
+            if 0 <= step + INTERLEAVE < TILES:
+                interleave(step + INTERLEAVE)
+            if 0 <= step + NORMALISE < TILES:
+                normalise(step + NORMALISE)
+            g, slot = divmod(step + NEWTON, BANK_TILES)
+            if slot == 0 and 0 <= g < len(groups):
+                newton(g)
+            if step in gpsimd_tables:
+                gpsimd_tables[step]()
+            if step >= 0 and step % UNIT == UNIT - 1:
+                store(step // UNIT)

@@ -47,6 +47,7 @@ def tile_block_pa_t_kernel(
         setup = ctx.enter_context(tc.tile_pool(name="setup", bufs=1))
         x_pool = ctx.enter_context(tc.tile_pool(name="x", bufs=1))
         small = ctx.enter_context(tc.tile_pool(name="small", bufs=4))
+        scratch = ctx.enter_context(tc.tile_pool(name="scratch", bufs=2))
         xhat_pool = ctx.enter_context(tc.tile_pool(name="xhat", bufs=3 * BANK_TILES))
         quant = ctx.enter_context(tc.tile_pool(name="quant", bufs=3))
         rope = ctx.enter_context(tc.tile_pool(name="rope", bufs=4))
@@ -161,63 +162,91 @@ def tile_block_pa_t_kernel(
         )
         cos_sin = setup.tile([P, 2, rows, FREQS], F32)
         nc.scalar.activation(out=cos_sin[:], in_=wrapped[:], func=ACT.Sin)
-        nc.scalar.activation(out=warm[:, 1:2], in_=one[:], func=ACT.Abs_reciprocal_sqrt)
+        nc.scalar.activation(out=warm[:, 1:2], in_=one[:], func=ACT.Sqrt)
         sign = setup.tile([P, 2], F32)
         nc.vector.memset(sign[:, 0:1], -1.0)
         nc.vector.memset(sign[:, 1:2], 1.0)
 
-        stats, mean_var, guess, rstd, minus_mean_rstd = {}, {}, {}, {}, {}
+        stats, mean_var, sums, minus_mean, squares, deviation, rstd, minus_mean_rstd = (
+            {}, {}, {}, {}, {}, {}, {}, {}
+        )
         xhat, banks, planes, grouped, codes, code_scales = {}, {}, {}, {}, {}, {}
         qk, v_pair, stage = {}, {}, {}
+
+        def on_scalar(g):
+            return g % 2 == 1
 
         def stats_of_tile(j):
             s, c = divmod(j, UNIT)
             g, slot = divmod(j, BANK_TILES)
+            if on_scalar(g):
+                return
             if slot == 0:
                 stats[g] = small.tile([P, BANK_TILES, 6], F32, name="stats")
                 mean_var[g] = small.tile([P, BANK_TILES, 2], F32, name="mean_var")
             nc.vector.bn_stats(out=stats[g][:, slot, :], in_=x_sb[s][:, c, :])
+
+        def aggregate(j):
+            g, slot = divmod(j, BANK_TILES)
+            if on_scalar(g):
+                return
             nc.vector.bn_aggr(out=mean_var[g][:, slot, :], in_=stats[g][:, slot, :])
 
-        def first_guess(g):
-            count = len(groups[g])
-            guess[g] = small.tile([P, BANK_TILES], F32, name="guess")
+        def sum_of_tile(j):
+            s, c = divmod(j, UNIT)
+            g, slot = divmod(j, BANK_TILES)
+            if not on_scalar(g):
+                return
+            if slot == 0:
+                sums[g] = small.tile([P, BANK_TILES], F32, name="sums")
+            unread = scratch.tile([P, C], BF16, name="unread")
             nc.scalar.activation(
-                out=guess[g][:, 0:count], in_=mean_var[g][:, 0:count, 1],
-                func=ACT.Abs_reciprocal_sqrt, bias=EPS,
+                out=unread[:], in_=x_sb[s][:, c, :], func=ACT.Identity, accum_out=sums[g][:, slot : slot + 1]
             )
 
-        def newton(g):
+        def mean_of_group(g):
+            minus_mean[g] = small.tile([P, BANK_TILES], F32, name="minus_mean")
+            nc.scalar.activation(out=minus_mean[g][:], in_=sums[g][:], func=ACT.Identity, scale=-1.0 / C)
+
+        def squares_of_tile(j):
+            s, c = divmod(j, UNIT)
+            g, slot = divmod(j, BANK_TILES)
+            if not on_scalar(g):
+                return
+            if slot == 0:
+                squares[g] = small.tile([P, BANK_TILES], F32, name="squares")
+            unread = scratch.tile([P, C], BF16, name="unread")
+            nc.scalar.activation(
+                out=unread[:], in_=x_sb[s][:, c, :], func=ACT.Square, bias=minus_mean[g][:, slot : slot + 1],
+                accum_out=squares[g][:, slot : slot + 1],
+            )
+
+        def root(g):
             count = len(groups[g])
-            mean = mean_var[g][:, 0:count, 0]
-            var = mean_var[g][:, 0:count, 1]
-            y = guess[g][:, 0:count]
-            half = small.tile([P, BANK_TILES], F32, name="half")
-            square = small.tile([P, BANK_TILES], F32, name="square")
-            product = small.tile([P, BANK_TILES], F32, name="product")
-            factor = small.tile([P, BANK_TILES], F32, name="factor")
-            mean_rstd = small.tile([P, BANK_TILES], F32, name="mean_rstd")
+            deviation[g] = small.tile([P, BANK_TILES], F32, name="deviation")
+            if on_scalar(g):
+                nc.scalar.activation(
+                    out=deviation[g][:], in_=squares[g][:], func=ACT.Sqrt, scale=1.0 / C, bias=EPS
+                )
+            else:
+                nc.scalar.activation(
+                    out=deviation[g][:, 0:count], in_=mean_var[g][:, 0:count, 1], func=ACT.Sqrt, bias=EPS
+                )
+
+        def finish_stats(g):
+            count = len(groups[g])
             rstd[g] = small.tile([P, BANK_TILES], F32, name="rstd")
             minus_mean_rstd[g] = small.tile([P, BANK_TILES], F32, name="minus_mean_rstd")
-            nc.gpsimd.tensor_scalar(
-                out=half[:, 0:count], in0=var, scalar1=-0.5, scalar2=-0.5 * EPS, op0=ALU.mult, op1=ALU.add
-            )
-            nc.gpsimd.tensor_tensor(out=square[:, 0:count], in0=y, in1=y, op=ALU.mult)
-            nc.gpsimd.tensor_tensor(
-                out=product[:, 0:count], in0=half[:, 0:count], in1=square[:, 0:count], op=ALU.mult
-            )
-            nc.gpsimd.tensor_scalar(
-                out=factor[:, 0:count], in0=product[:, 0:count], scalar1=1.0, scalar2=1.5,
-                op0=ALU.mult, op1=ALU.add,
-            )
-            nc.gpsimd.tensor_tensor(out=rstd[g][:, 0:count], in0=y, in1=factor[:, 0:count], op=ALU.mult)
-            nc.gpsimd.tensor_tensor(
-                out=mean_rstd[:, 0:count], in0=mean, in1=rstd[g][:, 0:count], op=ALU.mult
-            )
-            nc.gpsimd.tensor_scalar(
-                out=minus_mean_rstd[g][:, 0:count], in0=mean_rstd[:, 0:count], scalar1=-1.0, scalar2=0.0,
-                op0=ALU.mult, op1=ALU.add,
-            )
+            nc.vector.reciprocal(out=rstd[g][:, 0:count], in_=deviation[g][:, 0:count])
+            if on_scalar(g):
+                nc.vector.tensor_tensor(
+                    out=minus_mean_rstd[g][:], in0=minus_mean[g][:], in1=rstd[g][:], op=ALU.mult
+                )
+            else:
+                nc.vector.scalar_tensor_tensor(
+                    out=minus_mean_rstd[g][:, 0:count], in0=mean_var[g][:, 0:count, 0], scalar=-1.0,
+                    in1=rstd[g][:, 0:count], op0=ALU.mult, op1=ALU.mult,
+                )
 
         def normalise(j):
             s, c = divmod(j, UNIT)
@@ -243,13 +272,11 @@ def tile_block_pa_t_kernel(
                 scale=gain[:, t : t + 1], bias=shift[:, t : t + 1],
             )
 
-        def interleave(j):
-            g, slot = divmod(j, BANK_TILES)
-            if slot == 0:
-                grouped[g] = quant.tile([P, BANK_TILES * P, PACK], BF16, name="grouped", align_bytes=64)
-            tokens = slice(slot * P, (slot + 1) * P)
+        def interleave(g):
+            cols = len(groups[g]) * P
+            grouped[g] = quant.tile([P, BANK_TILES * P, PACK], BF16, name="grouped", align_bytes=64)
             nc.scalar.copy(
-                out=grouped[g][:, tokens, :], in_=planes[g][:, :, tokens].rearrange("p t j -> p j t")
+                out=grouped[g][:, 0:cols, :], in_=planes[g][:, :, 0:cols].rearrange("p t j -> p j t")
             )
 
         def quantise(g):
@@ -398,12 +425,16 @@ def tile_block_pa_t_kernel(
             -9: lambda: bias_sum(1),
         }
 
-        STATS, GUESS, NEWTON, NORMALISE, TRANSPOSE, AFFINE, INTERLEAVE, QUANTISE, PROJECT = (
-            28, 20, 19, 17, 13, 12, 8, 3, 2
-        )
-        for step in range(-STATS, TILES):
-            g, slot = divmod(step + QUANTISE, BANK_TILES)
-            if slot == 0 and 0 <= g < len(groups):
+        SUMS, MEAN, SQUARES, STATS, AGGREGATE, ROOT, FINISH = 29, 25, 24, 25, 24, 20, 19
+        NORMALISE, TRANSPOSE, AFFINE, INTERLEAVE, QUANTISE, PROJECT = 17, 13, 12, 8, 3, 2
+
+        def group_due(step, distance):
+            g, slot = divmod(step + distance, BANK_TILES)
+            return g if slot == 0 and 0 <= g < len(groups) else None
+
+        for step in range(-SUMS, TILES):
+            g = group_due(step, QUANTISE)
+            if g is not None:
                 quantise(g)
             g, t = divmod(step + TRANSPOSE, BANK_TILES)
             if 0 <= g < len(groups):
@@ -414,23 +445,33 @@ def tile_block_pa_t_kernel(
                 project(step + PROJECT)
             if step >= 0:
                 bias_v(step)
-            if step + STATS < TILES:
+            if 0 <= step + STATS < TILES:
                 stats_of_tile(step + STATS)
-            if step == 8 - STATS:
+            if 0 <= step + AGGREGATE < TILES:
+                aggregate(step + AGGREGATE)
+            g = group_due(step, FINISH)
+            if g is not None:
+                finish_stats(g)
+            if step == -20:
                 vector_tables()
-            g, slot = divmod(step + GUESS, BANK_TILES)
-            if slot == 0 and 0 <= g < len(groups):
-                first_guess(g)
+            g = group_due(step, ROOT)
+            if g is not None:
+                root(g)
             g, t = divmod(step + AFFINE, BANK_TILES)
             if 0 <= g < len(groups):
                 affine(g, t)
-            if 0 <= step + INTERLEAVE < TILES:
-                interleave(step + INTERLEAVE)
+            g = group_due(step, INTERLEAVE)
+            if g is not None:
+                interleave(g)
             if 0 <= step + NORMALISE < TILES:
                 normalise(step + NORMALISE)
-            g, slot = divmod(step + NEWTON, BANK_TILES)
-            if slot == 0 and 0 <= g < len(groups):
-                newton(g)
+            if 0 <= step + SUMS < TILES:
+                sum_of_tile(step + SUMS)
+            g = group_due(step, MEAN)
+            if g is not None and on_scalar(g):
+                mean_of_group(g)
+            if 0 <= step + SQUARES < TILES:
+                squares_of_tile(step + SQUARES)
             if step in gpsimd_tables:
                 gpsimd_tables[step]()
             if step >= 0 and step % UNIT == UNIT - 1:

@@ -174,7 +174,7 @@ def tile_block_pa_t_kernel(
         qk, v_pair, stage = {}, {}, {}
 
         def on_scalar(g):
-            return g % 2 == 1
+            return g in (2, 4, 6, 8, 10, 11)
 
         def stats_of_tile(j):
             s, c = divmod(j, UNIT)
@@ -252,11 +252,18 @@ def tile_block_pa_t_kernel(
             s, c = divmod(j, UNIT)
             g, slot = divmod(j, BANK_TILES)
             xhat[j] = xhat_pool.tile([P, PACK, P], F32, name="xhat")
-            nc.scalar.activation(
-                out=xhat[j][:], in_=x_sb[s][:, c, :].rearrange("p (q t) -> p t q", t=PACK),
-                func=ACT.Identity, scale=rstd[g][:, slot : slot + 1],
-                bias=minus_mean_rstd[g][:, slot : slot + 1],
-            )
+            source = x_sb[s][:, c, :].rearrange("p (q t) -> p t q", t=PACK)
+            if j >= 2 * BANK_TILES:
+                nc.scalar.activation(
+                    out=xhat[j][:], in_=source, func=ACT.Identity, scale=rstd[g][:, slot : slot + 1],
+                    bias=minus_mean_rstd[g][:, slot : slot + 1],
+                )
+            else:
+                engine = nc.vector if j % 2 == 0 else nc.gpsimd
+                engine.tensor_scalar(
+                    out=xhat[j][:], in0=source, scalar1=rstd[g][:, slot : slot + 1],
+                    scalar2=minus_mean_rstd[g][:, slot : slot + 1], op0=ALU.mult, op1=ALU.add,
+                )
 
         def transpose(g, t):
             banks[g, t] = psum_t.tile([P, BANK_TILES * P], F32, name="bank%d" % t)
@@ -275,9 +282,11 @@ def tile_block_pa_t_kernel(
         def interleave(g):
             cols = len(groups[g]) * P
             grouped[g] = quant.tile([P, BANK_TILES * P, PACK], BF16, name="grouped", align_bytes=64)
-            nc.scalar.copy(
-                out=grouped[g][:, 0:cols, :], in_=planes[g][:, :, 0:cols].rearrange("p t j -> p j t")
-            )
+            source = planes[g][:, :, 0:cols].rearrange("p t j -> p j t")
+            if g % 3 == 0:
+                nc.vector.tensor_copy(out=grouped[g][:, 0:cols, :], in_=source)
+            else:
+                nc.scalar.copy(out=grouped[g][:, 0:cols, :], in_=source)
 
         def quantise(g):
             cols = len(groups[g]) * P
@@ -321,12 +330,13 @@ def tile_block_pa_t_kernel(
                 in1=cos_tab[:, halves].unsqueeze(1).to_broadcast(shape),
                 op=ALU.mult,
             )
-            nc.gpsimd.tensor_tensor(
-                out=cos_part[:, 0:E].rearrange("p (h g d) -> p h g d", h=HEADS, g=2),
-                in0=cos_part[:, 0:E].rearrange("p (h g d) -> p h g d", h=HEADS, g=2),
-                in1=bias_tab[:, halves].rearrange("p g h d -> p h g d"),
-                op=ALU.add,
-            )
+            if s == UNIT - 1:
+                nc.vector.tensor_tensor(
+                    out=cos_part[:, 0:E].rearrange("p (h g d) -> p h g d", h=HEADS, g=2),
+                    in0=cos_part[:, 0:E].rearrange("p (h g d) -> p h g d", h=HEADS, g=2),
+                    in1=bias_tab[:, halves].rearrange("p g h d -> p h g d"),
+                    op=ALU.add,
+                )
             nc.vector.tensor_tensor(
                 out=sin_part[:].rearrange("p (a g m e) -> p a g m e", g=2, m=FREQS, e=2),
                 in0=qk[j][:].rearrange("p (a g m e) -> p a g m e", g=2, m=FREQS, e=2)[:, :, :, :, ::-1],
@@ -339,6 +349,15 @@ def tile_block_pa_t_kernel(
                 in1=sin_part[:].rearrange("p (a d) -> p a d", d=DH),
                 op=ALU.add,
             )
+
+        def bias_q(s):
+            shape = [P, HEADS, UNIT, HALF]
+            for half, table in (
+                (0, bias_tab[:, s].unsqueeze(2).to_broadcast(shape)),
+                (1, bias_tab[:, UNIT : 2 * UNIT].rearrange("p c h d -> p h c d")),
+            ):
+                q_half = stage[s][:, 0:HEADS, :, half * HALF : (half + 1) * HALF]
+                nc.gpsimd.tensor_tensor(out=q_half, in0=q_half, in1=table, op=ALU.add)
 
         def bias_v(j):
             s, c = divmod(j, UNIT)
@@ -358,13 +377,15 @@ def tile_block_pa_t_kernel(
             for o in (out_0, out_1, out_2)
         ]
 
-        def store(s):
-            for a in range(3 * HEADS):
+        def store(s, first, count):
+            for a in list(range(2 * HEADS, 3 * HEADS)) + list(range(2 * HEADS)):
                 for f in range(2):
                     nc.sync.dma_start(
-                        out=out_views[a // HEADS][s, a % HEADS, :, :, f, :],
-                        in_=stage[s][f:P:2, a].rearrange("p c d -> p (c d)"),
+                        out=out_views[a // HEADS][s, a % HEADS, :, :, f, first * DH : (first + count) * DH],
+                        in_=stage[s][f:P:2, a, first : first + count].rearrange("p c d -> p (c d)"),
                     )
+
+        stores = {UNIT * s + UNIT - 1: (s, 0, UNIT) for s in range(UNIT)}
 
         gain = consts.tile([P, PACK], F32)
         shift = consts.tile([P, PACK], F32)
@@ -416,17 +437,18 @@ def tile_block_pa_t_kernel(
                 out=bias_tab[:, half_rows], in0=bias_cos[:, half_rows], in1=bias_sin[:, half_rows], op=ALU.add
             )
 
-        gpsimd_tables = {
-            -18: lambda: bias_product(0, bias_cos, q_bias, cos_tab),
-            -17: lambda: bias_product(0, bias_sin, q_bias_swapped, sin_tab),
-            -14: lambda: bias_product(1, bias_cos, q_bias, cos_tab),
-            -13: lambda: bias_product(1, bias_sin, q_bias_swapped, sin_tab),
-            -10: lambda: bias_sum(0),
-            -9: lambda: bias_sum(1),
+        tables = {
+            -12: vector_tables,
+            -6: lambda: bias_product(0, bias_cos, q_bias, cos_tab),
+            -5: lambda: bias_product(0, bias_sin, q_bias_swapped, sin_tab),
+            -4: lambda: bias_product(1, bias_cos, q_bias, cos_tab),
+            -3: lambda: bias_product(1, bias_sin, q_bias_swapped, sin_tab),
+            -2: lambda: bias_sum(0),
+            -1: lambda: bias_sum(1),
         }
 
-        SUMS, MEAN, SQUARES, STATS, AGGREGATE, ROOT, FINISH = 29, 25, 24, 25, 24, 20, 19
-        NORMALISE, TRANSPOSE, AFFINE, INTERLEAVE, QUANTISE, PROJECT = 17, 13, 12, 8, 3, 2
+        SUMS, MEAN, SQUARES, STATS, AGGREGATE, ROOT, FINISH = 26, 22, 21, 22, 21, 17, 16
+        NORMALISE, TRANSPOSE, AFFINE, INTERLEAVE, QUANTISE, PROJECT = 14, 10, 9, 5, 3, 2
 
         def group_due(step, distance):
             g, slot = divmod(step + distance, BANK_TILES)
@@ -445,6 +467,8 @@ def tile_block_pa_t_kernel(
                 project(step + PROJECT)
             if step >= 0:
                 bias_v(step)
+            if 0 <= step + NORMALISE < TILES:
+                normalise(step + NORMALISE)
             if 0 <= step + STATS < TILES:
                 stats_of_tile(step + STATS)
             if 0 <= step + AGGREGATE < TILES:
@@ -452,8 +476,8 @@ def tile_block_pa_t_kernel(
             g = group_due(step, FINISH)
             if g is not None:
                 finish_stats(g)
-            if step == -20:
-                vector_tables()
+            if step in tables:
+                tables[step]()
             g = group_due(step, ROOT)
             if g is not None:
                 root(g)
@@ -463,8 +487,6 @@ def tile_block_pa_t_kernel(
             g = group_due(step, INTERLEAVE)
             if g is not None:
                 interleave(g)
-            if 0 <= step + NORMALISE < TILES:
-                normalise(step + NORMALISE)
             if 0 <= step + SUMS < TILES:
                 sum_of_tile(step + SUMS)
             g = group_due(step, MEAN)
@@ -472,7 +494,7 @@ def tile_block_pa_t_kernel(
                 mean_of_group(g)
             if 0 <= step + SQUARES < TILES:
                 squares_of_tile(step + SQUARES)
-            if step in gpsimd_tables:
-                gpsimd_tables[step]()
-            if step >= 0 and step % UNIT == UNIT - 1:
-                store(step // UNIT)
+            if step in stores:
+                if stores[step][0] < UNIT - 1:
+                    bias_q(stores[step][0])
+                store(*stores[step])

@@ -51,7 +51,7 @@ def tile_block_pa_t_kernel(
         xhat_pool = ctx.enter_context(tc.tile_pool(name="xhat", bufs=3 * BANK_TILES))
         quant = ctx.enter_context(tc.tile_pool(name="quant", bufs=3))
         rope = ctx.enter_context(tc.tile_pool(name="rope", bufs=4))
-        stage_pool = ctx.enter_context(tc.tile_pool(name="stage", bufs=2))
+        stage_pool = ctx.enter_context(tc.tile_pool(name="stage", bufs=3))
         psum_t = ctx.enter_context(tc.psum_pool(name="psum_t", bufs=1))
         psum_qk = ctx.enter_context(tc.psum_pool(name="psum_qk", bufs=2))
         psum_v = ctx.enter_context(tc.psum_pool(name="psum_v", bufs=2))
@@ -69,34 +69,36 @@ def tile_block_pa_t_kernel(
                 in_=x_rounds[s, :, :, first * C : (first + count) * C],
             )
 
-        load_group(0)
-
+        for g in range(5):
+            load_group(g)
         gain_bf = setup.tile([P, PACK], BF16)
         shift_bf = setup.tile([P, PACK], BF16)
-        nc.sync.dma_start(out=gain_bf[:], in_=ln1_w.rearrange("(p t) -> p t", t=PACK))
-        nc.sync.dma_start(out=shift_bf[:], in_=ln1_b.rearrange("(p t) -> p t", t=PACK))
-        load_group(1)
+        nc.scalar.dma_start(out=gain_bf[:], in_=ln1_w.rearrange("(p t) -> p t", t=PACK))
+        nc.scalar.dma_start(out=shift_bf[:], in_=ln1_b.rearrange("(p t) -> p t", t=PACK))
+        bias_rows = setup.tile([P, 2 * E], BF16)
+        nc.gpsimd.memset(bias_rows[:], 0.0)
+        nc.scalar.dma_start(out=bias_rows[0:1, 0:E], in_=q_b.rearrange("(a n) -> a n", a=1))
+        nc.scalar.dma_start(out=bias_rows[0:1, E : 2 * E], in_=v_b.rearrange("(a n) -> a n", a=1))
+        ones = setup.tile([P, P], BF16)
+        nc.gpsimd.memset(ones[:], 1.0)
+        biases = psum_t.tile([P, 2 * E], F32, name="bank3")
+        nc.tensor.matmul(out=biases[:], lhsT=ones[:], rhs=bias_rows[:], start=True, stop=True)
 
         w_words = consts.tile([P, 3 * E * PACK], U8, align_bytes=64)
         w_scales = consts.tile([P, 3 * E], U8, align_bytes=64)
         nc.vector.memset(w_scales[:].bitcast(I32), 0)
-        q_bias_bf = setup.tile([P, E], BF16)
-        v_bias_bf = setup.tile([P, E], BF16)
-        nc.sync.dma_start(out=q_bias_bf[:], in_=q_b.partition_broadcast(P))
-        for n, (words, scales) in enumerate(
-            ((q_w_words, q_w_scales), (k_w_words, k_w_scales), (v_w_words, v_w_scales))
-        ):
+        for n, words in enumerate((q_w_words, k_w_words, v_w_words)):
             nc.sync.dma_start(
                 out=w_words[:, n * E * PACK : (n + 1) * E * PACK].bitcast(I32),
                 in_=words[0].rearrange("p n t -> p (n t)").bitcast(I32),
             )
+        for n, scales in enumerate((q_w_scales, k_w_scales, v_w_scales)):
             for quadrant in range(4):
                 nc.sync.dma_start(
                     out=w_scales[32 * quadrant : 32 * quadrant + 4, n * E : (n + 1) * E].bitcast(I32),
                     in_=scales[0, 4 * quadrant : 4 * quadrant + 4, :].bitcast(I32),
                 )
-        nc.sync.dma_start(out=v_bias_bf[:], in_=v_b.partition_broadcast(P))
-        for g in range(2, len(pieces)):
+        for g in range(5, len(pieces)):
             load_group(g)
 
         ident = setup.tile([P, P], F32)
@@ -171,7 +173,7 @@ def tile_block_pa_t_kernel(
             {}, {}, {}, {}, {}, {}, {}, {}
         )
         xhat, banks, planes, grouped, codes, code_scales = {}, {}, {}, {}, {}, {}
-        qk, v_pair, stage = {}, {}, {}
+        qk, v_pair, stage, by_cos = {}, {}, {}, {}
 
         def on_scalar(g):
             return g in (2, 4, 6, 8, 10, 11)
@@ -316,37 +318,42 @@ def tile_block_pa_t_kernel(
                 rhs_scale=w_scales[:, 2 * E : 3 * E], start=True, stop=True,
             )
 
-        def rotate(j):
+        def tables_of(j):
+            s, c = divmod(j, UNIT)
+            return slice(s, UNIT + c + 1, UNIT + c - s)
+
+        def times_cos(j):
             s, c = divmod(j, UNIT)
             if c == 0:
                 stage[s] = stage_pool.tile([P, 3 * HEADS, UNIT, DH], F32, name="stage")
-            halves = slice(s, UNIT + c + 1, UNIT + c - s)
-            shape = [P, 2 * HEADS, 2, FREQS, 2]
-            cos_part = rope.tile([P, 2 * E], F32, name="by_cos")
-            sin_part = rope.tile([P, 2 * E], F32, name="by_sin")
+            by_cos[j] = rope.tile([P, 2 * E], F32, name="by_cos")
             nc.vector.tensor_tensor(
-                out=cos_part[:].rearrange("p (a g m e) -> p a g m e", g=2, m=FREQS, e=2),
+                out=by_cos[j][:].rearrange("p (a g m e) -> p a g m e", g=2, m=FREQS, e=2),
                 in0=qk[j][:].rearrange("p (a g m e) -> p a g m e", g=2, m=FREQS, e=2),
-                in1=cos_tab[:, halves].unsqueeze(1).to_broadcast(shape),
+                in1=cos_tab[:, tables_of(j)].unsqueeze(1).to_broadcast([P, 2 * HEADS, 2, FREQS, 2]),
                 op=ALU.mult,
             )
+
+        def times_sin(j):
+            s, c = divmod(j, UNIT)
             if s == UNIT - 1:
                 nc.vector.tensor_tensor(
-                    out=cos_part[:, 0:E].rearrange("p (h g d) -> p h g d", h=HEADS, g=2),
-                    in0=cos_part[:, 0:E].rearrange("p (h g d) -> p h g d", h=HEADS, g=2),
-                    in1=bias_tab[:, halves].rearrange("p g h d -> p h g d"),
+                    out=by_cos[j][:, 0:E].rearrange("p (h g d) -> p h g d", h=HEADS, g=2),
+                    in0=by_cos[j][:, 0:E].rearrange("p (h g d) -> p h g d", h=HEADS, g=2),
+                    in1=bias_tab[:, tables_of(j)].rearrange("p g h d -> p h g d"),
                     op=ALU.add,
                 )
+            by_sin = rope.tile([P, 2 * E], F32, name="by_sin")
             nc.vector.tensor_tensor(
-                out=sin_part[:].rearrange("p (a g m e) -> p a g m e", g=2, m=FREQS, e=2),
+                out=by_sin[:].rearrange("p (a g m e) -> p a g m e", g=2, m=FREQS, e=2),
                 in0=qk[j][:].rearrange("p (a g m e) -> p a g m e", g=2, m=FREQS, e=2)[:, :, :, :, ::-1],
-                in1=sin_tab[:, halves].unsqueeze(1).to_broadcast(shape),
+                in1=sin_tab[:, tables_of(j)].unsqueeze(1).to_broadcast([P, 2 * HEADS, 2, FREQS, 2]),
                 op=ALU.mult,
             )
             nc.gpsimd.tensor_tensor(
                 out=stage[s][:, 0 : 2 * HEADS, c, :],
-                in0=cos_part[:].rearrange("p (a d) -> p a d", d=DH),
-                in1=sin_part[:].rearrange("p (a d) -> p a d", d=DH),
+                in0=by_cos[j][:].rearrange("p (a d) -> p a d", d=DH),
+                in1=by_sin[:].rearrange("p (a d) -> p a d", d=DH),
                 op=ALU.add,
             )
 
@@ -385,7 +392,11 @@ def tile_block_pa_t_kernel(
                         in_=stage[s][f:P:2, a, first : first + count].rearrange("p c d -> p (c d)"),
                     )
 
-        stores = {UNIT * s + UNIT - 1: (s, 0, UNIT) for s in range(UNIT)}
+        stores = {}
+        for s in range(UNIT - 1):
+            last = UNIT * s + UNIT - 1
+            stores[last + (1 - last) % BANK_TILES] = (s, 0, UNIT)
+        stores[TILES - 1] = (UNIT - 1, 0, UNIT)
 
         gain = consts.tile([P, PACK], F32)
         shift = consts.tile([P, PACK], F32)
@@ -412,12 +423,12 @@ def tile_block_pa_t_kernel(
                 in1=sign[:].unsqueeze(1).to_broadcast([P, pairs, 2]),
                 op=ALU.mult,
             )
-            nc.vector.tensor_copy(out=q_bias[:], in_=q_bias_bf[:])
+            nc.vector.tensor_copy(out=q_bias[:], in_=biases[:, 0:E])
             nc.vector.tensor_copy(
                 out=q_bias_swapped[:].rearrange("p (m e) -> p m e", e=2),
-                in_=q_bias_bf[:].rearrange("p (m e) -> p m e", e=2)[:, :, ::-1],
+                in_=biases[:, 0:E].rearrange("p (m e) -> p m e", e=2)[:, :, ::-1],
             )
-            nc.vector.tensor_copy(out=v_bias[:], in_=v_bias_bf[:])
+            nc.vector.tensor_copy(out=v_bias[:], in_=biases[:, E : 2 * E])
 
         def bias_product(half, product, bias, table):
             half_rows = slice(half * UNIT, (half + 1) * UNIT)
@@ -433,18 +444,14 @@ def tile_block_pa_t_kernel(
 
         def bias_sum(half):
             half_rows = slice(half * UNIT, (half + 1) * UNIT)
-            nc.gpsimd.tensor_tensor(
+            nc.vector.tensor_tensor(
                 out=bias_tab[:, half_rows], in0=bias_cos[:, half_rows], in1=bias_sin[:, half_rows], op=ALU.add
             )
 
-        tables = {
-            -12: vector_tables,
-            -6: lambda: bias_product(0, bias_cos, q_bias, cos_tab),
-            -5: lambda: bias_product(0, bias_sin, q_bias_swapped, sin_tab),
-            -4: lambda: bias_product(1, bias_cos, q_bias, cos_tab),
-            -3: lambda: bias_product(1, bias_sin, q_bias_swapped, sin_tab),
-            -2: lambda: bias_sum(0),
-            -1: lambda: bias_sum(1),
+        tables = {-12: vector_tables, 7: lambda: bias_sum(0), 8: lambda: bias_sum(1)}
+        products = {
+            1: ((0, bias_cos, q_bias, cos_tab), (0, bias_sin, q_bias_swapped, sin_tab)),
+            5: ((1, bias_cos, q_bias, cos_tab), (1, bias_sin, q_bias_swapped, sin_tab)),
         }
 
         SUMS, MEAN, SQUARES, STATS, AGGREGATE, ROOT, FINISH = 26, 22, 21, 22, 21, 17, 16
@@ -455,17 +462,11 @@ def tile_block_pa_t_kernel(
             return g if slot == 0 and 0 <= g < len(groups) else None
 
         for step in range(-SUMS, TILES):
-            g = group_due(step, QUANTISE)
-            if g is not None:
-                quantise(g)
             g, t = divmod(step + TRANSPOSE, BANK_TILES)
             if 0 <= g < len(groups):
                 transpose(g, t)
             if step >= 0:
-                rotate(step)
-            if 0 <= step + PROJECT < TILES:
-                project(step + PROJECT)
-            if step >= 0:
+                times_cos(step)
                 bias_v(step)
             if 0 <= step + NORMALISE < TILES:
                 normalise(step + NORMALISE)
@@ -473,6 +474,9 @@ def tile_block_pa_t_kernel(
                 stats_of_tile(step + STATS)
             if 0 <= step + AGGREGATE < TILES:
                 aggregate(step + AGGREGATE)
+            g = group_due(step, QUANTISE)
+            if g is not None:
+                quantise(g)
             g = group_due(step, FINISH)
             if g is not None:
                 finish_stats(g)
@@ -494,6 +498,12 @@ def tile_block_pa_t_kernel(
                 mean_of_group(g)
             if 0 <= step + SQUARES < TILES:
                 squares_of_tile(step + SQUARES)
+            if step >= 0:
+                times_sin(step)
+            if 0 <= step + PROJECT < TILES:
+                project(step + PROJECT)
+            for arguments in products.get(step, ()):
+                bias_product(*arguments)
             if step in stores:
                 if stores[step][0] < UNIT - 1:
                     bias_q(stores[step][0])

@@ -30,23 +30,39 @@ STEP = 16.0 / 14.0
 
 FLOPS = 2 * 2 * 56 * 56 * C * 3 * E
 
+SUMS, MEAN, SQUARES, STATS, AGGREGATE, ROOT, FINISH = 25, 21, 20, 21, 20, 16, 15
+NORMALISE, TRANSPOSE, AFFINE, INTERLEAVE, QUANTISE, PROJECT = 14, 10, 9, 5, 3, 2
+S_STATS = (3, 6, 9)
+V_INTER = (0, 1)
+V_AFF = ((0, 1), (0, 3), (1, 1), (1, 3))
+V_NORM = (0, 1, 3)
+G_NORM = (2, 4, 5, 6, 7, 8)
+Q_AFTER = False
+G_BIAS_STEP = True
+TABLES_AT, SUM0_AT, SUM1_AT = -14, -4, -3
+PROD0_AT, PROD1_AT = -6, -5
+XFIRST = 4
+
 
 def tile_block_pa_t_kernel(
     tc, x, ln1_w, ln1_b, q_w_words, q_w_scales, q_b, k_w_words, k_w_scales,
     v_w_words, v_w_scales, v_b, out_0, out_1, out_2,
 ):
     nc = tc.nc
-    pieces = [
-        (s, first, min(BANK_TILES, UNIT - first))
-        for s in range(UNIT) for first in range(0, UNIT, BANK_TILES)
-    ]
-    groups = [list(range(first, min(first + BANK_TILES, TILES))) for first in range(0, TILES, BANK_TILES)]
+    pieces = [(0, 0, 1), (0, 1, 3), (0, 4, 3)]
+    pieces += [(s, first, min(4, UNIT - first)) for s in range(1, UNIT) for first in (0, 4)]
+    lead = BANK_TILES - 1
+    groups = [[j for j in range(first, first + BANK_TILES) if j >= 0] for first in range(-lead, TILES, BANK_TILES)]
+
+    def place_of(j):
+        g = (j + lead) // BANK_TILES
+        return g, j - groups[g][0]
 
     with ExitStack() as ctx:
         consts = ctx.enter_context(tc.tile_pool(name="consts", bufs=1))
         setup = ctx.enter_context(tc.tile_pool(name="setup", bufs=1))
         x_pool = ctx.enter_context(tc.tile_pool(name="x", bufs=1))
-        small = ctx.enter_context(tc.tile_pool(name="small", bufs=4))
+        small = ctx.enter_context(tc.tile_pool(name="small", bufs=6))
         scratch = ctx.enter_context(tc.tile_pool(name="scratch", bufs=2))
         xhat_pool = ctx.enter_context(tc.tile_pool(name="xhat", bufs=3 * BANK_TILES))
         quant = ctx.enter_context(tc.tile_pool(name="quant", bufs=3))
@@ -62,23 +78,30 @@ def tile_block_pa_t_kernel(
         )
         x_sb = [x_pool.tile([P, UNIT, C], BF16, name="x%d" % s) for s in range(UNIT)]
 
-        def load_group(g):
-            s, first, count = pieces[g]
+        def load_piece(n):
+            s, first, count = pieces[n]
             nc.sync.dma_start(
                 out=x_sb[s][:, first : first + count, :].rearrange("p c k -> p (c k)"),
                 in_=x_rounds[s, :, :, first * C : (first + count) * C],
             )
 
-        for g in range(5):
-            load_group(g)
+        for n in range(XFIRST):
+            load_piece(n)
         gain_bf = setup.tile([P, PACK], BF16)
         shift_bf = setup.tile([P, PACK], BF16)
         nc.scalar.dma_start(out=gain_bf[:], in_=ln1_w.rearrange("(p t) -> p t", t=PACK))
         nc.scalar.dma_start(out=shift_bf[:], in_=ln1_b.rearrange("(p t) -> p t", t=PACK))
+
+        part = setup.tile([P, 1], I32)
+        nc.gpsimd.iota(part[:], pattern=[[0, 1]], base=0, channel_multiplier=1)
+        count_i = setup.tile([P, 2, UNIT], I32)
+        nc.gpsimd.iota(count_i[:], pattern=[[0, 2], [1, UNIT]], base=0, channel_multiplier=0)
         bias_rows = setup.tile([P, 2 * E], BF16)
         nc.gpsimd.memset(bias_rows[:], 0.0)
         nc.scalar.dma_start(out=bias_rows[0:1, 0:E], in_=q_b.rearrange("(a n) -> a n", a=1))
         nc.scalar.dma_start(out=bias_rows[0:1, E : 2 * E], in_=v_b.rearrange("(a n) -> a n", a=1))
+        ident = setup.tile([P, P], F32)
+        make_identity(nc, ident[:])
         ones = setup.tile([P, P], BF16)
         nc.gpsimd.memset(ones[:], 1.0)
         biases = psum_t.tile([P, 2 * E], F32, name="bank3")
@@ -98,47 +121,34 @@ def tile_block_pa_t_kernel(
                     out=w_scales[32 * quadrant : 32 * quadrant + 4, n * E : (n + 1) * E].bitcast(I32),
                     in_=scales[0, 4 * quadrant : 4 * quadrant + 4, :].bitcast(I32),
                 )
-        for g in range(5, len(pieces)):
-            load_group(g)
+        for n in range(XFIRST, len(pieces)):
+            load_piece(n)
 
-        ident = setup.tile([P, P], F32)
-        make_identity(nc, ident[:])
-        order = consts.tile([P, P], F32)
-        nc.vector.tensor_copy(
-            out=order[:].rearrange("p (a j r h) -> p a j r h", a=8, j=4, r=2, h=2),
-            in_=ident[:].rearrange("p (a r j h) -> p a j r h", a=8, r=2, j=4, h=2),
-        )
-
-        part = setup.tile([P, 1], I32)
-        nc.gpsimd.iota(part[:], pattern=[[0, 1]], base=0, channel_multiplier=1)
-        count_i = setup.tile([P, 2, UNIT], I32)
-        nc.gpsimd.iota(count_i[:], pattern=[[0, 2], [1, UNIT]], base=0, channel_multiplier=0)
         one = setup.tile([P, 1], F32)
         nc.vector.memset(one[:], 1.0)
         warm = setup.tile([P, 2], F32)
         nc.scalar.activation(out=warm[:, 0:1], in_=one[:], func=ACT.Sin)
+        freq = setup.tile([P, FREQS], F32)
+        nc.vector.tensor_scalar_mul(out=freq[:, 0:1], in0=one[:], scalar1=STEP)
         bits_i = setup.tile([P, 2], I32)
         nc.vector.tensor_scalar(
             out=bits_i[:, 0:1], in0=part[:], scalar1=1, scalar2=1,
             op0=ALU.logical_shift_right, op1=ALU.bitwise_and,
         )
+        nc.vector.tensor_scalar_mul(out=freq[:, 1:2], in0=freq[:, 0:1], scalar1=THETA ** (-1 / FREQS))
         nc.vector.tensor_single_scalar(out=bits_i[:, 1:2], in_=part[:], scalar=1, op=ALU.bitwise_and)
+        nc.vector.tensor_scalar_mul(out=freq[:, 2:4], in0=freq[:, 0:2], scalar1=THETA ** (-2 / FREQS))
         bits = setup.tile([P, 2], F32)
         nc.vector.tensor_copy(out=bits[:], in_=bits_i[:])
+        nc.vector.tensor_scalar_mul(out=freq[:, 4:8], in0=freq[:, 0:4], scalar1=THETA ** (-4 / FREQS))
         count_f = setup.tile([P, 2, UNIT], F32)
         nc.vector.tensor_copy(out=count_f[:], in_=count_i[:])
+        nc.vector.tensor_scalar_mul(out=freq[:, 8:16], in0=freq[:, 0:8], scalar1=THETA ** (-8 / FREQS))
         place = setup.tile([P, 2, UNIT], F32)
         nc.vector.scalar_tensor_tensor(
             out=place[:], in0=bits[:].unsqueeze(2).to_broadcast([P, 2, UNIT]), scalar=float(UNIT),
             in1=count_f[:], op0=ALU.mult, op1=ALU.add,
         )
-        freq = setup.tile([P, FREQS], F32)
-        nc.vector.tensor_scalar_mul(out=freq[:, 0:1], in0=one[:], scalar1=STEP)
-        for width in (1, 2, 4, 8):
-            nc.vector.tensor_scalar_mul(
-                out=freq[:, width : 2 * width], in0=freq[:, 0:width],
-                scalar1=THETA ** (-width / FREQS),
-            )
         rows = 2 * UNIT
         phase = setup.tile([P, 2, rows, FREQS], F32)
         nc.vector.tensor_tensor(
@@ -148,39 +158,39 @@ def tile_block_pa_t_kernel(
             op=ALU.mult,
         )
         nc.vector.tensor_scalar_add(out=phase[:, 0], in0=phase[:, 1], scalar1=math.pi / 2)
-        turns = setup.tile([P, 2, rows, FREQS], F32)
-        nc.vector.tensor_single_scalar(out=turns[:], in_=phase[:], scalar=math.pi, op=ALU.is_ge)
+        fast = len([m for m in range(FREQS) if (rows - 1) * STEP * THETA ** (-m / FREQS) + math.pi / 2 >= math.pi])
+        turning = phase[:, :, :, 0:fast].rearrange("p a i m -> p (a i) m")
+        turns = setup.tile([P, 2 * rows, fast], F32)
+        nc.vector.tensor_single_scalar(out=turns[:], in_=turning, scalar=math.pi, op=ALU.is_ge)
         for odd in (3, 5):
             nc.vector.scalar_tensor_tensor(
-                out=turns[:].rearrange("p a b c -> p (a b c)"),
-                in0=phase[:].rearrange("p a b c -> p (a b c)"), scalar=odd * math.pi,
-                in1=turns[:].rearrange("p a b c -> p (a b c)"), op0=ALU.is_ge, op1=ALU.add,
+                out=turns[:], in0=turning, scalar=odd * math.pi, in1=turns[:], op0=ALU.is_ge, op1=ALU.add,
             )
-        wrapped = setup.tile([P, 2, rows, FREQS], F32)
         nc.vector.scalar_tensor_tensor(
-            out=wrapped[:].rearrange("p a b c -> p (a b c)"),
-            in0=turns[:].rearrange("p a b c -> p (a b c)"), scalar=-2.0 * math.pi,
-            in1=phase[:].rearrange("p a b c -> p (a b c)"), op0=ALU.mult, op1=ALU.add,
+            out=turning, in0=turns[:], scalar=-2.0 * math.pi, in1=turning, op0=ALU.mult, op1=ALU.add,
         )
         cos_sin = setup.tile([P, 2, rows, FREQS], F32)
-        nc.scalar.activation(out=cos_sin[:], in_=wrapped[:], func=ACT.Sin)
-        nc.scalar.activation(out=warm[:, 1:2], in_=one[:], func=ACT.Sqrt)
+        nc.scalar.activation(out=cos_sin[:], in_=phase[:], func=ACT.Sin)
+        nc.scalar.activation(out=warm[:, 1:2], in_=one[:], func=ACT.Abs_reciprocal_sqrt)
         sign = setup.tile([P, 2], F32)
         nc.vector.memset(sign[:, 0:1], -1.0)
         nc.vector.memset(sign[:, 1:2], 1.0)
-
-        stats, mean_var, sums, minus_mean, squares, deviation, rstd, minus_mean_rstd = (
-            {}, {}, {}, {}, {}, {}, {}, {}
+        order = consts.tile([P, P], F32)
+        nc.vector.tensor_copy(
+            out=order[:].rearrange("p (a j r h) -> p a j r h", a=8, j=4, r=2, h=2),
+            in_=ident[:].rearrange("p (a r j h) -> p a j r h", a=8, r=2, j=4, h=2),
         )
+
+        stats, mean_var, sums, minus_mean, squares, rstd, minus_mean_rstd = {}, {}, {}, {}, {}, {}, {}
         xhat, banks, planes, grouped, codes, code_scales = {}, {}, {}, {}, {}, {}
         qk, v_pair, stage, by_cos = {}, {}, {}, {}
 
         def on_scalar(g):
-            return g in (2, 4, 6, 8, 10, 11)
+            return g in S_STATS
 
         def stats_of_tile(j):
             s, c = divmod(j, UNIT)
-            g, slot = divmod(j, BANK_TILES)
+            g, slot = place_of(j)
             if on_scalar(g):
                 return
             if slot == 0:
@@ -189,14 +199,14 @@ def tile_block_pa_t_kernel(
             nc.vector.bn_stats(out=stats[g][:, slot, :], in_=x_sb[s][:, c, :])
 
         def aggregate(j):
-            g, slot = divmod(j, BANK_TILES)
+            g, slot = place_of(j)
             if on_scalar(g):
                 return
             nc.vector.bn_aggr(out=mean_var[g][:, slot, :], in_=stats[g][:, slot, :])
 
         def sum_of_tile(j):
             s, c = divmod(j, UNIT)
-            g, slot = divmod(j, BANK_TILES)
+            g, slot = place_of(j)
             if not on_scalar(g):
                 return
             if slot == 0:
@@ -212,7 +222,7 @@ def tile_block_pa_t_kernel(
 
         def squares_of_tile(j):
             s, c = divmod(j, UNIT)
-            g, slot = divmod(j, BANK_TILES)
+            g, slot = place_of(j)
             if not on_scalar(g):
                 return
             if slot == 0:
@@ -225,46 +235,43 @@ def tile_block_pa_t_kernel(
 
         def root(g):
             count = len(groups[g])
-            deviation[g] = small.tile([P, BANK_TILES], F32, name="deviation")
+            rstd[g] = small.tile([P, BANK_TILES], F32, name="rstd")
             if on_scalar(g):
                 nc.scalar.activation(
-                    out=deviation[g][:], in_=squares[g][:], func=ACT.Sqrt, scale=1.0 / C, bias=EPS
+                    out=rstd[g][:], in_=squares[g][:], func=ACT.Abs_reciprocal_sqrt, scale=1.0 / C, bias=EPS
                 )
             else:
                 nc.scalar.activation(
-                    out=deviation[g][:, 0:count], in_=mean_var[g][:, 0:count, 1], func=ACT.Sqrt, bias=EPS
+                    out=rstd[g][:, 0:count], in_=mean_var[g][:, 0:count, 1], func=ACT.Abs_reciprocal_sqrt, bias=EPS
+                )
+                minus_mean[g] = small.tile([P, BANK_TILES], F32, name="minus_mean")
+                nc.scalar.activation(
+                    out=minus_mean[g][:, 0:count], in_=mean_var[g][:, 0:count, 0], func=ACT.Identity, scale=-1.0
                 )
 
         def finish_stats(g):
             count = len(groups[g])
-            rstd[g] = small.tile([P, BANK_TILES], F32, name="rstd")
             minus_mean_rstd[g] = small.tile([P, BANK_TILES], F32, name="minus_mean_rstd")
-            nc.vector.reciprocal(out=rstd[g][:, 0:count], in_=deviation[g][:, 0:count])
-            if on_scalar(g):
-                nc.vector.tensor_tensor(
-                    out=minus_mean_rstd[g][:], in0=minus_mean[g][:], in1=rstd[g][:], op=ALU.mult
-                )
-            else:
-                nc.vector.scalar_tensor_tensor(
-                    out=minus_mean_rstd[g][:, 0:count], in0=mean_var[g][:, 0:count, 0], scalar=-1.0,
-                    in1=rstd[g][:, 0:count], op0=ALU.mult, op1=ALU.mult,
-                )
+            nc.gpsimd.tensor_tensor(
+                out=minus_mean_rstd[g][:, 0:count], in0=minus_mean[g][:, 0:count], in1=rstd[g][:, 0:count],
+                op=ALU.mult,
+            )
 
         def normalise(j):
             s, c = divmod(j, UNIT)
-            g, slot = divmod(j, BANK_TILES)
+            g, slot = place_of(j)
             xhat[j] = xhat_pool.tile([P, PACK, P], F32, name="xhat")
             source = x_sb[s][:, c, :].rearrange("p (q t) -> p t q", t=PACK)
-            if j >= 2 * BANK_TILES:
-                nc.scalar.activation(
-                    out=xhat[j][:], in_=source, func=ACT.Identity, scale=rstd[g][:, slot : slot + 1],
-                    bias=minus_mean_rstd[g][:, slot : slot + 1],
-                )
-            else:
-                engine = nc.vector if j % 2 == 0 else nc.gpsimd
+            if j in V_NORM or j in G_NORM:
+                engine = nc.vector if j in V_NORM else nc.gpsimd
                 engine.tensor_scalar(
                     out=xhat[j][:], in0=source, scalar1=rstd[g][:, slot : slot + 1],
                     scalar2=minus_mean_rstd[g][:, slot : slot + 1], op0=ALU.mult, op1=ALU.add,
+                )
+            else:
+                nc.scalar.activation(
+                    out=xhat[j][:], in_=source, func=ACT.Identity, scale=rstd[g][:, slot : slot + 1],
+                    bias=minus_mean_rstd[g][:, slot : slot + 1],
                 )
 
         def transpose(g, t):
@@ -276,19 +283,26 @@ def tile_block_pa_t_kernel(
             cols = len(groups[g]) * P
             if t == 0:
                 planes[g] = quant.tile([P, PACK, BANK_TILES * P], BF16, name="planes")
-            nc.scalar.activation(
-                out=planes[g][:, t, 0:cols], in_=banks[g, t][:, 0:cols], func=ACT.Identity,
-                scale=gain[:, t : t + 1], bias=shift[:, t : t + 1],
-            )
+            if (g, t) in V_AFF:
+                nc.vector.tensor_scalar(
+                    out=planes[g][:, t, 0:cols], in0=banks[g, t][:, 0:cols], scalar1=gain[:, t : t + 1],
+                    scalar2=shift[:, t : t + 1], op0=ALU.mult, op1=ALU.add,
+                )
+            else:
+                nc.scalar.activation(
+                    out=planes[g][:, t, 0:cols], in_=banks[g, t][:, 0:cols], func=ACT.Identity,
+                    scale=gain[:, t : t + 1], bias=shift[:, t : t + 1],
+                )
 
         def interleave(g):
             cols = len(groups[g]) * P
             grouped[g] = quant.tile([P, BANK_TILES * P, PACK], BF16, name="grouped", align_bytes=64)
-            source = planes[g][:, :, 0:cols].rearrange("p t j -> p j t")
-            if g % 3 == 0:
-                nc.vector.tensor_copy(out=grouped[g][:, 0:cols, :], in_=source)
+            source = planes[g][:, :, 0:cols].rearrange("p t (j i) -> p j t i", i=4)
+            target = grouped[g][:, 0:cols, :].rearrange("p (j i) t -> p j t i", i=4)
+            if g in V_INTER:
+                nc.vector.tensor_copy(out=target, in_=source)
             else:
-                nc.scalar.copy(out=grouped[g][:, 0:cols, :], in_=source)
+                nc.scalar.copy(out=target, in_=source)
 
         def quantise(g):
             cols = len(groups[g]) * P
@@ -301,7 +315,7 @@ def tile_block_pa_t_kernel(
 
         def project(j):
             s, c = divmod(j, UNIT)
-            g, slot = divmod(j, BANK_TILES)
+            g, slot = place_of(j)
             tokens = slice(slot * P, (slot + 1) * P)
             qk[j] = psum_qk.tile([P, 2 * E], F32, name="qk")
             nc.tensor.matmul_mx(
@@ -334,15 +348,16 @@ def tile_block_pa_t_kernel(
                 op=ALU.mult,
             )
 
+        def add_bias(j):
+            nc.gpsimd.tensor_tensor(
+                out=by_cos[j][:, 0:E].rearrange("p (h g d) -> p h g d", h=HEADS, g=2),
+                in0=by_cos[j][:, 0:E].rearrange("p (h g d) -> p h g d", h=HEADS, g=2),
+                in1=bias_tab[:, tables_of(j)].rearrange("p g h d -> p h g d"),
+                op=ALU.add,
+            )
+
         def times_sin(j):
             s, c = divmod(j, UNIT)
-            if s == UNIT - 1:
-                nc.vector.tensor_tensor(
-                    out=by_cos[j][:, 0:E].rearrange("p (h g d) -> p h g d", h=HEADS, g=2),
-                    in0=by_cos[j][:, 0:E].rearrange("p (h g d) -> p h g d", h=HEADS, g=2),
-                    in1=bias_tab[:, tables_of(j)].rearrange("p g h d -> p h g d"),
-                    op=ALU.add,
-                )
             by_sin = rope.tile([P, 2 * E], F32, name="by_sin")
             nc.vector.tensor_tensor(
                 out=by_sin[:].rearrange("p (a g m e) -> p a g m e", g=2, m=FREQS, e=2),
@@ -356,15 +371,6 @@ def tile_block_pa_t_kernel(
                 in1=by_sin[:].rearrange("p (a d) -> p a d", d=DH),
                 op=ALU.add,
             )
-
-        def bias_q(s):
-            shape = [P, HEADS, UNIT, HALF]
-            for half, table in (
-                (0, bias_tab[:, s].unsqueeze(2).to_broadcast(shape)),
-                (1, bias_tab[:, UNIT : 2 * UNIT].rearrange("p c h d -> p h c d")),
-            ):
-                q_half = stage[s][:, 0:HEADS, :, half * HALF : (half + 1) * HALF]
-                nc.gpsimd.tensor_tensor(out=q_half, in0=q_half, in1=table, op=ALU.add)
 
         def bias_v(j):
             s, c = divmod(j, UNIT)
@@ -380,23 +386,23 @@ def tile_block_pa_t_kernel(
             )
 
         out_views = [
-            o.rearrange("w h (r s f c) d -> s h w r f (c d)", r=2, s=UNIT, f=2, c=UNIT)
+            o.rearrange("w h (r s f c) d -> s r f w h (c d)", r=2, s=UNIT, f=2, c=UNIT)
             for o in (out_0, out_1, out_2)
         ]
 
         def store(s, first, count):
-            for a in list(range(2 * HEADS, 3 * HEADS)) + list(range(2 * HEADS)):
-                for f in range(2):
+            for n in (2, 0, 1):
+                for rf in range(4):
                     nc.sync.dma_start(
-                        out=out_views[a // HEADS][s, a % HEADS, :, :, f, first * DH : (first + count) * DH],
-                        in_=stage[s][f:P:2, a, first : first + count].rearrange("p c d -> p (c d)"),
+                        out=out_views[n][s, rf // 2, rf % 2, :, :, first * DH : (first + count) * DH],
+                        in_=stage[s][rf:P:4, n * HEADS : (n + 1) * HEADS, first : first + count].rearrange(
+                            "p h c d -> p h (c d)"
+                        ),
                     )
 
-        stores = {}
-        for s in range(UNIT - 1):
-            last = UNIT * s + UNIT - 1
-            stores[last + (1 - last) % BANK_TILES] = (s, 0, UNIT)
-        stores[TILES - 1] = (UNIT - 1, 0, UNIT)
+        stores = {UNIT * s + UNIT - 1: (s, 0, UNIT) for s in range(UNIT - 1)}
+        stores[TILES - 4] = (UNIT - 1, 0, 4)
+        stores[TILES - 1] = (UNIT - 1, 4, 3)
 
         gain = consts.tile([P, PACK], F32)
         shift = consts.tile([P, PACK], F32)
@@ -413,6 +419,12 @@ def tile_block_pa_t_kernel(
 
         def vector_tables():
             pairs = rows * FREQS
+            nc.vector.tensor_copy(out=q_bias[:], in_=biases[:, 0:E])
+            nc.vector.tensor_copy(
+                out=q_bias_swapped[:].rearrange("p (m e) -> p m e", e=2),
+                in_=biases[:, 0:E].rearrange("p (m e) -> p m e", e=2)[:, :, ::-1],
+            )
+            nc.vector.tensor_copy(out=v_bias[:], in_=biases[:, E : 2 * E])
             nc.vector.tensor_copy(
                 out=cos_tab[:].rearrange("p i m e -> p (i m) e"),
                 in_=cos_sin[:, 0].rearrange("p i m -> p (i m)").unsqueeze(2).to_broadcast([P, pairs, 2]),
@@ -423,12 +435,6 @@ def tile_block_pa_t_kernel(
                 in1=sign[:].unsqueeze(1).to_broadcast([P, pairs, 2]),
                 op=ALU.mult,
             )
-            nc.vector.tensor_copy(out=q_bias[:], in_=biases[:, 0:E])
-            nc.vector.tensor_copy(
-                out=q_bias_swapped[:].rearrange("p (m e) -> p m e", e=2),
-                in_=biases[:, 0:E].rearrange("p (m e) -> p m e", e=2)[:, :, ::-1],
-            )
-            nc.vector.tensor_copy(out=v_bias[:], in_=biases[:, E : 2 * E])
 
         def bias_product(half, product, bias, table):
             half_rows = slice(half * UNIT, (half + 1) * UNIT)
@@ -448,49 +454,52 @@ def tile_block_pa_t_kernel(
                 out=bias_tab[:, half_rows], in0=bias_cos[:, half_rows], in1=bias_sin[:, half_rows], op=ALU.add
             )
 
-        tables = {-12: vector_tables, 7: lambda: bias_sum(0), 8: lambda: bias_sum(1)}
+        tables = {TABLES_AT: vector_tables, SUM0_AT: lambda: bias_sum(0), SUM1_AT: lambda: bias_sum(1)}
         products = {
-            1: ((0, bias_cos, q_bias, cos_tab), (0, bias_sin, q_bias_swapped, sin_tab)),
-            5: ((1, bias_cos, q_bias, cos_tab), (1, bias_sin, q_bias_swapped, sin_tab)),
+            PROD0_AT: ((0, bias_cos, q_bias, cos_tab), (0, bias_sin, q_bias_swapped, sin_tab)),
+            PROD1_AT: ((1, bias_cos, q_bias, cos_tab), (1, bias_sin, q_bias_swapped, sin_tab)),
         }
 
-        SUMS, MEAN, SQUARES, STATS, AGGREGATE, ROOT, FINISH = 26, 22, 21, 22, 21, 17, 16
-        NORMALISE, TRANSPOSE, AFFINE, INTERLEAVE, QUANTISE, PROJECT = 14, 10, 9, 5, 3, 2
-
         def group_due(step, distance):
-            g, slot = divmod(step + distance, BANK_TILES)
+            g, slot = divmod(step + distance + lead, BANK_TILES)
             return g if slot == 0 and 0 <= g < len(groups) else None
 
-        for step in range(-SUMS, TILES):
-            g, t = divmod(step + TRANSPOSE, BANK_TILES)
-            if 0 <= g < len(groups):
-                transpose(g, t)
+        def quarter_due(step, distance):
+            g, t = divmod(step + distance + lead, BANK_TILES)
+            return (g, t) if 0 <= g < len(groups) else None
+
+        for step in range(-SUMS - lead, TILES):
+            due = quarter_due(step, TRANSPOSE)
+            if due:
+                transpose(*due)
             if step >= 0:
                 times_cos(step)
+                if G_BIAS_STEP:
+                    add_bias(step)
                 bias_v(step)
-            if 0 <= step + NORMALISE < TILES:
-                normalise(step + NORMALISE)
             if 0 <= step + STATS < TILES:
                 stats_of_tile(step + STATS)
             if 0 <= step + AGGREGATE < TILES:
                 aggregate(step + AGGREGATE)
-            g = group_due(step, QUANTISE)
-            if g is not None:
-                quantise(g)
-            g = group_due(step, FINISH)
-            if g is not None:
-                finish_stats(g)
-            if step in tables:
-                tables[step]()
             g = group_due(step, ROOT)
             if g is not None:
                 root(g)
-            g, t = divmod(step + AFFINE, BANK_TILES)
-            if 0 <= g < len(groups):
-                affine(g, t)
+            g = group_due(step, FINISH)
+            if g is not None:
+                finish_stats(g)
+            if 0 <= step + NORMALISE < TILES:
+                normalise(step + NORMALISE)
+            due = quarter_due(step, AFFINE)
+            if due:
+                affine(*due)
             g = group_due(step, INTERLEAVE)
             if g is not None:
                 interleave(g)
+            g = group_due(step, QUANTISE)
+            if g is not None and not Q_AFTER:
+                quantise(g)
+            if step in tables:
+                tables[step]()
             if 0 <= step + SUMS < TILES:
                 sum_of_tile(step + SUMS)
             g = group_due(step, MEAN)
@@ -500,11 +509,12 @@ def tile_block_pa_t_kernel(
                 squares_of_tile(step + SQUARES)
             if step >= 0:
                 times_sin(step)
-            if 0 <= step + PROJECT < TILES:
-                project(step + PROJECT)
+            g = group_due(step, QUANTISE)
+            if g is not None and Q_AFTER:
+                quantise(g)
             for arguments in products.get(step, ()):
                 bias_product(*arguments)
+            if 0 <= step + PROJECT < TILES:
+                project(step + PROJECT)
             if step in stores:
-                if stores[step][0] < UNIT - 1:
-                    bias_q(stores[step][0])
                 store(*stores[step])

@@ -30,17 +30,15 @@ STEP = 16.0 / 14.0
 
 FLOPS = 2 * 2 * 56 * 56 * C * 3 * E
 
-SUMS, MEAN, SQUARES, STATS, AGGREGATE, ROOT, FINISH = 25, 21, 20, 21, 20, 16, 15
-NORMALISE, TRANSPOSE, AFFINE, INTERLEAVE, QUANTISE, PROJECT = 14, 10, 9, 5, 3, 2
-S_STATS = (3, 6, 9)
+SUMS, SQUARES, STATS, AGGREGATE, ROOT, FINISH = 22, 21, 20, 19, 15, 14
+NORMALISE, TRANSPOSE, AFFINE, INTERLEAVE, QUANTISE, PROJECT = 13, 9, 8, 4, 2, 1
+S_FROM, S_TO = 3, 12
 V_INTER = (0, 1)
-V_AFF = ((0, 1), (0, 3), (1, 1), (1, 3))
-V_NORM = (0, 1, 3)
-G_NORM = (2, 4, 5, 6, 7, 8)
-Q_AFTER = False
-G_BIAS_STEP = True
-TABLES_AT, SUM0_AT, SUM1_AT = -14, -4, -3
-PROD0_AT, PROD1_AT = -6, -5
+V_AFF = ((1, 1), (1, 3))
+V_NORM = ()
+G_NORM = ()
+TABLES_AT, SUM0_AT, SUM1_AT = -14, -1, 0
+PROD = (-13, -12, -11, -10)
 XFIRST = 4
 
 
@@ -73,6 +71,16 @@ def tile_block_pa_t_kernel(
         psum_v = ctx.enter_context(tc.psum_pool(name="psum_v", bufs=2))
         ctx.enter_context(tc.manual_schedule())
 
+        bias_rows = setup.tile([P, 2 * E], BF16)
+        nc.vector.memset(bias_rows[:], 0.0)
+        ones = setup.tile([P, P], BF16)
+        nc.gpsimd.memset(ones[:], 1.0)
+        nc.scalar.dma_start(out=bias_rows[0:1, 0:E], in_=q_b.rearrange("(a n) -> a n", a=1))
+        nc.scalar.dma_start(out=bias_rows[0:1, E : 2 * E], in_=v_b.rearrange("(a n) -> a n", a=1))
+        gain_bf = setup.tile([P, PACK], BF16)
+        shift_bf = setup.tile([P, PACK], BF16)
+        nc.scalar.dma_start(out=gain_bf[:], in_=ln1_w.rearrange("(p t) -> p t", t=PACK))
+        nc.scalar.dma_start(out=shift_bf[:], in_=ln1_b.rearrange("(p t) -> p t", t=PACK))
         x_rounds = x.rearrange(
             "b (i r s) (u c) k -> s (b i r) u (c k)", i=4, r=2, s=UNIT, u=8, c=UNIT
         )
@@ -87,23 +95,13 @@ def tile_block_pa_t_kernel(
 
         for n in range(XFIRST):
             load_piece(n)
-        gain_bf = setup.tile([P, PACK], BF16)
-        shift_bf = setup.tile([P, PACK], BF16)
-        nc.scalar.dma_start(out=gain_bf[:], in_=ln1_w.rearrange("(p t) -> p t", t=PACK))
-        nc.scalar.dma_start(out=shift_bf[:], in_=ln1_b.rearrange("(p t) -> p t", t=PACK))
 
         part = setup.tile([P, 1], I32)
         nc.gpsimd.iota(part[:], pattern=[[0, 1]], base=0, channel_multiplier=1)
         count_i = setup.tile([P, 2, UNIT], I32)
         nc.gpsimd.iota(count_i[:], pattern=[[0, 2], [1, UNIT]], base=0, channel_multiplier=0)
-        bias_rows = setup.tile([P, 2 * E], BF16)
-        nc.gpsimd.memset(bias_rows[:], 0.0)
-        nc.scalar.dma_start(out=bias_rows[0:1, 0:E], in_=q_b.rearrange("(a n) -> a n", a=1))
-        nc.scalar.dma_start(out=bias_rows[0:1, E : 2 * E], in_=v_b.rearrange("(a n) -> a n", a=1))
         ident = setup.tile([P, P], F32)
         make_identity(nc, ident[:])
-        ones = setup.tile([P, P], BF16)
-        nc.gpsimd.memset(ones[:], 1.0)
         biases = psum_t.tile([P, 2 * E], F32, name="bank3")
         nc.tensor.matmul(out=biases[:], lhsT=ones[:], rhs=bias_rows[:], start=True, stop=True)
 
@@ -128,27 +126,22 @@ def tile_block_pa_t_kernel(
         nc.vector.memset(one[:], 1.0)
         warm = setup.tile([P, 2], F32)
         nc.scalar.activation(out=warm[:, 0:1], in_=one[:], func=ACT.Sin)
-        freq = setup.tile([P, FREQS], F32)
-        nc.vector.tensor_scalar_mul(out=freq[:, 0:1], in0=one[:], scalar1=STEP)
         bits_i = setup.tile([P, 2], I32)
         nc.vector.tensor_scalar(
             out=bits_i[:, 0:1], in0=part[:], scalar1=1, scalar2=1,
             op0=ALU.logical_shift_right, op1=ALU.bitwise_and,
         )
-        nc.vector.tensor_scalar_mul(out=freq[:, 1:2], in0=freq[:, 0:1], scalar1=THETA ** (-1 / FREQS))
         nc.vector.tensor_single_scalar(out=bits_i[:, 1:2], in_=part[:], scalar=1, op=ALU.bitwise_and)
-        nc.vector.tensor_scalar_mul(out=freq[:, 2:4], in0=freq[:, 0:2], scalar1=THETA ** (-2 / FREQS))
-        bits = setup.tile([P, 2], F32)
-        nc.vector.tensor_copy(out=bits[:], in_=bits_i[:])
-        nc.vector.tensor_scalar_mul(out=freq[:, 4:8], in0=freq[:, 0:4], scalar1=THETA ** (-4 / FREQS))
-        count_f = setup.tile([P, 2, UNIT], F32)
-        nc.vector.tensor_copy(out=count_f[:], in_=count_i[:])
-        nc.vector.tensor_scalar_mul(out=freq[:, 8:16], in0=freq[:, 0:8], scalar1=THETA ** (-8 / FREQS))
+        freq = setup.tile([P, FREQS], F32)
+        for m in range(4):
+            nc.vector.tensor_scalar_mul(out=freq[:, m : m + 1], in0=one[:], scalar1=STEP * THETA ** (-m / FREQS))
         place = setup.tile([P, 2, UNIT], F32)
         nc.vector.scalar_tensor_tensor(
-            out=place[:], in0=bits[:].unsqueeze(2).to_broadcast([P, 2, UNIT]), scalar=float(UNIT),
-            in1=count_f[:], op0=ALU.mult, op1=ALU.add,
+            out=place[:], in0=bits_i[:].unsqueeze(2).to_broadcast([P, 2, UNIT]), scalar=float(UNIT),
+            in1=count_i[:], op0=ALU.mult, op1=ALU.add,
         )
+        for m in range(4, FREQS, 4):
+            nc.vector.tensor_scalar_mul(out=freq[:, m : m + 4], in0=freq[:, 0:4], scalar1=THETA ** (-m / FREQS))
         rows = 2 * UNIT
         phase = setup.tile([P, 2, rows, FREQS], F32)
         nc.vector.tensor_tensor(
@@ -181,17 +174,18 @@ def tile_block_pa_t_kernel(
             in_=ident[:].rearrange("p (a r j h) -> p a j r h", a=8, r=2, j=4, h=2),
         )
 
-        stats, mean_var, sums, minus_mean, squares, rstd, minus_mean_rstd = {}, {}, {}, {}, {}, {}, {}
+        stats, mean_var, minus_mean, squares, rstd, minus_mean_rstd = {}, {}, {}, {}, {}, {}
         xhat, banks, planes, grouped, codes, code_scales = {}, {}, {}, {}, {}, {}
         qk, v_pair, stage, by_cos = {}, {}, {}, {}
 
-        def on_scalar(g):
-            return g in S_STATS
+        def on_scalar(j):
+            g, slot = place_of(j)
+            return S_FROM <= g <= S_TO and slot == BANK_TILES - 1
 
         def stats_of_tile(j):
             s, c = divmod(j, UNIT)
             g, slot = place_of(j)
-            if on_scalar(g):
+            if on_scalar(j):
                 return
             if slot == 0:
                 stats[g] = small.tile([P, BANK_TILES, 6], F32, name="stats")
@@ -200,62 +194,59 @@ def tile_block_pa_t_kernel(
 
         def aggregate(j):
             g, slot = place_of(j)
-            if on_scalar(g):
+            if on_scalar(j):
                 return
             nc.vector.bn_aggr(out=mean_var[g][:, slot, :], in_=stats[g][:, slot, :])
 
         def sum_of_tile(j):
             s, c = divmod(j, UNIT)
             g, slot = place_of(j)
-            if not on_scalar(g):
+            if not on_scalar(j):
                 return
-            if slot == 0:
-                sums[g] = small.tile([P, BANK_TILES], F32, name="sums")
+            minus_mean[g] = small.tile([P, BANK_TILES], F32, name="minus_mean")
             unread = scratch.tile([P, C], BF16, name="unread")
             nc.scalar.activation(
-                out=unread[:], in_=x_sb[s][:, c, :], func=ACT.Identity, accum_out=sums[g][:, slot : slot + 1]
+                out=unread[:], in_=x_sb[s][:, c, :], func=ACT.Identity, scale=-1.0 / C,
+                accum_out=minus_mean[g][:, slot : slot + 1],
             )
-
-        def mean_of_group(g):
-            minus_mean[g] = small.tile([P, BANK_TILES], F32, name="minus_mean")
-            nc.scalar.activation(out=minus_mean[g][:], in_=sums[g][:], func=ACT.Identity, scale=-1.0 / C)
 
         def squares_of_tile(j):
             s, c = divmod(j, UNIT)
             g, slot = place_of(j)
-            if not on_scalar(g):
+            if not on_scalar(j):
                 return
-            if slot == 0:
-                squares[g] = small.tile([P, BANK_TILES], F32, name="squares")
+            squares[g] = small.tile([P, 1], F32, name="squares")
             unread = scratch.tile([P, C], BF16, name="unread")
             nc.scalar.activation(
                 out=unread[:], in_=x_sb[s][:, c, :], func=ACT.Square, bias=minus_mean[g][:, slot : slot + 1],
-                accum_out=squares[g][:, slot : slot + 1],
+                accum_out=squares[g][:],
             )
 
         def root(g):
-            count = len(groups[g])
             rstd[g] = small.tile([P, BANK_TILES], F32, name="rstd")
-            if on_scalar(g):
+            count = len(groups[g])
+            if on_scalar(groups[g][-1]):
+                count -= 1
                 nc.scalar.activation(
-                    out=rstd[g][:], in_=squares[g][:], func=ACT.Abs_reciprocal_sqrt, scale=1.0 / C, bias=EPS
+                    out=rstd[g][:, count : count + 1], in_=squares[g][:], func=ACT.Abs_reciprocal_sqrt,
+                    scale=1.0 / C, bias=EPS,
                 )
             else:
-                nc.scalar.activation(
-                    out=rstd[g][:, 0:count], in_=mean_var[g][:, 0:count, 1], func=ACT.Abs_reciprocal_sqrt, bias=EPS
-                )
                 minus_mean[g] = small.tile([P, BANK_TILES], F32, name="minus_mean")
-                nc.scalar.activation(
-                    out=minus_mean[g][:, 0:count], in_=mean_var[g][:, 0:count, 0], func=ACT.Identity, scale=-1.0
-                )
+            nc.scalar.activation(
+                out=rstd[g][:, 0:count], in_=mean_var[g][:, 0:count, 1], func=ACT.Abs_reciprocal_sqrt, bias=EPS
+            )
+            nc.scalar.activation(
+                out=minus_mean[g][:, 0:count], in_=mean_var[g][:, 0:count, 0], func=ACT.Identity, scale=-1.0
+            )
 
         def finish_stats(g):
-            count = len(groups[g])
             minus_mean_rstd[g] = small.tile([P, BANK_TILES], F32, name="minus_mean_rstd")
-            nc.gpsimd.tensor_tensor(
-                out=minus_mean_rstd[g][:, 0:count], in0=minus_mean[g][:, 0:count], in1=rstd[g][:, 0:count],
-                op=ALU.mult,
-            )
+            for slot in range(len(groups[g])):
+                nc.scalar.activation(
+                    out=minus_mean_rstd[g][:, slot : slot + 1], in_=minus_mean[g][:, slot : slot + 1],
+                    func=ACT.Identity, scale=rstd[g][:, slot : slot + 1],
+                )
 
         def normalise(j):
             s, c = divmod(j, UNIT)
@@ -294,11 +285,15 @@ def tile_block_pa_t_kernel(
                     scale=gain[:, t : t + 1], bias=shift[:, t : t + 1],
                 )
 
-        def interleave(g):
-            cols = len(groups[g]) * P
-            grouped[g] = quant.tile([P, BANK_TILES * P, PACK], BF16, name="grouped", align_bytes=64)
-            source = planes[g][:, :, 0:cols].rearrange("p t (j i) -> p j t i", i=4)
-            target = grouped[g][:, 0:cols, :].rearrange("p (j i) t -> p j t i", i=4)
+        def interleave(g, half):
+            tiles = BANK_TILES // 2
+            cols = slice(half * tiles * P, min((half + 1) * tiles, len(groups[g])) * P)
+            if cols.stop <= cols.start:
+                return
+            if half == 0:
+                grouped[g] = quant.tile([P, BANK_TILES * P, PACK], BF16, name="grouped", align_bytes=64)
+            source = planes[g][:, :, cols].rearrange("p t (j i) -> p j t i", i=4)
+            target = grouped[g][:, cols, :].rearrange("p (j i) t -> p j t i", i=4)
             if g in V_INTER:
                 nc.vector.tensor_copy(out=target, in_=source)
             else:
@@ -406,8 +401,6 @@ def tile_block_pa_t_kernel(
 
         gain = consts.tile([P, PACK], F32)
         shift = consts.tile([P, PACK], F32)
-        nc.vector.tensor_copy(out=gain[:], in_=gain_bf[:])
-        nc.vector.tensor_copy(out=shift[:], in_=shift_bf[:])
         cos_tab = consts.tile([P, rows, FREQS, 2], F32)
         sin_tab = consts.tile([P, rows, FREQS, 2], F32)
         q_bias = setup.tile([P, E], F32)
@@ -419,6 +412,8 @@ def tile_block_pa_t_kernel(
 
         def vector_tables():
             pairs = rows * FREQS
+            nc.vector.tensor_copy(out=gain[:], in_=gain_bf[:])
+            nc.vector.tensor_copy(out=shift[:], in_=shift_bf[:])
             nc.vector.tensor_copy(out=q_bias[:], in_=biases[:, 0:E])
             nc.vector.tensor_copy(
                 out=q_bias_swapped[:].rearrange("p (m e) -> p m e", e=2),
@@ -456,8 +451,10 @@ def tile_block_pa_t_kernel(
 
         tables = {TABLES_AT: vector_tables, SUM0_AT: lambda: bias_sum(0), SUM1_AT: lambda: bias_sum(1)}
         products = {
-            PROD0_AT: ((0, bias_cos, q_bias, cos_tab), (0, bias_sin, q_bias_swapped, sin_tab)),
-            PROD1_AT: ((1, bias_cos, q_bias, cos_tab), (1, bias_sin, q_bias_swapped, sin_tab)),
+            PROD[0]: ((0, bias_cos, q_bias, cos_tab),),
+            PROD[1]: ((0, bias_sin, q_bias_swapped, sin_tab),),
+            PROD[2]: ((1, bias_cos, q_bias, cos_tab),),
+            PROD[3]: ((1, bias_sin, q_bias_swapped, sin_tab),),
         }
 
         def group_due(step, distance):
@@ -474,8 +471,6 @@ def tile_block_pa_t_kernel(
                 transpose(*due)
             if step >= 0:
                 times_cos(step)
-                if G_BIAS_STEP:
-                    add_bias(step)
                 bias_v(step)
             if 0 <= step + STATS < TILES:
                 stats_of_tile(step + STATS)
@@ -492,26 +487,23 @@ def tile_block_pa_t_kernel(
             due = quarter_due(step, AFFINE)
             if due:
                 affine(*due)
-            g = group_due(step, INTERLEAVE)
-            if g is not None:
-                interleave(g)
+            for half in range(2):
+                g = group_due(step, INTERLEAVE - half)
+                if g is not None:
+                    interleave(g, half)
             g = group_due(step, QUANTISE)
-            if g is not None and not Q_AFTER:
+            if g is not None:
                 quantise(g)
             if step in tables:
                 tables[step]()
+            if step >= 0:
+                add_bias(step)
             if 0 <= step + SUMS < TILES:
                 sum_of_tile(step + SUMS)
-            g = group_due(step, MEAN)
-            if g is not None and on_scalar(g):
-                mean_of_group(g)
             if 0 <= step + SQUARES < TILES:
                 squares_of_tile(step + SQUARES)
             if step >= 0:
                 times_sin(step)
-            g = group_due(step, QUANTISE)
-            if g is not None and Q_AFTER:
-                quantise(g)
             for arguments in products.get(step, ()):
                 bias_product(*arguments)
             if 0 <= step + PROJECT < TILES:

@@ -30,15 +30,16 @@ STEP = 16.0 / 14.0
 
 FLOPS = 2 * 2 * 56 * 56 * C * 3 * E
 
-SUMS, SQUARES, STATS, AGGREGATE, ROOT, FINISH = 22, 21, 20, 19, 15, 14
-NORMALISE, TRANSPOSE, AFFINE, INTERLEAVE, QUANTISE, PROJECT = 13, 9, 8, 4, 2, 1
-S_FROM, S_TO = 3, 12
-V_INTER = (0, 1)
-V_AFF = ((1, 1), (1, 3))
+SUMS, SQUARES, STATS, AGGREGATE, ROOT, FINISH = 24, 20, 20, 19, 15, 14
+NORMALISE, TRANSPOSE, AFFINE, INTERLEAVE, QUANTISE, PROJECT = 14, 10, 8, 4, 2, 1
+S_FROM, S_TO = 4, 12
+S_SLOT = 3
+V_INTER = (1,)
+V_AFF = ((0, 2), (0, 3), (1, 2), (1, 3))
 V_NORM = ()
-G_NORM = ()
-TABLES_AT, SUM0_AT, SUM1_AT = -14, -1, 0
-PROD = (-13, -12, -11, -10)
+G_NORM = (6, 8, 10, 12, 14)
+TABLES_AT, SUM0_AT, SUM1_AT = -15, -8, 0
+PROD = (-12, -11, -7, -6)
 XFIRST = 4
 
 
@@ -64,7 +65,7 @@ def tile_block_pa_t_kernel(
         scratch = ctx.enter_context(tc.tile_pool(name="scratch", bufs=2))
         xhat_pool = ctx.enter_context(tc.tile_pool(name="xhat", bufs=3 * BANK_TILES))
         quant = ctx.enter_context(tc.tile_pool(name="quant", bufs=3))
-        rope = ctx.enter_context(tc.tile_pool(name="rope", bufs=4))
+        rope = ctx.enter_context(tc.tile_pool(name="rope", bufs=3))
         stage_pool = ctx.enter_context(tc.tile_pool(name="stage", bufs=3))
         psum_t = ctx.enter_context(tc.psum_pool(name="psum_t", bufs=1))
         psum_qk = ctx.enter_context(tc.psum_pool(name="psum_qk", bufs=2))
@@ -176,11 +177,11 @@ def tile_block_pa_t_kernel(
 
         stats, mean_var, minus_mean, squares, rstd, minus_mean_rstd = {}, {}, {}, {}, {}, {}
         xhat, banks, planes, grouped, codes, code_scales = {}, {}, {}, {}, {}, {}
-        qk, v_pair, stage, by_cos = {}, {}, {}, {}
+        qk, v_pair, stage, by_cos, by_sin = {}, {}, {}, {}, {}
 
         def on_scalar(j):
             g, slot = place_of(j)
-            return S_FROM <= g <= S_TO and slot == BANK_TILES - 1
+            return S_FROM <= g <= S_TO and slot >= S_SLOT
 
         def stats_of_tile(j):
             s, c = divmod(j, UNIT)
@@ -203,7 +204,8 @@ def tile_block_pa_t_kernel(
             g, slot = place_of(j)
             if not on_scalar(j):
                 return
-            minus_mean[g] = small.tile([P, BANK_TILES], F32, name="minus_mean")
+            if g not in minus_mean:
+                minus_mean[g] = small.tile([P, BANK_TILES], F32, name="minus_mean")
             unread = scratch.tile([P, C], BF16, name="unread")
             nc.scalar.activation(
                 out=unread[:], in_=x_sb[s][:, c, :], func=ACT.Identity, scale=-1.0 / C,
@@ -215,20 +217,20 @@ def tile_block_pa_t_kernel(
             g, slot = place_of(j)
             if not on_scalar(j):
                 return
-            squares[g] = small.tile([P, 1], F32, name="squares")
+            if g not in squares:
+                squares[g] = small.tile([P, BANK_TILES], F32, name="squares")
             unread = scratch.tile([P, C], BF16, name="unread")
             nc.scalar.activation(
                 out=unread[:], in_=x_sb[s][:, c, :], func=ACT.Square, bias=minus_mean[g][:, slot : slot + 1],
-                accum_out=squares[g][:],
+                accum_out=squares[g][:, slot : slot + 1],
             )
 
         def root(g):
             rstd[g] = small.tile([P, BANK_TILES], F32, name="rstd")
-            count = len(groups[g])
-            if on_scalar(groups[g][-1]):
-                count -= 1
+            count = len([j for j in groups[g] if not on_scalar(j)])
+            if count < len(groups[g]):
                 nc.scalar.activation(
-                    out=rstd[g][:, count : count + 1], in_=squares[g][:], func=ACT.Abs_reciprocal_sqrt,
+                    out=rstd[g][:, count:], in_=squares[g][:, count:], func=ACT.Abs_reciprocal_sqrt,
                     scale=1.0 / C, bias=EPS,
                 )
             else:
@@ -331,41 +333,55 @@ def tile_block_pa_t_kernel(
             s, c = divmod(j, UNIT)
             return slice(s, UNIT + c + 1, UNIT + c - s)
 
-        def times_cos(j):
+        def in_pair(j):
             s, c = divmod(j, UNIT)
-            if c == 0:
+            if s == UNIT - 1:
+                return s, c, 1, 0
+            return s, c - c % 2, min(2, UNIT - c + c % 2), c % 2
+
+        def times_cos(j):
+            s, first, count, half = in_pair(j)
+            if j % UNIT == 0:
                 stage[s] = stage_pool.tile([P, 3 * HEADS, UNIT, DH], F32, name="stage")
-            by_cos[j] = rope.tile([P, 2 * E], F32, name="by_cos")
+            if half == 0:
+                by_cos[s, first] = rope.tile([P, 2, 2 * E], F32, name="by_cos")
+                by_sin[s, first] = rope.tile([P, 2, 2 * E], F32, name="by_sin")
             nc.vector.tensor_tensor(
-                out=by_cos[j][:].rearrange("p (a g m e) -> p a g m e", g=2, m=FREQS, e=2),
+                out=by_cos[s, first][:, half].rearrange("p (a g m e) -> p a g m e", g=2, m=FREQS, e=2),
                 in0=qk[j][:].rearrange("p (a g m e) -> p a g m e", g=2, m=FREQS, e=2),
                 in1=cos_tab[:, tables_of(j)].unsqueeze(1).to_broadcast([P, 2 * HEADS, 2, FREQS, 2]),
                 op=ALU.mult,
             )
 
-        def add_bias(j):
-            nc.gpsimd.tensor_tensor(
-                out=by_cos[j][:, 0:E].rearrange("p (h g d) -> p h g d", h=HEADS, g=2),
-                in0=by_cos[j][:, 0:E].rearrange("p (h g d) -> p h g d", h=HEADS, g=2),
-                in1=bias_tab[:, tables_of(j)].rearrange("p g h d -> p h g d"),
-                op=ALU.add,
-            )
-
         def times_sin(j):
-            s, c = divmod(j, UNIT)
-            by_sin = rope.tile([P, 2 * E], F32, name="by_sin")
+            s, first, count, half = in_pair(j)
+            if s == UNIT - 1:
+                u_cos = by_cos[s, first][:, half, 0:E].rearrange("p (h g d) -> p h g d", h=HEADS, g=2)
+                nc.vector.tensor_tensor(
+                    out=u_cos, in0=u_cos, in1=bias_tab[:, tables_of(j)].rearrange("p g h d -> p h g d"), op=ALU.add,
+                )
             nc.vector.tensor_tensor(
-                out=by_sin[:].rearrange("p (a g m e) -> p a g m e", g=2, m=FREQS, e=2),
+                out=by_sin[s, first][:, half].rearrange("p (a g m e) -> p a g m e", g=2, m=FREQS, e=2),
                 in0=qk[j][:].rearrange("p (a g m e) -> p a g m e", g=2, m=FREQS, e=2)[:, :, :, :, ::-1],
                 in1=sin_tab[:, tables_of(j)].unsqueeze(1).to_broadcast([P, 2 * HEADS, 2, FREQS, 2]),
                 op=ALU.mult,
             )
-            nc.gpsimd.tensor_tensor(
-                out=stage[s][:, 0 : 2 * HEADS, c, :],
-                in0=by_cos[j][:].rearrange("p (a d) -> p a d", d=DH),
-                in1=by_sin[:].rearrange("p (a d) -> p a d", d=DH),
-                op=ALU.add,
-            )
+            if half == count - 1:
+                nc.gpsimd.tensor_tensor(
+                    out=stage[s][:, 0 : 2 * HEADS, first : first + count, :].rearrange("p a c d -> p c a d"),
+                    in0=by_cos[s, first][:, 0:count].rearrange("p c (a d) -> p c a d", d=DH),
+                    in1=by_sin[s, first][:, 0:count].rearrange("p c (a d) -> p c a d", d=DH),
+                    op=ALU.add,
+                )
+
+        def bias_q(s, first, count):
+            shape = [P, HEADS, count, HALF]
+            for half, table in (
+                (0, bias_tab[:, s].unsqueeze(2).to_broadcast(shape)),
+                (1, bias_tab[:, UNIT + first : UNIT + first + count].rearrange("p c h d -> p h c d")),
+            ):
+                q_half = stage[s][:, 0:HEADS, first : first + count, half * HALF : (half + 1) * HALF]
+                nc.gpsimd.tensor_tensor(out=q_half, in0=q_half, in1=table, op=ALU.add)
 
         def bias_v(j):
             s, c = divmod(j, UNIT)
@@ -496,8 +512,6 @@ def tile_block_pa_t_kernel(
                 quantise(g)
             if step in tables:
                 tables[step]()
-            if step >= 0:
-                add_bias(step)
             if 0 <= step + SUMS < TILES:
                 sum_of_tile(step + SUMS)
             if 0 <= step + SQUARES < TILES:
@@ -508,5 +522,8 @@ def tile_block_pa_t_kernel(
                 bias_product(*arguments)
             if 0 <= step + PROJECT < TILES:
                 project(step + PROJECT)
+            s, c = divmod(step, UNIT)
+            if 0 <= s < UNIT - 1 and c in (3, UNIT - 1):
+                bias_q(s, 0 if c == 3 else 4, 4 if c == 3 else 3)
             if step in stores:
                 store(*stores[step])

@@ -30,17 +30,27 @@ STEP = 16.0 / 14.0
 
 FLOPS = 2 * 2 * 56 * 56 * C * 3 * E
 
-SUMS, SQUARES, STATS, AGGREGATE, ROOT, FINISH = 24, 20, 20, 19, 15, 14
-NORMALISE, TRANSPOSE, AFFINE, INTERLEAVE, QUANTISE, PROJECT = 14, 10, 8, 4, 2, 1
+SUMS, SQUARES, STATS, AGGREGATE, ROOT, FINISH = 22, 20, 21, 19, 15, 14
+NORMALISE, TRANSPOSE, AFFINE, INTERLEAVE, QUANTISE, PROJECT = 14, 9, 8, 4, 2, 1
 S_FROM, S_TO = 4, 12
 S_SLOT = 3
-V_INTER = (1,)
-V_AFF = ((0, 2), (0, 3), (1, 2), (1, 3))
+V_INTER = (0, 1)
+V_AFF = ()
 V_NORM = ()
-G_NORM = (6, 8, 10, 12, 14)
-TABLES_AT, SUM0_AT, SUM1_AT = -15, -8, 0
-PROD = (-12, -11, -7, -6)
-XFIRST = 4
+G_NORM = (6, 8, 10, 12, 14, 18, 22, 26, 30)
+TABLES_AT, SUM0_AT, SUM1_AT = -17, -11, -2
+PROD = (-16, -13, -8, -5)
+XFIRST = 3
+S_ODD = 0
+WHOLE = (0, 1, 2, 3, 4, 5)
+QPOS = 2
+SINGLES = (0,)
+BIAS_DELAY = 0
+V_SUM = ()
+V_BIAS = (43, 45, 47, 48)
+PE_SUM = (41, 42, 44, 46)
+V_COPY = ()
+PE_WAIT = 2
 
 
 def tile_block_pa_t_kernel(
@@ -72,10 +82,18 @@ def tile_block_pa_t_kernel(
         psum_v = ctx.enter_context(tc.psum_pool(name="psum_v", bufs=2))
         ctx.enter_context(tc.manual_schedule())
 
+        part = setup.tile([P, 1], I32)
+        nc.gpsimd.iota(part[:], pattern=[[0, 1]], base=0, channel_multiplier=1)
+        count_i = setup.tile([P, 2, UNIT], I32)
+        nc.gpsimd.iota(count_i[:], pattern=[[0, 2], [1, UNIT]], base=0, channel_multiplier=0)
         bias_rows = setup.tile([P, 2 * E], BF16)
-        nc.vector.memset(bias_rows[:], 0.0)
+        nc.gpsimd.memset(bias_rows[:], 0.0)
         ones = setup.tile([P, P], BF16)
         nc.gpsimd.memset(ones[:], 1.0)
+        one = setup.tile([P, 1], F32)
+        nc.vector.memset(one[:], 1.0)
+        warm = setup.tile([P, 2], F32)
+        nc.scalar.activation(out=warm[:, 0:1], in_=one[:], func=ACT.Sin)
         nc.scalar.dma_start(out=bias_rows[0:1, 0:E], in_=q_b.rearrange("(a n) -> a n", a=1))
         nc.scalar.dma_start(out=bias_rows[0:1, E : 2 * E], in_=v_b.rearrange("(a n) -> a n", a=1))
         gain_bf = setup.tile([P, PACK], BF16)
@@ -97,11 +115,7 @@ def tile_block_pa_t_kernel(
         for n in range(XFIRST):
             load_piece(n)
 
-        part = setup.tile([P, 1], I32)
-        nc.gpsimd.iota(part[:], pattern=[[0, 1]], base=0, channel_multiplier=1)
-        count_i = setup.tile([P, 2, UNIT], I32)
-        nc.gpsimd.iota(count_i[:], pattern=[[0, 2], [1, UNIT]], base=0, channel_multiplier=0)
-        ident = setup.tile([P, P], F32)
+        ident = consts.tile([P, P], F32)
         make_identity(nc, ident[:])
         biases = psum_t.tile([P, 2 * E], F32, name="bank3")
         nc.tensor.matmul(out=biases[:], lhsT=ones[:], rhs=bias_rows[:], start=True, stop=True)
@@ -123,10 +137,6 @@ def tile_block_pa_t_kernel(
         for n in range(XFIRST, len(pieces)):
             load_piece(n)
 
-        one = setup.tile([P, 1], F32)
-        nc.vector.memset(one[:], 1.0)
-        warm = setup.tile([P, 2], F32)
-        nc.scalar.activation(out=warm[:, 0:1], in_=one[:], func=ACT.Sin)
         bits_i = setup.tile([P, 2], I32)
         nc.vector.tensor_scalar(
             out=bits_i[:, 0:1], in0=part[:], scalar1=1, scalar2=1,
@@ -177,11 +187,11 @@ def tile_block_pa_t_kernel(
 
         stats, mean_var, minus_mean, squares, rstd, minus_mean_rstd = {}, {}, {}, {}, {}, {}
         xhat, banks, planes, grouped, codes, code_scales = {}, {}, {}, {}, {}, {}
-        qk, v_pair, stage, by_cos, by_sin = {}, {}, {}, {}, {}
+        qk, v_pair, stage, by_cos, by_sin, total = {}, {}, {}, {}, {}, {}
 
         def on_scalar(j):
             g, slot = place_of(j)
-            return S_FROM <= g <= S_TO and slot >= S_SLOT
+            return S_FROM <= g <= S_TO and slot >= S_SLOT - (S_ODD if g % 2 else 0)
 
         def stats_of_tile(j):
             s, c = divmod(j, UNIT)
@@ -335,7 +345,7 @@ def tile_block_pa_t_kernel(
 
         def in_pair(j):
             s, c = divmod(j, UNIT)
-            if s == UNIT - 1:
+            if s == UNIT - 1 or s in SINGLES:
                 return s, c, 1, 0
             return s, c - c % 2, min(2, UNIT - c + c % 2), c % 2
 
@@ -355,7 +365,7 @@ def tile_block_pa_t_kernel(
 
         def times_sin(j):
             s, first, count, half = in_pair(j)
-            if s == UNIT - 1:
+            if j in V_BIAS:
                 u_cos = by_cos[s, first][:, half, 0:E].rearrange("p (h g d) -> p h g d", h=HEADS, g=2)
                 nc.vector.tensor_tensor(
                     out=u_cos, in0=u_cos, in1=bias_tab[:, tables_of(j)].rearrange("p g h d -> p h g d"), op=ALU.add,
@@ -366,13 +376,36 @@ def tile_block_pa_t_kernel(
                 in1=sin_tab[:, tables_of(j)].unsqueeze(1).to_broadcast([P, 2 * HEADS, 2, FREQS, 2]),
                 op=ALU.mult,
             )
-            if half == count - 1:
-                nc.gpsimd.tensor_tensor(
+            if half == count - 1 and j not in PE_SUM:
+                engine = nc.vector if j in V_SUM else nc.gpsimd
+                engine.tensor_tensor(
                     out=stage[s][:, 0 : 2 * HEADS, first : first + count, :].rearrange("p a c d -> p c a d"),
                     in0=by_cos[s, first][:, 0:count].rearrange("p c (a d) -> p c a d", d=DH),
                     in1=by_sin[s, first][:, 0:count].rearrange("p c (a d) -> p c a d", d=DH),
                     op=ALU.add,
                 )
+
+        def add_up(j):
+            s, first, count, half = in_pair(j)
+            total[j] = psum_t.tile([P, 2 * E], F32, name="bank%d" % (j % BANK_TILES))
+            nc.tensor.matmul(out=total[j][:], lhsT=ident[:], rhs=by_cos[s, first][:, half], start=True, stop=False)
+            nc.tensor.matmul(
+                out=total[j][:, 0:E], lhsT=ident[:],
+                rhs=bias_tab[:, tables_of(j)].rearrange("p g h d -> p h g d"), start=False, stop=False,
+            )
+
+        def add_up_rest(j):
+            s, first, count, half = in_pair(j)
+            nc.tensor.matmul(out=total[j][:], lhsT=ident[:], rhs=by_sin[s, first][:, half], start=False, stop=True)
+
+        def copy_total(j):
+            s, c = divmod(j, UNIT)
+            target = stage[s][:, 0 : 2 * HEADS, c, :]
+            source = total[j][:].rearrange("p (a d) -> p a d", d=DH)
+            if j in V_COPY:
+                nc.vector.tensor_copy(out=target, in_=source)
+            else:
+                nc.scalar.copy(out=target, in_=source)
 
         def bias_q(s, first, count):
             shape = [P, HEADS, count, HALF]
@@ -411,9 +444,12 @@ def tile_block_pa_t_kernel(
                         ),
                     )
 
-        stores = {UNIT * s + UNIT - 1: (s, 0, UNIT) for s in range(UNIT - 1)}
-        stores[TILES - 4] = (UNIT - 1, 0, 4)
-        stores[TILES - 1] = (UNIT - 1, 4, 3)
+        def after(j):
+            return j + PE_WAIT if j in PE_SUM else j + (BIAS_DELAY if j < TILES - UNIT else 0)
+
+        stores = {}
+        for s, first, count in [(s, 0, UNIT) for s in range(UNIT - 1)] + [(UNIT - 1, 0, 4), (UNIT - 1, 4, 3)]:
+            stores.setdefault(max(after(s * UNIT + c) for c in range(first, first + count)), []).append((s, first, count))
 
         gain = consts.tile([P, PACK], F32)
         shift = consts.tile([P, PACK], F32)
@@ -481,11 +517,14 @@ def tile_block_pa_t_kernel(
             g, t = divmod(step + distance + lead, BANK_TILES)
             return (g, t) if 0 <= g < len(groups) else None
 
-        for step in range(-SUMS - lead, TILES):
+        for step in range(-SUMS - lead, TILES + max(PE_WAIT, BIAS_DELAY) + 1):
             due = quarter_due(step, TRANSPOSE)
             if due:
                 transpose(*due)
-            if step >= 0:
+            g = group_due(step, QUANTISE)
+            if g is not None and QPOS == 2:
+                quantise(g)
+            if 0 <= step < TILES:
                 times_cos(step)
                 bias_v(step)
             if 0 <= step + STATS < TILES:
@@ -508,7 +547,7 @@ def tile_block_pa_t_kernel(
                 if g is not None:
                     interleave(g, half)
             g = group_due(step, QUANTISE)
-            if g is not None:
+            if g is not None and QPOS == 0:
                 quantise(g)
             if step in tables:
                 tables[step]()
@@ -516,14 +555,25 @@ def tile_block_pa_t_kernel(
                 sum_of_tile(step + SUMS)
             if 0 <= step + SQUARES < TILES:
                 squares_of_tile(step + SQUARES)
-            if step >= 0:
+            if 0 <= step < TILES:
                 times_sin(step)
+            g = group_due(step, QUANTISE)
+            if g is not None and QPOS == 1:
+                quantise(g)
             for arguments in products.get(step, ()):
                 bias_product(*arguments)
             if 0 <= step + PROJECT < TILES:
                 project(step + PROJECT)
-            s, c = divmod(step, UNIT)
-            if 0 <= s < UNIT - 1 and c in (3, UNIT - 1):
-                bias_q(s, 0 if c == 3 else 4, 4 if c == 3 else 3)
-            if step in stores:
-                store(*stores[step])
+            if step in PE_SUM:
+                add_up(step)
+            if step - 1 in PE_SUM:
+                add_up_rest(step - 1)
+            if step - PE_WAIT in PE_SUM:
+                copy_total(step - PE_WAIT)
+            due = step - BIAS_DELAY
+            s, c = divmod(due, UNIT)
+            if 0 <= s < UNIT - 1 and c in ((UNIT - 1,) if s in WHOLE else (3, UNIT - 1)) and due not in V_BIAS:
+                first = 0 if c == 3 or s in WHOLE else 4
+                bias_q(s, first, len([j for j in range(s * UNIT + first, due + 1) if j not in PE_SUM]))
+            for arguments in stores.get(step, ()):
+                store(*arguments)

@@ -330,6 +330,11 @@ def tile_block_pa_t_kernel(
                 rhs=w_words[:, 0 : 2 * E * PACK].bitcast(FP8X4), rhs_scale=w_scales[:, 0 : 2 * E],
                 start=True, stop=True,
             )
+            nc.tensor.matmul_mx(
+                out=qk[j][:], lhsT=codes[g][:, tokens].bitcast(FP8X4), lhsT_scale=code_scales[g][:, tokens],
+                rhs=w_words[:, 0 : 2 * E * PACK].bitcast(FP8X4), rhs_scale=w_scales[:, 0 : 2 * E],
+                start=True, stop=True,
+            )
             if c % 2 == 0:
                 v_pair[s, c // 2] = psum_v.tile([P, 2, E], F32, name="v")
             nc.tensor.matmul_mx(

@@ -30,27 +30,26 @@ STEP = 16.0 / 14.0
 
 FLOPS = 2 * 2 * 56 * 56 * C * 3 * E
 
-SUMS, SQUARES, STATS, AGGREGATE, ROOT, FINISH = 22, 20, 21, 19, 15, 14
-NORMALISE, TRANSPOSE, AFFINE, INTERLEAVE, QUANTISE, PROJECT = 14, 9, 8, 4, 2, 1
-S_FROM, S_TO = 4, 12
+SUMS, SQUARES, STATS, AGGREGATE, ROOT, FINISH = 24, 23, 25, 23, 18, 17
+NORMALISE, TRANSPOSE, AFFINE, INTERLEAVE, QUANTISE, PROJECT = 17, 12, 11, 8, 4, 1
+Q_FIRST, Q_SECOND = 4, 4
+S_FROM, S_TO = 2, 12
 S_SLOT = 3
-V_INTER = (0, 1)
+V_INTER = (0, 1, 2)
 V_AFF = ()
 V_NORM = ()
-G_NORM = (6, 8, 10, 12, 14, 18, 22, 26, 30)
-TABLES_AT, SUM0_AT, SUM1_AT = -17, -11, -2
-PROD = (-16, -13, -8, -5)
-XFIRST = 3
-S_ODD = 0
-WHOLE = (0, 1, 2, 3, 4, 5)
-QPOS = 2
-SINGLES = (0,)
-BIAS_DELAY = 0
+G_NORM = [j for j in range(1, 49) if j < 22 or (j + 3) % 4 < 3]
+TABLES_AT = -19
+XFIRST = 5
+S_TWO = ()
+SINGLES = (0, 1, 2)
 V_SUM = ()
-V_BIAS = (43, 45, 47, 48)
-PE_SUM = (41, 42, 44, 46)
+PE_SUM = ()
 V_COPY = ()
 PE_WAIT = 2
+EARLY = (0,)
+DUMMY = 0
+T_BANKS = 2
 
 
 def tile_block_pa_t_kernel(
@@ -78,28 +77,11 @@ def tile_block_pa_t_kernel(
         rope = ctx.enter_context(tc.tile_pool(name="rope", bufs=3))
         stage_pool = ctx.enter_context(tc.tile_pool(name="stage", bufs=3))
         psum_t = ctx.enter_context(tc.psum_pool(name="psum_t", bufs=1))
+        psum_q = ctx.enter_context(tc.psum_pool(name="psum_q", bufs=4 - T_BANKS))
         psum_qk = ctx.enter_context(tc.psum_pool(name="psum_qk", bufs=2))
         psum_v = ctx.enter_context(tc.psum_pool(name="psum_v", bufs=2))
         ctx.enter_context(tc.manual_schedule())
 
-        part = setup.tile([P, 1], I32)
-        nc.gpsimd.iota(part[:], pattern=[[0, 1]], base=0, channel_multiplier=1)
-        count_i = setup.tile([P, 2, UNIT], I32)
-        nc.gpsimd.iota(count_i[:], pattern=[[0, 2], [1, UNIT]], base=0, channel_multiplier=0)
-        bias_rows = setup.tile([P, 2 * E], BF16)
-        nc.gpsimd.memset(bias_rows[:], 0.0)
-        ones = setup.tile([P, P], BF16)
-        nc.gpsimd.memset(ones[:], 1.0)
-        one = setup.tile([P, 1], F32)
-        nc.vector.memset(one[:], 1.0)
-        warm = setup.tile([P, 2], F32)
-        nc.scalar.activation(out=warm[:, 0:1], in_=one[:], func=ACT.Sin)
-        nc.scalar.dma_start(out=bias_rows[0:1, 0:E], in_=q_b.rearrange("(a n) -> a n", a=1))
-        nc.scalar.dma_start(out=bias_rows[0:1, E : 2 * E], in_=v_b.rearrange("(a n) -> a n", a=1))
-        gain_bf = setup.tile([P, PACK], BF16)
-        shift_bf = setup.tile([P, PACK], BF16)
-        nc.scalar.dma_start(out=gain_bf[:], in_=ln1_w.rearrange("(p t) -> p t", t=PACK))
-        nc.scalar.dma_start(out=shift_bf[:], in_=ln1_b.rearrange("(p t) -> p t", t=PACK))
         x_rounds = x.rearrange(
             "b (i r s) (u c) k -> s (b i r) u (c k)", i=4, r=2, s=UNIT, u=8, c=UNIT
         )
@@ -112,13 +94,38 @@ def tile_block_pa_t_kernel(
                 in_=x_rounds[s, :, :, first * C : (first + count) * C],
             )
 
-        for n in range(XFIRST):
+        one = setup.tile([P, 1], F32)
+        nc.vector.memset(one[:], 1.0)
+        warm = setup.tile([P, 2], F32)
+        nc.scalar.activation(out=warm[:, 0:1], in_=one[:], func=ACT.Sin)
+        part = setup.tile([P, 1], I32)
+        nc.gpsimd.iota(part[:], pattern=[[0, 1]], base=0, channel_multiplier=1)
+        count_i = setup.tile([P, 2, UNIT], I32)
+        nc.gpsimd.iota(count_i[:], pattern=[[0, 2], [1, UNIT]], base=0, channel_multiplier=0)
+        bias_rows = setup.tile([P, 2 * E], BF16)
+        nc.gpsimd.memset(bias_rows[:], 0.0)
+        ones = setup.tile([P, P], BF16)
+        nc.gpsimd.memset(ones[:], 1.0)
+        gain_bf = setup.tile([P, PACK], BF16)
+        shift_bf = setup.tile([P, PACK], BF16)
+        load_piece(0)
+        load_piece(1)
+        nc.sync.dma_start(out=gain_bf[:], in_=ln1_w.rearrange("(p t) -> p t", t=PACK))
+        nc.sync.dma_start(out=shift_bf[:], in_=ln1_b.rearrange("(p t) -> p t", t=PACK))
+        nc.sync.dma_start(out=bias_rows[0:1, 0:E], in_=q_b.rearrange("(a n) -> a n", a=1))
+        nc.sync.dma_start(out=bias_rows[0:1, E : 2 * E], in_=v_b.rearrange("(a n) -> a n", a=1))
+        for n in range(2, XFIRST):
             load_piece(n)
 
         ident = consts.tile([P, P], F32)
         make_identity(nc, ident[:])
-        biases = psum_t.tile([P, 2 * E], F32, name="bank3")
-        nc.tensor.matmul(out=biases[:], lhsT=ones[:], rhs=bias_rows[:], start=True, stop=True)
+        biases = psum_t.tile([P, 2 * E], F32, name="bank1")
+        nc.tensor.matmul(out=biases[:, 0:E], lhsT=ones[:], rhs=bias_rows[:, E : 2 * E], start=True, stop=True)
+        for m in range(2):
+            nc.tensor.matmul(
+                out=biases[:, E + 2 * m : E + 2 * m + 2], lhsT=bias_rows[:, m * P : (m + 1) * P], rhs=ones[:, 0:2],
+                start=True, stop=True,
+            )
 
         w_words = consts.tile([P, 3 * E * PACK], U8, align_bytes=64)
         w_scales = consts.tile([P, 3 * E], U8, align_bytes=64)
@@ -176,6 +183,10 @@ def tile_block_pa_t_kernel(
         cos_sin = setup.tile([P, 2, rows, FREQS], F32)
         nc.scalar.activation(out=cos_sin[:], in_=phase[:], func=ACT.Sin)
         nc.scalar.activation(out=warm[:, 1:2], in_=one[:], func=ACT.Abs_reciprocal_sqrt)
+        gain = consts.tile([P, PACK], F32)
+        shift = consts.tile([P, PACK], F32)
+        nc.scalar.copy(out=gain[:], in_=gain_bf[:])
+        nc.scalar.copy(out=shift[:], in_=shift_bf[:])
         sign = setup.tile([P, 2], F32)
         nc.vector.memset(sign[:, 0:1], -1.0)
         nc.vector.memset(sign[:, 1:2], 1.0)
@@ -187,11 +198,11 @@ def tile_block_pa_t_kernel(
 
         stats, mean_var, minus_mean, squares, rstd, minus_mean_rstd = {}, {}, {}, {}, {}, {}
         xhat, banks, planes, grouped, codes, code_scales = {}, {}, {}, {}, {}, {}
-        qk, v_pair, stage, by_cos, by_sin, total = {}, {}, {}, {}, {}, {}
+        q_turned, q_biased, qk, v_pair, stage, by_cos, by_sin, total = {}, {}, {}, {}, {}, {}, {}, {}
 
         def on_scalar(j):
             g, slot = place_of(j)
-            return S_FROM <= g <= S_TO and slot >= S_SLOT - (S_ODD if g % 2 else 0)
+            return S_FROM <= g <= S_TO and slot >= S_SLOT - (1 if g in S_TWO else 0)
 
         def stats_of_tile(j):
             s, c = divmod(j, UNIT)
@@ -278,7 +289,7 @@ def tile_block_pa_t_kernel(
                 )
 
         def transpose(g, t):
-            banks[g, t] = psum_t.tile([P, BANK_TILES * P], F32, name="bank%d" % t)
+            banks[g, t] = psum_t.tile([P, BANK_TILES * P], F32, name="bank%d" % ((BANK_TILES * g + t) % T_BANKS))
             for slot, j in enumerate(groups[g]):
                 nc.tensor.transpose(banks[g, t][:, slot * P : (slot + 1) * P], xhat[j][:, t, :], order[:])
 
@@ -320,29 +331,48 @@ def tile_block_pa_t_kernel(
                 in_=grouped[g][:, 0:cols, :].rearrange("p j t -> p (j t)"),
             )
 
+        def project_q(g, m):
+            cols = len(groups[g]) * P
+            columns = slice(m * P, (m + 1) * P)
+            q_turned[g, m] = psum_q.tile([P, BANK_TILES * P], F32, name="q_turned")
+            nc.tensor.matmul_mx(
+                out=q_turned[g, m][:, 0:cols],
+                lhsT=w_words[:, m * P * PACK : (m + 1) * P * PACK].bitcast(FP8X4), lhsT_scale=w_scales[:, columns],
+                rhs=codes[g][:, 0:cols].bitcast(FP8X4), rhs_scale=code_scales[g][:, 0:cols],
+                start=True, stop=True,
+            )
+
+        def bias_q(g, m):
+            cols = len(groups[g]) * P
+            if m == 0:
+                q_biased[g] = quant.tile([P, 2, BANK_TILES * P], F32, name="q_biased")
+            nc.scalar.activation(
+                out=q_biased[g][:, m, 0:cols], in_=q_turned[g, m][:, 0:cols], func=ACT.Identity,
+                bias=q_bias[:, 2 * m : 2 * m + 1],
+            )
+
+        def turn_back(j):
+            g, slot = place_of(j)
+            qk[j] = psum_qk.tile([P, 2 * E], F32, name="qk")
+            for m in range(2):
+                nc.tensor.transpose(
+                    qk[j][:, m * P : (m + 1) * P], q_biased[g][:, m, slot * P : (slot + 1) * P], ident[:]
+                )
+
         def project(j):
             s, c = divmod(j, UNIT)
             g, slot = place_of(j)
             tokens = slice(slot * P, (slot + 1) * P)
-            qk[j] = psum_qk.tile([P, 2 * E], F32, name="qk")
-            nc.tensor.matmul_mx(
-                out=qk[j][:], lhsT=codes[g][:, tokens].bitcast(FP8X4), lhsT_scale=code_scales[g][:, tokens],
-                rhs=w_words[:, 0 : 2 * E * PACK].bitcast(FP8X4), rhs_scale=w_scales[:, 0 : 2 * E],
-                start=True, stop=True,
-            )
-            nc.tensor.matmul_mx(
-                out=qk[j][:], lhsT=codes[g][:, tokens].bitcast(FP8X4), lhsT_scale=code_scales[g][:, tokens],
-                rhs=w_words[:, 0 : 2 * E * PACK].bitcast(FP8X4), rhs_scale=w_scales[:, 0 : 2 * E],
-                start=True, stop=True,
-            )
             if c % 2 == 0:
                 v_pair[s, c // 2] = psum_v.tile([P, 2, E], F32, name="v")
-            nc.tensor.matmul_mx(
-                out=v_pair[s, c // 2][:, c % 2, :],
-                lhsT=codes[g][:, tokens].bitcast(FP8X4), lhsT_scale=code_scales[g][:, tokens],
-                rhs=w_words[:, 2 * E * PACK : 3 * E * PACK].bitcast(FP8X4),
-                rhs_scale=w_scales[:, 2 * E : 3 * E], start=True, stop=True,
-            )
+            targets = [(1, qk[j][:, E : 2 * E])] * (1 + DUMMY) + [(2, v_pair[s, c // 2][:, c % 2, :])] * (1 + DUMMY)
+            for n, target in targets:
+                nc.tensor.matmul_mx(
+                    out=target,
+                    lhsT=codes[g][:, tokens].bitcast(FP8X4), lhsT_scale=code_scales[g][:, tokens],
+                    rhs=w_words[:, n * E * PACK : (n + 1) * E * PACK].bitcast(FP8X4),
+                    rhs_scale=w_scales[:, n * E : (n + 1) * E], start=True, stop=True,
+                )
 
         def tables_of(j):
             s, c = divmod(j, UNIT)
@@ -370,11 +400,6 @@ def tile_block_pa_t_kernel(
 
         def times_sin(j):
             s, first, count, half = in_pair(j)
-            if j in V_BIAS:
-                u_cos = by_cos[s, first][:, half, 0:E].rearrange("p (h g d) -> p h g d", h=HEADS, g=2)
-                nc.vector.tensor_tensor(
-                    out=u_cos, in0=u_cos, in1=bias_tab[:, tables_of(j)].rearrange("p g h d -> p h g d"), op=ALU.add,
-                )
             nc.vector.tensor_tensor(
                 out=by_sin[s, first][:, half].rearrange("p (a g m e) -> p a g m e", g=2, m=FREQS, e=2),
                 in0=qk[j][:].rearrange("p (a g m e) -> p a g m e", g=2, m=FREQS, e=2)[:, :, :, :, ::-1],
@@ -394,10 +419,6 @@ def tile_block_pa_t_kernel(
             s, first, count, half = in_pair(j)
             total[j] = psum_t.tile([P, 2 * E], F32, name="bank%d" % (j % BANK_TILES))
             nc.tensor.matmul(out=total[j][:], lhsT=ident[:], rhs=by_cos[s, first][:, half], start=True, stop=False)
-            nc.tensor.matmul(
-                out=total[j][:, 0:E], lhsT=ident[:],
-                rhs=bias_tab[:, tables_of(j)].rearrange("p g h d -> p h g d"), start=False, stop=False,
-            )
 
         def add_up_rest(j):
             s, first, count, half = in_pair(j)
@@ -411,15 +432,6 @@ def tile_block_pa_t_kernel(
                 nc.vector.tensor_copy(out=target, in_=source)
             else:
                 nc.scalar.copy(out=target, in_=source)
-
-        def bias_q(s, first, count):
-            shape = [P, HEADS, count, HALF]
-            for half, table in (
-                (0, bias_tab[:, s].unsqueeze(2).to_broadcast(shape)),
-                (1, bias_tab[:, UNIT + first : UNIT + first + count].rearrange("p c h d -> p h c d")),
-            ):
-                q_half = stage[s][:, 0:HEADS, first : first + count, half * HALF : (half + 1) * HALF]
-                nc.gpsimd.tensor_tensor(out=q_half, in0=q_half, in1=table, op=ALU.add)
 
         def bias_v(j):
             s, c = divmod(j, UNIT)
@@ -450,33 +462,21 @@ def tile_block_pa_t_kernel(
                     )
 
         def after(j):
-            return j + PE_WAIT if j in PE_SUM else j + (BIAS_DELAY if j < TILES - UNIT else 0)
+            return j + PE_WAIT if j in PE_SUM else j
 
         stores = {}
         for s, first, count in [(s, 0, UNIT) for s in range(UNIT - 1)] + [(UNIT - 1, 0, 4), (UNIT - 1, 4, 3)]:
             stores.setdefault(max(after(s * UNIT + c) for c in range(first, first + count)), []).append((s, first, count))
 
-        gain = consts.tile([P, PACK], F32)
-        shift = consts.tile([P, PACK], F32)
         cos_tab = consts.tile([P, rows, FREQS, 2], F32)
         sin_tab = consts.tile([P, rows, FREQS, 2], F32)
-        q_bias = setup.tile([P, E], F32)
-        q_bias_swapped = setup.tile([P, E], F32)
+        q_bias = consts.tile([P, 2 * 2], F32)
         v_bias = consts.tile([P, E], F32)
-        bias_tab = consts.tile([P, rows, HEADS, HALF], F32)
-        bias_cos = setup.tile([P, rows, HEADS, HALF], F32)
-        bias_sin = setup.tile([P, rows, HEADS, HALF], F32)
 
         def vector_tables():
             pairs = rows * FREQS
-            nc.vector.tensor_copy(out=gain[:], in_=gain_bf[:])
-            nc.vector.tensor_copy(out=shift[:], in_=shift_bf[:])
-            nc.vector.tensor_copy(out=q_bias[:], in_=biases[:, 0:E])
-            nc.vector.tensor_copy(
-                out=q_bias_swapped[:].rearrange("p (m e) -> p m e", e=2),
-                in_=biases[:, 0:E].rearrange("p (m e) -> p m e", e=2)[:, :, ::-1],
-            )
-            nc.vector.tensor_copy(out=v_bias[:], in_=biases[:, E : 2 * E])
+            nc.vector.tensor_copy(out=q_bias[:], in_=biases[:, E : E + 4])
+            nc.vector.tensor_copy(out=v_bias[:], in_=biases[:, 0:E])
             nc.vector.tensor_copy(
                 out=cos_tab[:].rearrange("p i m e -> p (i m) e"),
                 in_=cos_sin[:, 0].rearrange("p i m -> p (i m)").unsqueeze(2).to_broadcast([P, pairs, 2]),
@@ -488,97 +488,71 @@ def tile_block_pa_t_kernel(
                 op=ALU.mult,
             )
 
-        def bias_product(half, product, bias, table):
-            half_rows = slice(half * UNIT, (half + 1) * UNIT)
-            shape = [P, UNIT, HEADS, HALF]
-            nc.gpsimd.tensor_tensor(
-                out=product[:, half_rows],
-                in0=bias[:].rearrange("p (h g d) -> p g h d", h=HEADS, g=2)[:, half]
-                .unsqueeze(1).to_broadcast(shape),
-                in1=table[:, half_rows].rearrange("p i m e -> p i (m e)")
-                .unsqueeze(2).to_broadcast(shape),
-                op=ALU.mult,
-            )
+        tables = {TABLES_AT: vector_tables}
 
-        def bias_sum(half):
-            half_rows = slice(half * UNIT, (half + 1) * UNIT)
-            nc.vector.tensor_tensor(
-                out=bias_tab[:, half_rows], in0=bias_cos[:, half_rows], in1=bias_sin[:, half_rows], op=ALU.add
-            )
+        def early(g):
+            return EARLY[g] if g < len(EARLY) else 0
 
-        tables = {TABLES_AT: vector_tables, SUM0_AT: lambda: bias_sum(0), SUM1_AT: lambda: bias_sum(1)}
-        products = {
-            PROD[0]: ((0, bias_cos, q_bias, cos_tab),),
-            PROD[1]: ((0, bias_sin, q_bias_swapped, sin_tab),),
-            PROD[2]: ((1, bias_cos, q_bias, cos_tab),),
-            PROD[3]: ((1, bias_sin, q_bias_swapped, sin_tab),),
-        }
+        def due(step, distance):
+            found = []
+            for g in range(len(groups)):
+                slot = step + distance + early(g) - (BANK_TILES * g - lead)
+                if 0 <= slot < BANK_TILES:
+                    found.append((g, slot))
+            return found
 
-        def group_due(step, distance):
-            g, slot = divmod(step + distance + lead, BANK_TILES)
-            return g if slot == 0 and 0 <= g < len(groups) else None
+        def tiles_due(step, distance):
+            return [BANK_TILES * g - lead + slot for g, slot in due(step, distance) if BANK_TILES * g - lead + slot >= 0]
 
-        def quarter_due(step, distance):
-            g, t = divmod(step + distance + lead, BANK_TILES)
-            return (g, t) if 0 <= g < len(groups) else None
+        def groups_due(step, distance):
+            return [g for g, slot in due(step, distance) if slot == 0]
 
-        for step in range(-SUMS - lead, TILES + max(PE_WAIT, BIAS_DELAY) + 1):
-            due = quarter_due(step, TRANSPOSE)
-            if due:
-                transpose(*due)
-            g = group_due(step, QUANTISE)
-            if g is not None and QPOS == 2:
+        for step in range(-SUMS - lead - max(EARLY), TILES + PE_WAIT + 1):
+            for g, t in due(step, TRANSPOSE):
+                transpose(g, t)
+            if 0 <= step + PROJECT < TILES:
+                turn_back(step + PROJECT)
+            for g in groups_due(step, QUANTISE):
                 quantise(g)
             if 0 <= step < TILES:
                 times_cos(step)
                 bias_v(step)
-            if 0 <= step + STATS < TILES:
-                stats_of_tile(step + STATS)
-            if 0 <= step + AGGREGATE < TILES:
-                aggregate(step + AGGREGATE)
-            g = group_due(step, ROOT)
-            if g is not None:
+            for j in tiles_due(step, STATS):
+                stats_of_tile(j)
+            for j in tiles_due(step, AGGREGATE):
+                aggregate(j)
+            for g in groups_due(step, ROOT):
                 root(g)
-            g = group_due(step, FINISH)
-            if g is not None:
+            for g in groups_due(step, FINISH):
                 finish_stats(g)
-            if 0 <= step + NORMALISE < TILES:
-                normalise(step + NORMALISE)
-            due = quarter_due(step, AFFINE)
-            if due:
-                affine(*due)
+            for j in tiles_due(step, NORMALISE):
+                normalise(j)
+            for g, t in due(step, AFFINE):
+                affine(g, t)
             for half in range(2):
-                g = group_due(step, INTERLEAVE - half)
-                if g is not None:
+                for g in groups_due(step, INTERLEAVE - half):
                     interleave(g, half)
-            g = group_due(step, QUANTISE)
-            if g is not None and QPOS == 0:
-                quantise(g)
             if step in tables:
                 tables[step]()
-            if 0 <= step + SUMS < TILES:
-                sum_of_tile(step + SUMS)
-            if 0 <= step + SQUARES < TILES:
-                squares_of_tile(step + SQUARES)
+            for m, distance in enumerate((Q_FIRST - 1, Q_SECOND - 1)):
+                for g in groups_due(step, distance):
+                    bias_q(g, m)
+            for j in tiles_due(step, SUMS):
+                sum_of_tile(j)
+            for j in tiles_due(step, SQUARES):
+                squares_of_tile(j)
             if 0 <= step < TILES:
                 times_sin(step)
-            g = group_due(step, QUANTISE)
-            if g is not None and QPOS == 1:
-                quantise(g)
-            for arguments in products.get(step, ()):
-                bias_product(*arguments)
             if 0 <= step + PROJECT < TILES:
                 project(step + PROJECT)
+            for m, distance in enumerate((Q_FIRST, Q_SECOND)):
+                for g in groups_due(step, distance):
+                    project_q(g, m)
             if step in PE_SUM:
                 add_up(step)
             if step - 1 in PE_SUM:
                 add_up_rest(step - 1)
             if step - PE_WAIT in PE_SUM:
                 copy_total(step - PE_WAIT)
-            due = step - BIAS_DELAY
-            s, c = divmod(due, UNIT)
-            if 0 <= s < UNIT - 1 and c in ((UNIT - 1,) if s in WHOLE else (3, UNIT - 1)) and due not in V_BIAS:
-                first = 0 if c == 3 or s in WHOLE else 4
-                bias_q(s, first, len([j for j in range(s * UNIT + first, due + 1) if j not in PE_SUM]))
             for arguments in stores.get(step, ()):
                 store(*arguments)

@@ -30,17 +30,17 @@ STEP = 16.0 / 14.0
 
 FLOPS = 2 * 2 * 56 * 56 * C * 3 * E
 
-SUMS, SQUARES, STATS, AGGREGATE, ROOT, FINISH = 24, 23, 25, 23, 18, 17
-NORMALISE, TRANSPOSE, AFFINE, INTERLEAVE, QUANTISE, PROJECT = 17, 12, 11, 8, 4, 1
+SUMS, SQUARES, STATS, AGGREGATE, ROOT, FINISH = 28, 27, 26, 25, 20, 19
+NORMALISE, TRANSPOSE, AFFINE, INTERLEAVE, QUANTISE, PROJECT = 18, 12, 11, 7, 4, 1
 Q_FIRST, Q_SECOND = 4, 4
-S_FROM, S_TO = 2, 12
+S_FROM, S_TO = 6, 12
 S_SLOT = 3
 V_INTER = (0, 1, 2)
 V_AFF = ()
 V_NORM = ()
-G_NORM = [j for j in range(1, 49) if j < 22 or (j + 3) % 4 < 3]
-TABLES_AT = -19
-XFIRST = 5
+G_NORM = [j for j in range(3, 49) if j < 7 or j % 2]
+TABLES_AT = -25
+XFIRST = 7
 S_TWO = ()
 SINGLES = (0, 1, 2)
 V_SUM = ()
@@ -50,6 +50,8 @@ PE_WAIT = 2
 EARLY = (0,)
 DUMMY = 0
 T_BANKS = 2
+G_INTER = ()
+HALVES = 2
 
 
 def tile_block_pa_t_kernel(
@@ -309,7 +311,7 @@ def tile_block_pa_t_kernel(
                 )
 
         def interleave(g, half):
-            tiles = BANK_TILES // 2
+            tiles = BANK_TILES // HALVES
             cols = slice(half * tiles * P, min((half + 1) * tiles, len(groups[g])) * P)
             if cols.stop <= cols.start:
                 return
@@ -319,6 +321,8 @@ def tile_block_pa_t_kernel(
             target = grouped[g][:, cols, :].rearrange("p (j i) t -> p j t i", i=4)
             if g in V_INTER:
                 nc.vector.tensor_copy(out=target, in_=source)
+            elif g in G_INTER:
+                nc.gpsimd.tensor_scalar(out=target, in0=source, scalar1=1.0, scalar2=0.0, op0=ALU.mult, op1=ALU.add)
             else:
                 nc.scalar.copy(out=target, in_=source)
 
@@ -529,7 +533,7 @@ def tile_block_pa_t_kernel(
                 normalise(j)
             for g, t in due(step, AFFINE):
                 affine(g, t)
-            for half in range(2):
+            for half in range(HALVES):
                 for g in groups_due(step, INTERLEAVE - half):
                     interleave(g, half)
             if step in tables:

import math
from contextlib import ExitStack

import concourse.mybir as mybir
from concourse.masks import make_identity

F32 = mybir.dt.float32
BF16 = mybir.dt.bfloat16
I32 = mybir.dt.int32
U32 = mybir.dt.uint32
U8 = mybir.dt.uint8
FP8X4 = mybir.dt.float8_e4m3fn_x4
ALU = mybir.AluOpType
ACT = mybir.ActivationFunctionType

P = 128
C = 512
PACK = 4
E = 256
HEADS = 4
DH = 64
HALF = 32
FREQS = 16
UNIT = 7
TILES = UNIT * UNIT
BANK_TILES = 4
EPS = 1e-6
THETA = 10000.0
STEP = 16.0 / 14.0

FLOPS = 2 * 2 * 56 * 56 * C * 3 * E

SUMS, SQUARES, STATS, AGGREGATE, ROOT, FINISH = 28, 27, 26, 25, 20, 19
NORMALISE, TRANSPOSE, AFFINE, INTERLEAVE, QUANTISE, PROJECT = 18, 12, 11, 7, 4, 1
Q_FIRST, Q_SECOND = 4, 4
S_FROM, S_TO = 6, 12
S_SLOT = 3
V_INTER = (0, 1, 2)
V_AFF = ()
V_NORM = ()
G_NORM = [j for j in range(3, 49) if j < 7 or j % 2]
TABLES_AT = -25
XFIRST = 7
S_TWO = ()
SINGLES = (0, 1, 2)
V_SUM = ()
PE_SUM = ()
V_COPY = ()
PE_WAIT = 2
EARLY = (0,)
DUMMY = 0
T_BANKS = 2
G_INTER = ()
HALVES = 2


def tile_block_pa_t_kernel(
    tc, x, ln1_w, ln1_b, q_w_words, q_w_scales, q_b, k_w_words, k_w_scales,
    v_w_words, v_w_scales, v_b, out_0, out_1, out_2,
):
    nc = tc.nc
    pieces = [(0, 0, 1), (0, 1, 3), (0, 4, 3)]
    pieces += [(s, first, min(4, UNIT - first)) for s in range(1, UNIT) for first in (0, 4)]
    lead = BANK_TILES - 1
    groups = [[j for j in range(first, first + BANK_TILES) if j >= 0] for first in range(-lead, TILES, BANK_TILES)]

    def place_of(j):
        g = (j + lead) // BANK_TILES
        return g, j - groups[g][0]

    with ExitStack() as ctx:
        consts = ctx.enter_context(tc.tile_pool(name="consts", bufs=1))
        setup = ctx.enter_context(tc.tile_pool(name="setup", bufs=1))
        x_pool = ctx.enter_context(tc.tile_pool(name="x", bufs=1))
        small = ctx.enter_context(tc.tile_pool(name="small", bufs=6))
        scratch = ctx.enter_context(tc.tile_pool(name="scratch", bufs=2))
        xhat_pool = ctx.enter_context(tc.tile_pool(name="xhat", bufs=3 * BANK_TILES))
        quant = ctx.enter_context(tc.tile_pool(name="quant", bufs=3))
        rope = ctx.enter_context(tc.tile_pool(name="rope", bufs=3))
        stage_pool = ctx.enter_context(tc.tile_pool(name="stage", bufs=3))
        psum_t = ctx.enter_context(tc.psum_pool(name="psum_t", bufs=1))
        psum_q = ctx.enter_context(tc.psum_pool(name="psum_q", bufs=4 - T_BANKS))
        psum_qk = ctx.enter_context(tc.psum_pool(name="psum_qk", bufs=2))
        psum_v = ctx.enter_context(tc.psum_pool(name="psum_v", bufs=2))
        ctx.enter_context(tc.manual_schedule())

        x_rounds = x.rearrange(
            "b (i r s) (u c) k -> s (b i r) u (c k)", i=4, r=2, s=UNIT, u=8, c=UNIT
        )
        x_sb = [x_pool.tile([P, UNIT, C], BF16, name="x%d" % s) for s in range(UNIT)]

        def load_piece(n):
            s, first, count = pieces[n]
            nc.sync.dma_start(
                out=x_sb[s][:, first : first + count, :].rearrange("p c k -> p (c k)"),
                in_=x_rounds[s, :, :, first * C : (first + count) * C],
            )

        one = setup.tile([P, 1], F32)
        nc.vector.memset(one[:], 1.0)
        warm = setup.tile([P, 2], F32)
        nc.scalar.activation(out=warm[:, 0:1], in_=one[:], func=ACT.Sin)
        part = setup.tile([P, 1], I32)
        nc.gpsimd.iota(part[:], pattern=[[0, 1]], base=0, channel_multiplier=1)
        count_i = setup.tile([P, 2, UNIT], I32)
        nc.gpsimd.iota(count_i[:], pattern=[[0, 2], [1, UNIT]], base=0, channel_multiplier=0)
        bias_rows = setup.tile([P, 2 * E], BF16)
        nc.gpsimd.memset(bias_rows[:], 0.0)
        ones = setup.tile([P, P], BF16)
        nc.gpsimd.memset(ones[:], 1.0)
        gain_bf = setup.tile([P, PACK], BF16)
        shift_bf = setup.tile([P, PACK], BF16)
        load_piece(0)
        load_piece(1)
        nc.sync.dma_start(out=gain_bf[:], in_=ln1_w.rearrange("(p t) -> p t", t=PACK))
        nc.sync.dma_start(out=shift_bf[:], in_=ln1_b.rearrange("(p t) -> p t", t=PACK))
        nc.sync.dma_start(out=bias_rows[0:1, 0:E], in_=q_b.rearrange("(a n) -> a n", a=1))
        nc.sync.dma_start(out=bias_rows[0:1, E : 2 * E], in_=v_b.rearrange("(a n) -> a n", a=1))
        for n in range(2, XFIRST):
            load_piece(n)

        ident = consts.tile([P, P], F32)
        make_identity(nc, ident[:])
        biases = psum_t.tile([P, 2 * E], F32, name="bank1")
        nc.tensor.matmul(out=biases[:, 0:E], lhsT=ones[:], rhs=bias_rows[:, E : 2 * E], start=True, stop=True)
        for m in range(2):
            nc.tensor.matmul(
                out=biases[:, E + 2 * m : E + 2 * m + 2], lhsT=bias_rows[:, m * P : (m + 1) * P], rhs=ones[:, 0:2],
                start=True, stop=True,
            )

        w_words = consts.tile([P, 3 * E * PACK], U8, align_bytes=64)
        w_scales = consts.tile([P, 3 * E], U8, align_bytes=64)
        nc.vector.memset(w_scales[:].bitcast(I32), 0)
        for n, words in enumerate((q_w_words, k_w_words, v_w_words)):
            nc.sync.dma_start(
                out=w_words[:, n * E * PACK : (n + 1) * E * PACK].bitcast(I32),
                in_=words[0].rearrange("p n t -> p (n t)").bitcast(I32),
            )
        for n, scales in enumerate((q_w_scales, k_w_scales, v_w_scales)):
            for quadrant in range(4):
                nc.sync.dma_start(
                    out=w_scales[32 * quadrant : 32 * quadrant + 4, n * E : (n + 1) * E].bitcast(I32),
                    in_=scales[0, 4 * quadrant : 4 * quadrant + 4, :].bitcast(I32),
                )
        for n in range(XFIRST, len(pieces)):
            load_piece(n)

        bits_i = setup.tile([P, 2], I32)
        nc.vector.tensor_scalar(
            out=bits_i[:, 0:1], in0=part[:], scalar1=1, scalar2=1,
            op0=ALU.logical_shift_right, op1=ALU.bitwise_and,
        )
        nc.vector.tensor_single_scalar(out=bits_i[:, 1:2], in_=part[:], scalar=1, op=ALU.bitwise_and)
        freq = setup.tile([P, FREQS], F32)
        for m in range(4):
            nc.vector.tensor_scalar_mul(out=freq[:, m : m + 1], in0=one[:], scalar1=STEP * THETA ** (-m / FREQS))
        place = setup.tile([P, 2, UNIT], F32)
        nc.vector.scalar_tensor_tensor(
            out=place[:], in0=bits_i[:].unsqueeze(2).to_broadcast([P, 2, UNIT]), scalar=float(UNIT),
            in1=count_i[:], op0=ALU.mult, op1=ALU.add,
        )
        for m in range(4, FREQS, 4):
            nc.vector.tensor_scalar_mul(out=freq[:, m : m + 4], in0=freq[:, 0:4], scalar1=THETA ** (-m / FREQS))
        rows = 2 * UNIT
        phase = setup.tile([P, 2, rows, FREQS], F32)
        nc.vector.tensor_tensor(
            out=phase[:, 1],
            in0=place[:].rearrange("p g i -> p (g i)").unsqueeze(2).to_broadcast([P, rows, FREQS]),
            in1=freq[:].unsqueeze(1).to_broadcast([P, rows, FREQS]),
            op=ALU.mult,
        )
        nc.vector.tensor_scalar_add(out=phase[:, 0], in0=phase[:, 1], scalar1=math.pi / 2)
        fast = len([m for m in range(FREQS) if (rows - 1) * STEP * THETA ** (-m / FREQS) + math.pi / 2 >= math.pi])
        turning = phase[:, :, :, 0:fast].rearrange("p a i m -> p (a i) m")
        turns = setup.tile([P, 2 * rows, fast], F32)
        nc.vector.tensor_single_scalar(out=turns[:], in_=turning, scalar=math.pi, op=ALU.is_ge)
        for odd in (3, 5):
            nc.vector.scalar_tensor_tensor(
                out=turns[:], in0=turning, scalar=odd * math.pi, in1=turns[:], op0=ALU.is_ge, op1=ALU.add,
            )
        nc.vector.scalar_tensor_tensor(
            out=turning, in0=turns[:], scalar=-2.0 * math.pi, in1=turning, op0=ALU.mult, op1=ALU.add,
        )
        cos_sin = setup.tile([P, 2, rows, FREQS], F32)
        nc.scalar.activation(out=cos_sin[:], in_=phase[:], func=ACT.Sin)
        nc.scalar.activation(out=warm[:, 1:2], in_=one[:], func=ACT.Abs_reciprocal_sqrt)
        gain = consts.tile([P, PACK], F32)
        shift = consts.tile([P, PACK], F32)
        nc.scalar.copy(out=gain[:], in_=gain_bf[:])
        nc.scalar.copy(out=shift[:], in_=shift_bf[:])
        sign = setup.tile([P, 2], F32)
        nc.vector.memset(sign[:, 0:1], -1.0)
        nc.vector.memset(sign[:, 1:2], 1.0)
        order = consts.tile([P, P], F32)
        nc.vector.tensor_copy(
            out=order[:].rearrange("p (a j r h) -> p a j r h", a=8, j=4, r=2, h=2),
            in_=ident[:].rearrange("p (a r j h) -> p a j r h", a=8, r=2, j=4, h=2),
        )

        stats, mean_var, minus_mean, squares, rstd, minus_mean_rstd = {}, {}, {}, {}, {}, {}
        xhat, banks, planes, grouped, codes, code_scales = {}, {}, {}, {}, {}, {}
        q_turned, q_biased, qk, v_pair, stage, by_cos, by_sin, total = {}, {}, {}, {}, {}, {}, {}, {}

        def on_scalar(j):
            g, slot = place_of(j)
            return S_FROM <= g <= S_TO and slot >= S_SLOT - (1 if g in S_TWO else 0)

        def stats_of_tile(j):
            s, c = divmod(j, UNIT)
            g, slot = place_of(j)
            if on_scalar(j):
                return
            if slot == 0:
                stats[g] = small.tile([P, BANK_TILES, 6], F32, name="stats")
                mean_var[g] = small.tile([P, BANK_TILES, 2], F32, name="mean_var")
            nc.vector.bn_stats(out=stats[g][:, slot, :], in_=x_sb[s][:, c, :])

        def aggregate(j):
            g, slot = place_of(j)
            if on_scalar(j):
                return
            nc.vector.bn_aggr(out=mean_var[g][:, slot, :], in_=stats[g][:, slot, :])

        def sum_of_tile(j):
            s, c = divmod(j, UNIT)
            g, slot = place_of(j)
            if not on_scalar(j):
                return
            if g not in minus_mean:
                minus_mean[g] = small.tile([P, BANK_TILES], F32, name="minus_mean")
            unread = scratch.tile([P, C], BF16, name="unread")
            nc.scalar.activation(
                out=unread[:], in_=x_sb[s][:, c, :], func=ACT.Identity, scale=-1.0 / C,
                accum_out=minus_mean[g][:, slot : slot + 1],
            )

        def squares_of_tile(j):
            s, c = divmod(j, UNIT)
            g, slot = place_of(j)
            if not on_scalar(j):
                return
            if g not in squares:
                squares[g] = small.tile([P, BANK_TILES], F32, name="squares")
            unread = scratch.tile([P, C], BF16, name="unread")
            nc.scalar.activation(
                out=unread[:], in_=x_sb[s][:, c, :], func=ACT.Square, bias=minus_mean[g][:, slot : slot + 1],
                accum_out=squares[g][:, slot : slot + 1],
            )

        def root(g):
            rstd[g] = small.tile([P, BANK_TILES], F32, name="rstd")
            count = len([j for j in groups[g] if not on_scalar(j)])
            if count < len(groups[g]):
                nc.scalar.activation(
                    out=rstd[g][:, count:], in_=squares[g][:, count:], func=ACT.Abs_reciprocal_sqrt,
                    scale=1.0 / C, bias=EPS,
                )
            else:
                minus_mean[g] = small.tile([P, BANK_TILES], F32, name="minus_mean")
            nc.scalar.activation(
                out=rstd[g][:, 0:count], in_=mean_var[g][:, 0:count, 1], func=ACT.Abs_reciprocal_sqrt, bias=EPS
            )
            nc.scalar.activation(
                out=minus_mean[g][:, 0:count], in_=mean_var[g][:, 0:count, 0], func=ACT.Identity, scale=-1.0
            )

        def finish_stats(g):
            minus_mean_rstd[g] = small.tile([P, BANK_TILES], F32, name="minus_mean_rstd")
            for slot in range(len(groups[g])):
                nc.scalar.activation(
                    out=minus_mean_rstd[g][:, slot : slot + 1], in_=minus_mean[g][:, slot : slot + 1],
                    func=ACT.Identity, scale=rstd[g][:, slot : slot + 1],
                )

        def normalise(j):
            s, c = divmod(j, UNIT)
            g, slot = place_of(j)
            xhat[j] = xhat_pool.tile([P, PACK, P], F32, name="xhat")
            source = x_sb[s][:, c, :].rearrange("p (q t) -> p t q", t=PACK)
            if j in V_NORM or j in G_NORM:
                engine = nc.vector if j in V_NORM else nc.gpsimd
                engine.tensor_scalar(
                    out=xhat[j][:], in0=source, scalar1=rstd[g][:, slot : slot + 1],
                    scalar2=minus_mean_rstd[g][:, slot : slot + 1], op0=ALU.mult, op1=ALU.add,
                )
            else:
                nc.scalar.activation(
                    out=xhat[j][:], in_=source, func=ACT.Identity, scale=rstd[g][:, slot : slot + 1],
                    bias=minus_mean_rstd[g][:, slot : slot + 1],
                )

        def transpose(g, t):
            banks[g, t] = psum_t.tile([P, BANK_TILES * P], F32, name="bank%d" % ((BANK_TILES * g + t) % T_BANKS))
            for slot, j in enumerate(groups[g]):
                nc.tensor.transpose(banks[g, t][:, slot * P : (slot + 1) * P], xhat[j][:, t, :], order[:])

        def affine(g, t):
            cols = len(groups[g]) * P
            if t == 0:
                planes[g] = quant.tile([P, PACK, BANK_TILES * P], BF16, name="planes")
            if (g, t) in V_AFF:
                nc.vector.tensor_scalar(
                    out=planes[g][:, t, 0:cols], in0=banks[g, t][:, 0:cols], scalar1=gain[:, t : t + 1],
                    scalar2=shift[:, t : t + 1], op0=ALU.mult, op1=ALU.add,
                )
            else:
                nc.scalar.activation(
                    out=planes[g][:, t, 0:cols], in_=banks[g, t][:, 0:cols], func=ACT.Identity,
                    scale=gain[:, t : t + 1], bias=shift[:, t : t + 1],
                )

        def interleave(g, half):
            tiles = BANK_TILES // HALVES
            cols = slice(half * tiles * P, min((half + 1) * tiles, len(groups[g])) * P)
            if cols.stop <= cols.start:
                return
            if half == 0:
                grouped[g] = quant.tile([P, BANK_TILES * P, PACK], BF16, name="grouped", align_bytes=64)
            source = planes[g][:, :, cols].rearrange("p t (j i) -> p j t i", i=4)
            target = grouped[g][:, cols, :].rearrange("p (j i) t -> p j t i", i=4)
            if g in V_INTER:
                nc.vector.tensor_copy(out=target, in_=source)
            elif g in G_INTER:
                nc.gpsimd.tensor_scalar(out=target, in0=source, scalar1=1.0, scalar2=0.0, op0=ALU.mult, op1=ALU.add)
            else:
                nc.scalar.copy(out=target, in_=source)

        def quantise(g):
            cols = len(groups[g]) * P
            codes[g] = quant.tile([P, BANK_TILES * P], U32, name="codes", align_bytes=64)
            code_scales[g] = quant.tile([P, BANK_TILES * P], U8, name="code_scales", align_bytes=64)
            nc.vector.quantize_mx(
                out=codes[g][:, 0:cols].bitcast(FP8X4), scales=code_scales[g][:, 0:cols],
                in_=grouped[g][:, 0:cols, :].rearrange("p j t -> p (j t)"),
            )

        def project_q(g, m):
            cols = len(groups[g]) * P
            columns = slice(m * P, (m + 1) * P)
            q_turned[g, m] = psum_q.tile([P, BANK_TILES * P], F32, name="q_turned")
            nc.tensor.matmul_mx(
                out=q_turned[g, m][:, 0:cols],
                lhsT=w_words[:, m * P * PACK : (m + 1) * P * PACK].bitcast(FP8X4), lhsT_scale=w_scales[:, columns],
                rhs=codes[g][:, 0:cols].bitcast(FP8X4), rhs_scale=code_scales[g][:, 0:cols],
                start=True, stop=True,
            )

        def bias_q(g, m):
            cols = len(groups[g]) * P
            if m == 0:
                q_biased[g] = quant.tile([P, 2, BANK_TILES * P], F32, name="q_biased")
            nc.scalar.activation(
                out=q_biased[g][:, m, 0:cols], in_=q_turned[g, m][:, 0:cols], func=ACT.Identity,
                bias=q_bias[:, 2 * m : 2 * m + 1],
            )

        def turn_back(j):
            g, slot = place_of(j)
            qk[j] = psum_qk.tile([P, 2 * E], F32, name="qk")
            for m in range(2):
                nc.tensor.transpose(
                    qk[j][:, m * P : (m + 1) * P], q_biased[g][:, m, slot * P : (slot + 1) * P], ident[:]
                )

        def project(j):
            s, c = divmod(j, UNIT)
            g, slot = place_of(j)
            tokens = slice(slot * P, (slot + 1) * P)
            if c % 2 == 0:
                v_pair[s, c // 2] = psum_v.tile([P, 2, E], F32, name="v")
            targets = [(1, qk[j][:, E : 2 * E])] * (1 + DUMMY) + [(2, v_pair[s, c // 2][:, c % 2, :])] * (1 + DUMMY)
            for n, target in targets:
                nc.tensor.matmul_mx(
                    out=target,
                    lhsT=codes[g][:, tokens].bitcast(FP8X4), lhsT_scale=code_scales[g][:, tokens],
                    rhs=w_words[:, n * E * PACK : (n + 1) * E * PACK].bitcast(FP8X4),
                    rhs_scale=w_scales[:, n * E : (n + 1) * E], start=True, stop=True,
                )

        def tables_of(j):
            s, c = divmod(j, UNIT)
            return slice(s, UNIT + c + 1, UNIT + c - s)

        def in_pair(j):
            s, c = divmod(j, UNIT)
            if s == UNIT - 1 or s in SINGLES:
                return s, c, 1, 0
            return s, c - c % 2, min(2, UNIT - c + c % 2), c % 2

        def times_cos(j):
            s, first, count, half = in_pair(j)
            if j % UNIT == 0:
                stage[s] = stage_pool.tile([P, 3 * HEADS, UNIT, DH], F32, name="stage")
            if half == 0:
                by_cos[s, first] = rope.tile([P, 2, 2 * E], F32, name="by_cos")
                by_sin[s, first] = rope.tile([P, 2, 2 * E], F32, name="by_sin")
            nc.vector.tensor_tensor(
                out=by_cos[s, first][:, half].rearrange("p (a g m e) -> p a g m e", g=2, m=FREQS, e=2),
                in0=qk[j][:].rearrange("p (a g m e) -> p a g m e", g=2, m=FREQS, e=2),
                in1=cos_tab[:, tables_of(j)].unsqueeze(1).to_broadcast([P, 2 * HEADS, 2, FREQS, 2]),
                op=ALU.mult,
            )

        def times_sin(j):
            s, first, count, half = in_pair(j)
            nc.vector.tensor_tensor(
                out=by_sin[s, first][:, half].rearrange("p (a g m e) -> p a g m e", g=2, m=FREQS, e=2),
                in0=qk[j][:].rearrange("p (a g m e) -> p a g m e", g=2, m=FREQS, e=2)[:, :, :, :, ::-1],
                in1=sin_tab[:, tables_of(j)].unsqueeze(1).to_broadcast([P, 2 * HEADS, 2, FREQS, 2]),
                op=ALU.mult,
            )
            if half == count - 1 and j not in PE_SUM:
                engine = nc.vector if j in V_SUM else nc.gpsimd
                engine.tensor_tensor(
                    out=stage[s][:, 0 : 2 * HEADS, first : first + count, :].rearrange("p a c d -> p c a d"),
                    in0=by_cos[s, first][:, 0:count].rearrange("p c (a d) -> p c a d", d=DH),
                    in1=by_sin[s, first][:, 0:count].rearrange("p c (a d) -> p c a d", d=DH),
                    op=ALU.add,
                )

        def add_up(j):
            s, first, count, half = in_pair(j)
            total[j] = psum_t.tile([P, 2 * E], F32, name="bank%d" % (j % BANK_TILES))
            nc.tensor.matmul(out=total[j][:], lhsT=ident[:], rhs=by_cos[s, first][:, half], start=True, stop=False)

        def add_up_rest(j):
            s, first, count, half = in_pair(j)
            nc.tensor.matmul(out=total[j][:], lhsT=ident[:], rhs=by_sin[s, first][:, half], start=False, stop=True)

        def copy_total(j):
            s, c = divmod(j, UNIT)
            target = stage[s][:, 0 : 2 * HEADS, c, :]
            source = total[j][:].rearrange("p (a d) -> p a d", d=DH)
            if j in V_COPY:
                nc.vector.tensor_copy(out=target, in_=source)
            else:
                nc.scalar.copy(out=target, in_=source)

        def bias_v(j):
            s, c = divmod(j, UNIT)
            if c % 2 == 0 and c != UNIT - 1:
                return
            count = c % 2 + 1
            first = c + 1 - count
            nc.vector.tensor_tensor(
                out=stage[s][:, 2 * HEADS : 3 * HEADS, first : first + count, :].rearrange("p h c d -> p c h d"),
                in0=v_pair[s, c // 2][:, 0:count, :].rearrange("p c (h d) -> p c h d", d=DH),
                in1=v_bias[:].rearrange("p (h d) -> p h d", d=DH).unsqueeze(1).to_broadcast([P, count, HEADS, DH]),
                op=ALU.add,
            )

        out_views = [
            o.rearrange("w h (r s f c) d -> s r f w h (c d)", r=2, s=UNIT, f=2, c=UNIT)
            for o in (out_0, out_1, out_2)
        ]

        def store(s, first, count):
            for n in (2, 0, 1):
                for rf in range(4):
                    nc.sync.dma_start(
                        out=out_views[n][s, rf // 2, rf % 2, :, :, first * DH : (first + count) * DH],
                        in_=stage[s][rf:P:4, n * HEADS : (n + 1) * HEADS, first : first + count].rearrange(
                            "p h c d -> p h (c d)"
                        ),
                    )

        def after(j):
            return j + PE_WAIT if j in PE_SUM else j

        stores = {}
        for s, first, count in [(s, 0, UNIT) for s in range(UNIT - 1)] + [(UNIT - 1, 0, 4), (UNIT - 1, 4, 3)]:
            stores.setdefault(max(after(s * UNIT + c) for c in range(first, first + count)), []).append((s, first, count))

        cos_tab = consts.tile([P, rows, FREQS, 2], F32)
        sin_tab = consts.tile([P, rows, FREQS, 2], F32)
        q_bias = consts.tile([P, 2 * 2], F32)
        v_bias = consts.tile([P, E], F32)

        def vector_tables():
            pairs = rows * FREQS
            nc.vector.tensor_copy(out=q_bias[:], in_=biases[:, E : E + 4])
            nc.vector.tensor_copy(out=v_bias[:], in_=biases[:, 0:E])
            nc.vector.tensor_copy(
                out=cos_tab[:].rearrange("p i m e -> p (i m) e"),
                in_=cos_sin[:, 0].rearrange("p i m -> p (i m)").unsqueeze(2).to_broadcast([P, pairs, 2]),
            )
            nc.vector.tensor_tensor(
                out=sin_tab[:].rearrange("p i m e -> p (i m) e"),
                in0=cos_sin[:, 1].rearrange("p i m -> p (i m)").unsqueeze(2).to_broadcast([P, pairs, 2]),
                in1=sign[:].unsqueeze(1).to_broadcast([P, pairs, 2]),
                op=ALU.mult,
            )

        tables = {TABLES_AT: vector_tables}

        def early(g):
            return EARLY[g] if g < len(EARLY) else 0

        def due(step, distance):
            found = []
            for g in range(len(groups)):
                slot = step + distance + early(g) - (BANK_TILES * g - lead)
                if 0 <= slot < BANK_TILES:
                    found.append((g, slot))
            return found

        def tiles_due(step, distance):
            return [BANK_TILES * g - lead + slot for g, slot in due(step, distance) if BANK_TILES * g - lead + slot >= 0]

        def groups_due(step, distance):
            return [g for g, slot in due(step, distance) if slot == 0]

        for step in range(-SUMS - lead - max(EARLY), TILES + PE_WAIT + 1):
            for g, t in due(step, TRANSPOSE):
                transpose(g, t)
            if 0 <= step + PROJECT < TILES:
                turn_back(step + PROJECT)
            for g in groups_due(step, QUANTISE):
                quantise(g)
            if 0 <= step < TILES:
                times_cos(step)
                bias_v(step)
            for j in tiles_due(step, STATS):
                stats_of_tile(j)
            for j in tiles_due(step, AGGREGATE):
                aggregate(j)
            for g in groups_due(step, ROOT):
                root(g)
            for g in groups_due(step, FINISH):
                finish_stats(g)
            for j in tiles_due(step, NORMALISE):
                normalise(j)
            for g, t in due(step, AFFINE):
                affine(g, t)
            for half in range(HALVES):
                for g in groups_due(step, INTERLEAVE - half):
                    interleave(g, half)
            if step in tables:
                tables[step]()
            for m, distance in enumerate((Q_FIRST - 1, Q_SECOND - 1)):
                for g in groups_due(step, distance):
                    bias_q(g, m)
            for j in tiles_due(step, SUMS):
                sum_of_tile(j)
            for j in tiles_due(step, SQUARES):
                squares_of_tile(j)
            if 0 <= step < TILES:
                times_sin(step)
            if 0 <= step + PROJECT < TILES:
                project(step + PROJECT)
            for m, distance in enumerate((Q_FIRST, Q_SECOND)):
                for g in groups_due(step, distance):
                    project_q(g, m)
            if step in PE_SUM:
                add_up(step)
            if step - 1 in PE_SUM:
                add_up_rest(step - 1)
            if step - PE_WAIT in PE_SUM:
                copy_total(step - PE_WAIT)
            for arguments in stores.get(step, ()):
                store(*arguments)
